import numpy as np
import ml_dtypes


def mxq(x, axis, fmt="e4m3"):
    dtype, down = {"e4m3": (ml_dtypes.float8_e4m3fn, 7), "e5m2": (ml_dtypes.float8_e5m2, 14)}[fmt]
    v = np.moveaxis(np.asarray(x, np.float32).astype(ml_dtypes.bfloat16).astype(np.float64), axis, -1)
    blocks = v.reshape(v.shape[:-1] + (-1, 32))
    amax = np.abs(blocks).max(-1, keepdims=True)
    byte = np.maximum(np.where(amax > 0, np.frexp(amax)[1] - 1 + 127, 0) - down, 1)
    scale = np.exp2(byte - 127.0)
    codes = (blocks / scale).astype(np.float32).astype(dtype).astype(np.float64)
    return np.moveaxis((codes * scale).reshape(v.shape), -1, axis)


WIDE = False


def mx_kscale(k):
    if not WIDE:
        return np.ones(k)
    levels = np.array([10, -10, 5, -5, 0])
    a = np.random.permutation(np.resize(levels, k // 512 * 4)).reshape(k // 512, 4)
    idx = np.arange(k)
    return np.exp2(a[idx // 512, idx % 128 // 32])


BF16 = ml_dtypes.bfloat16


def bf(x):
    return np.asarray(x, np.float32).astype(BF16)


def f64(x):
    return np.asarray(x).astype(np.float64)


B, S, HID, NH = 1, 512, 1024, 8
D = HID // NH
COS_EPS = 1e-8
D2_EPS = 1e-12
SW_BASE = np.array([0.0, 1.5, 0.5])


def setup_inputs():
    s = mx_kscale(HID)
    return {
        "q": bf(np.random.standard_normal((B, NH, S, D)) * 1.1),
        "k": bf(np.random.standard_normal((B, NH, S, D)) * 1.1),
        "value": bf(np.random.standard_normal((B, S, HID)) * s),
        "Wv": bf(np.random.standard_normal((HID, HID)) * 2.0 / np.sqrt(HID) / s[None, :]),
        "bv": bf(np.random.standard_normal(HID) * 0.1),
        "scoring_weights": bf(SW_BASE + 0.1 * np.random.standard_normal(SW_BASE.shape)),
    }


def reference(q, k, value, Wv, bv, scoring_weights):
    vp = (mxq(f64(value), 2, "e4m3") @ mxq(f64(Wv), 1, "e4m3").T) + f64(bv)
    v = vp.reshape(B, S, NH, D).transpose(0, 2, 1, 3)
    dot = f64(q) @ f64(k).transpose(0, 1, 3, 2)
    qn = np.sqrt((f64(q) ** 2).sum(-1))
    kn = np.sqrt((f64(k) ** 2).sum(-1))
    cos = dot / np.maximum(qn[..., :, None] * kn[..., None, :], COS_EPS)
    d2 = qn[..., :, None] ** 2 + kn[..., None, :] ** 2 - 2.0 * dot
    euc = -np.sqrt(np.maximum(d2, D2_EPS))
    sw = f64(scoring_weights)
    w = np.exp(sw - sw.max())
    w = w / w.sum()
    scores = w[0] * dot + w[1] * cos + w[2] * euc
    e = np.exp(scores - scores.max(-1, keepdims=True))
    ctx = (mxq(e, 3, "e4m3") @ mxq(v, 2, "e4m3")) / e.sum(-1, keepdims=True)
    return ctx.transpose(0, 2, 1, 3).reshape(B, S, HID)

@@ -1,0 +1,355 @@
+from contextlib import ExitStack
+
+import concourse.mybir as mybir
+from concourse.masks import make_identity
+
+F32 = mybir.dt.float32
+BF16 = mybir.dt.bfloat16
+U32 = mybir.dt.uint32
+U8 = mybir.dt.uint8
+FP8X4 = mybir.dt.float8_e4m3fn_x4
+ALU = mybir.AluOpType
+ACT = mybir.ActivationFunctionType
+AX = mybir.AxisListType
+
+P = 128
+NH = 8
+S = 512
+D = 128
+HID = NH * D
+NT = S // P
+PACK = 4
+K_PASS = P * PACK
+N_PASS = HID // K_PASS
+WORDS = K_PASS // 2
+D2_EPS = 1e-12
+NORM_SQ_FLOOR = 1e-24
+
+FLOPS = 2 * S * HID * HID + 2 * 2 * NH * S * S * D
+
+
+GROUP = 2
+N_GROUPS = NH // GROUP
+
+
+def tile_adaptiveattention_pa_kernel(tc, q, k, value, Wv, bv, scoring_weights, out):
+    nc = tc.nc
+    with ExitStack() as stack:
+        stack.enter_context(tc.manual_schedule())
+        keep = stack.enter_context(tc.tile_pool(name="keep", bufs=1))
+        psum = stack.enter_context(tc.psum_pool(name="psum", bufs=3))
+
+        kT = keep.tile([P, NH, S], BF16)
+        qT = keep.tile([P, NH, S], BF16)
+        half_k_sq_rows = keep.tile([P, NH, S], F32)
+        cos_k_rows = keep.tile([P, NH, S], F32)
+        v_codes = keep.tile([P, NH * D], U32, align_bytes=64)
+        v_scales = keep.tile([P, NH * D], U8, align_bytes=64)
+        row_sum = keep.tile([P, NH * NT], F32)
+
+        with tc.tile_pool(name="prep", bufs=1) as prep:
+            sw_bf = prep.tile([P, 3], BF16)
+            nc.scalar.dma_start(out=sw_bf[:], in_=scoring_weights.partition_broadcast(P))
+            bv_bf = prep.tile([P, HID], BF16)
+            nc.scalar.dma_start(out=bv_bf[:], in_=bv.partition_broadcast(P))
+            k_sb = prep.tile([P, NH * NT, D], BF16)
+            nc.sync.dma_start(out=k_sb[:], in_=k.rearrange("b h (t p) d -> p (b h t) d", p=P))
+            q_sb = prep.tile([P, NH * NT, D], BF16)
+            nc.sync.dma_start(
+                out=q_sb[:].rearrange("p (h t) d -> p h (t d)", t=NT),
+                in_=q.rearrange("b h (p t) d -> p (b h) (t d)", t=NT),
+            )
+            value_sb = prep.tile([P, PACK, HID], BF16)
+            nc.sync.dma_start(
+                out=value_sb[:].rearrange("p (u e) c -> p u (e c)", e=2),
+                in_=value.rearrange("b (u p e) c -> p (b u) (e c)", u=2, e=2),
+            )
+            wv_sb = prep.tile([P, N_PASS, NH, K_PASS], BF16)
+            wv_passes = Wv.rearrange("(h p) (g c) -> p g h c", p=P, g=N_PASS)
+            for g in range(N_PASS):
+                nc.sync.dma_start(out=wv_sb[:, g, :, :], in_=wv_passes[:, g, :, :])
+
+            ident_b = keep.tile([P, P], BF16)
+            make_identity(nc, ident_b[:])
+            ident_f = keep.tile([P, P], F32)
+            make_identity(nc, ident_f[:])
+
+            sw = prep.tile([P, 3], F32)
+            nc.vector.tensor_copy(out=sw[:], in_=sw_bf[:])
+            neg_sw_max = prep.tile([P, 1], F32)
+            nc.vector.tensor_reduce(out=neg_sw_max[:], in_=sw[:], axis=AX.X, op=ALU.max, negate=True)
+            sw_exp = prep.tile([P, 3], F32)
+            sw_sum = prep.tile([P, 1], F32)
+            nc.scalar.activation(
+                out=sw_exp[:], in_=sw[:], func=ACT.Exp, bias=neg_sw_max[:], accum_out=sw_sum[:]
+            )
+            sw_rsum = prep.tile([P, 1], F32)
+            nc.vector.reciprocal(out=sw_rsum[:], in_=sw_sum[:])
+            w = prep.tile([P, 3], F32)
+            nc.vector.tensor_scalar_mul(out=w[:], in0=sw_exp[:], scalar1=sw_rsum[:])
+
+            def squared_norms(rows_sb, name):
+                squares = prep.tile([P, NH * NT, D], BF16, name=name + "_squares")
+                sums = keep.tile([P, NH * NT], F32, name=name + "_sq")
+                for c in range(NH * NT):
+                    nc.scalar.activation(
+                        out=squares[:, c, :], in_=rows_sb[:, c, :], func=ACT.Square, accum_out=sums[:, c : c + 1]
+                    )
+                return sums
+
+            def transpose_heads(rows_sb, flipped_sb):
+                for h0 in range(0, NH, 2):
+                    flipped = psum.tile([P, 2, S], BF16, tag="flip", name="head_flipped")
+                    for a in range(2):
+                        for t in range(NT):
+                            nc.tensor.transpose(
+                                out=flipped[:, a, t * P : (t + 1) * P],
+                                in_=rows_sb[:, (h0 + a) * NT + t, :],
+                                identity=ident_b[:],
+                            )
+                    nc.vector.tensor_copy(out=flipped_sb[:, h0 : h0 + 2, :], in_=flipped[:])
+
+            k_sq = squared_norms(k_sb, "k")
+            transpose_heads(k_sb, kT)
+            q_sq = squared_norms(q_sb, "q")
+            transpose_heads(q_sb, qT)
+
+            def group_pass(block_of, n_blocks, grouped):
+                for b0 in range(0, n_blocks, 2):
+                    flipped = psum.tile([P, 2, 2 * P], F32, tag="flip", name="pass_flipped")
+                    for a in range(2):
+                        words = block_of(b0 + a).bitcast(F32)
+                        for u in range(2):
+                            nc.tensor.transpose(
+                                out=flipped[:, u, a * P : (a + 1) * P],
+                                in_=words[:, u * P : (u + 1) * P],
+                                identity=ident_f[:],
+                            )
+                    nc.vector.tensor_copy(
+                        out=grouped[:, b0 * P : (b0 + 2) * P, :], in_=flipped[:].rearrange("p u r -> p r u")
+                    )
+
+            def quantise_pass(grouped, codes, scales):
+                nc.vector.quantize_mx(
+                    out=codes.bitcast(FP8X4), scales=scales, in_=grouped.rearrange("p r u -> p (r u)").bitcast(BF16)
+                )
+
+            value_grouped = prep.tile([P, N_PASS, S, 2], F32, align_bytes=64)
+            value_codes = prep.tile([P, N_PASS, S], U32, align_bytes=64)
+            value_scales = prep.tile([P, N_PASS, S], U8, align_bytes=64)
+            wv_grouped = prep.tile([P, N_PASS, HID, 2], F32, align_bytes=64)
+            wv_codes = prep.tile([P, N_PASS, HID], U32, align_bytes=64)
+            wv_scales = prep.tile([P, N_PASS, HID], U8, align_bytes=64)
+
+            for g in range(N_PASS):
+                group_pass(
+                    lambda b: value_sb[:, b, g * K_PASS : (g + 1) * K_PASS], PACK, value_grouped[:, g, :, :]
+                )
+            for g in range(N_PASS):
+                quantise_pass(value_grouped[:, g, :, :], value_codes[:, g, :], value_scales[:, g, :])
+            group_pass(lambda b: wv_sb[:, 0, b, :], NH, wv_grouped[:, 0, :, :])
+
+            def floored_norm(sums, name):
+                floored = prep.tile([P, NH * NT], F32, name=name + "_floored")
+                nc.vector.tensor_scalar_max(out=floored[:], in0=sums[:], scalar1=NORM_SQ_FLOOR)
+                norm = prep.tile([P, NH * NT], F32, name=name + "_norm")
+                nc.scalar.activation(out=norm[:], in_=floored[:], func=ACT.Sqrt)
+                return norm
+
+            k_norm = floored_norm(k_sq, "k")
+            q_norm = floored_norm(q_sq, "q")
+            half_k_sq = prep.tile([P, NH * NT], F32)
+            nc.vector.tensor_scalar_mul(out=half_k_sq[:], in0=k_sq[:], scalar1=0.5)
+            half_q_sq = keep.tile([P, NH * NT], F32)
+            nc.vector.tensor_scalar_mul(out=half_q_sq[:], in0=q_sq[:], scalar1=0.5)
+            k_rnorm = prep.tile([P, NH * NT], F32)
+            nc.vector.reciprocal(out=k_rnorm[:], in_=k_norm[:])
+            cos_k = prep.tile([P, NH * NT], F32)
+            nc.vector.tensor_scalar_mul(out=cos_k[:], in0=k_rnorm[:], scalar1=w[:, 1:2])
+            q_rnorm = keep.tile([P, NH * NT], F32)
+            nc.vector.reciprocal(out=q_rnorm[:], in_=q_norm[:])
+            dot_q = keep.tile([P, NH * NT], F32)
+            nc.vector.tensor_scalar_mul(out=dot_q[:], in0=q_norm[:], scalar1=w[:, 0:1])
+            euc_q = prep.tile([P, NH * NT], F32)
+            nc.vector.tensor_scalar_mul(out=euc_q[:], in0=q_norm[:], scalar1=w[:, 2:3])
+            sqrt_scale = keep.tile([P, NH * NT], F32)
+            nc.vector.scalar_tensor_tensor(
+                out=sqrt_scale[:], in0=euc_q[:], scalar=-2.0, in1=euc_q[:], op0=ALU.mult, op1=ALU.mult
+            )
+
+            quantise_pass(wv_grouped[:, 0, :, :], wv_codes[:, 0, :], wv_scales[:, 0, :])
+            group_pass(lambda b: wv_sb[:, 1, b, :], NH, wv_grouped[:, 1, :, :])
+            quantise_pass(wv_grouped[:, 1, :, :], wv_codes[:, 1, :], wv_scales[:, 1, :])
+
+            v_grouped = prep.tile([P, NH, D, PACK], BF16, align_bytes=64)
+            for h in range(NH):
+                head = slice(h * D, (h + 1) * D)
+                vp = psum.tile([P, PACK, D], F32, tag="acc", bufs=2, name="vp")
+                for t in range(PACK):
+                    block = slice(t * P, (t + 1) * P)
+                    for g in range(N_PASS):
+                        nc.tensor.matmul_mx(
+                            out=vp[:, t, :],
+                            lhsT=value_codes[:, g, block].bitcast(FP8X4),
+                            lhsT_scale=value_scales[:, g, block],
+                            rhs=wv_codes[:, g, head].bitcast(FP8X4),
+                            rhs_scale=wv_scales[:, g, head],
+                            start=(g == 0),
+                            stop=(g == N_PASS - 1),
+                        )
+                nc.vector.tensor_tensor(
+                    out=v_grouped[:, h, :, :],
+                    in0=vp[:].rearrange("p t d -> p d t"),
+                    in1=bv_bf[:, head].unsqueeze(2).to_broadcast([P, D, PACK]),
+                    op=ALU.add,
+                )
+
+            for h in range(NH):
+                for column_tile, rows in ((half_k_sq, half_k_sq_rows), (cos_k, cos_k_rows)):
+                    spread = psum.tile([P, S], F32, tag="flip", name="spread")
+                    for t in range(NT):
+                        c = h * NT + t
+                        nc.tensor.transpose(
+                            out=spread[:, t * P : (t + 1) * P],
+                            in_=column_tile[:, c : c + 1].to_broadcast([P, P]),
+                            identity=ident_f[:],
+                        )
+                    nc.scalar.copy(out=rows[:, h, :], in_=spread[:])
+
+            nc.vector.quantize_mx(
+                out=v_codes[:].bitcast(FP8X4), scales=v_scales[:], in_=v_grouped[:].rearrange("p h d t -> p (h d t)")
+            )
+
+        work = stack.enter_context(tc.tile_pool(name="work", bufs=2 * GROUP, reuse_waits="tile"))
+        out_rows = out.rearrange("b (p t) c -> p (b t) c", t=NT)
+        neg_half_d2 = {}
+        mixed = {}
+        e_grouped = {}
+
+        def heads_of(group):
+            return range(group * GROUP, (group + 1) * GROUP)
+
+        def scores(group):
+            for h in heads_of(group):
+                neg_half_d2[h] = work.tile([P, NT, S], F32, name="neg_half_d2")
+                mixed[h] = work.tile([P, NT, S], F32, name="mixed", bufs=3 * GROUP)
+                for t in range(NT):
+                    c = h * NT + t
+                    dot = psum.tile([P, S], F32, tag="dot")
+                    nc.tensor.matmul(
+                        out=dot[:], lhsT=qT[:, h, t * P : (t + 1) * P], rhs=kT[:, h, :], start=True, stop=True
+                    )
+                    nc.vector.scalar_tensor_tensor(
+                        out=neg_half_d2[h][:, t, :],
+                        in0=dot[:],
+                        scalar=half_q_sq[:, c : c + 1],
+                        in1=half_k_sq_rows[:, h, :],
+                        op0=ALU.subtract,
+                        op1=ALU.subtract,
+                    )
+                    nc.vector.scalar_tensor_tensor(
+                        out=mixed[h][:, t, :],
+                        in0=cos_k_rows[:, h, :],
+                        scalar=dot_q[:, c : c + 1],
+                        in1=dot[:],
+                        op0=ALU.add,
+                        op1=ALU.mult,
+                    )
+                nc.gpsimd.tensor_scalar(
+                    out=neg_half_d2[h][:],
+                    in0=neg_half_d2[h][:],
+                    scalar1=-0.5 * D2_EPS,
+                    scalar2=-3.0e38,
+                    op0=ALU.min,
+                    op1=ALU.max,
+                )
+
+        def distances(group):
+            for h in heads_of(group):
+                for t in range(NT):
+                    c = h * NT + t
+                    nc.scalar.activation(
+                        out=neg_half_d2[h][:, t, :],
+                        in_=neg_half_d2[h][:, t, :],
+                        func=ACT.Sqrt,
+                        scale=sqrt_scale[:, c : c + 1],
+                    )
+                nc.gpsimd.tensor_tensor(out=mixed[h][:], in0=mixed[h][:], in1=neg_half_d2[h][:], op=ALU.subtract)
+
+        def exponentials(group):
+            exp_bias = {}
+            e = {}
+            for h in heads_of(group):
+                neg_max = work.tile([P, NT], F32, name="neg_max")
+                nc.vector.tensor_reduce(out=neg_max[:], in_=mixed[h][:], axis=AX.X, op=ALU.max, negate=True)
+                exp_bias[h] = work.tile([P, NT], F32, name="exp_bias")
+                nc.vector.tensor_tensor(
+                    out=exp_bias[h][:], in0=neg_max[:], in1=q_rnorm[:, h * NT : (h + 1) * NT], op=ALU.mult
+                )
+            for h in heads_of(group):
+                e[h] = work.tile([P, NT, S], BF16, name="e")
+                for t in range(NT):
+                    c = h * NT + t
+                    nc.scalar.activation(
+                        out=e[h][:, t, :],
+                        in_=mixed[h][:, t, :],
+                        func=ACT.Exp,
+                        scale=q_rnorm[:, c : c + 1],
+                        bias=exp_bias[h][:, t : t + 1],
+                        accum_out=row_sum[:, c : c + 1],
+                    )
+            for h in heads_of(group):
+                e_grouped[h] = work.tile([P, NT, P, 2], F32, name="e_grouped", align_bytes=64)
+                for t0 in range(0, NT, 2):
+                    e_flipped = psum.tile([P, 2, 2, P], F32, tag="flip", name="e_flipped")
+                    for a in range(2):
+                        words = e[h][:, t0 + a, :].bitcast(F32)
+                        for u in range(2):
+                            nc.tensor.transpose(
+                                out=e_flipped[:, a, u, :], in_=words[:, u * P : (u + 1) * P], identity=ident_f[:]
+                            )
+                    nc.scalar.copy(
+                        out=e_grouped[h][:, t0 : t0 + 2, :, :], in_=e_flipped[:].rearrange("p a u i -> p a i u")
+                    )
+
+        def context(group):
+            e_codes = {}
+            e_scales = {}
+            for h in heads_of(group):
+                e_codes[h] = work.tile([P, S], U32, name="e_codes", align_bytes=64)
+                e_scales[h] = work.tile([P, S], U8, name="e_scales", align_bytes=64)
+                nc.vector.quantize_mx(
+                    out=e_codes[h][:].bitcast(FP8X4),
+                    scales=e_scales[h][:],
+                    in_=e_grouped[h][:].rearrange("p t i u -> p (t i u)").bitcast(BF16),
+                )
+            for h in heads_of(group):
+                head = slice(h * D, (h + 1) * D)
+                ctx = psum.tile([P, NT, D], F32, tag="acc", bufs=2, name="ctx")
+                for t in range(NT):
+                    block = slice(t * P, (t + 1) * P)
+                    nc.tensor.matmul_mx(
+                        out=ctx[:, t, :],
+                        lhsT=e_codes[h][:, block].bitcast(FP8X4),
+                        lhsT_scale=e_scales[h][:, block],
+                        rhs=v_codes[:, head].bitcast(FP8X4),
+                        rhs_scale=v_scales[:, head],
+                        start=True,
+                        stop=True,
+                    )
+                row_rsum = work.tile([P, NT], F32, name="row_rsum")
+                nc.vector.reciprocal(out=row_rsum[:], in_=row_sum[:, h * NT : (h + 1) * NT])
+                result = work.tile([P, NT, D], F32, name="result")
+                nc.vector.tensor_tensor(
+                    out=result[:], in0=ctx[:], in1=row_rsum[:].unsqueeze(2).to_broadcast([P, NT, D]), op=ALU.mult
+                )
+                nc.sync.dma_start(out=out_rows[:, :, head], in_=result[:])
+
+        for step in range(N_GROUPS + 2):
+            if step < N_GROUPS:
+                scores(step)
+                distances(step)
+            if 1 <= step <= N_GROUPS:
+                exponentials(step - 1)
+            if step >= 2:
+                context(step - 2)

@@ -35,7 +35,6 @@ N_GROUPS = NH // GROUP
 def tile_adaptiveattention_pa_kernel(tc, q, k, value, Wv, bv, scoring_weights, out):
     nc = tc.nc
     with ExitStack() as stack:
-        stack.enter_context(tc.manual_schedule())
         keep = stack.enter_context(tc.tile_pool(name="keep", bufs=1))
         psum = stack.enter_context(tc.psum_pool(name="psum", bufs=3))
 
@@ -125,7 +124,7 @@ def tile_adaptiveattention_pa_kernel(tc, q, k, value, Wv, bv, scoring_weights, o
                                 in_=words[:, u * P : (u + 1) * P],
                                 identity=ident_f[:],
                             )
-                    nc.vector.tensor_copy(
+                    nc.scalar.copy(
                         out=grouped[:, b0 * P : (b0 + 2) * P, :], in_=flipped[:].rearrange("p u r -> p r u")
                     )
 
@@ -255,14 +254,7 @@ def tile_adaptiveattention_pa_kernel(tc, q, k, value, Wv, bv, scoring_weights, o
                         op0=ALU.add,
                         op1=ALU.mult,
                     )
-                nc.gpsimd.tensor_scalar(
-                    out=neg_half_d2[h][:],
-                    in0=neg_half_d2[h][:],
-                    scalar1=-0.5 * D2_EPS,
-                    scalar2=-3.0e38,
-                    op0=ALU.min,
-                    op1=ALU.max,
-                )
+                nc.vector.tensor_scalar_min(out=neg_half_d2[h][:], in0=neg_half_d2[h][:], scalar1=-0.5 * D2_EPS)
 
         def distances(group):
             for h in heads_of(group):

@@ -30,226 +30,163 @@ FLOPS = 2 * S * HID * HID + 2 * 2 * NH * S * S * D
 
 GROUP = 2
 N_GROUPS = NH // GROUP
+GC = GROUP * NT
 
 
 def tile_adaptiveattention_pa_kernel(tc, q, k, value, Wv, bv, scoring_weights, out):
     nc = tc.nc
     with ExitStack() as stack:
         keep = stack.enter_context(tc.tile_pool(name="keep", bufs=1))
+        work = stack.enter_context(tc.tile_pool(name="work", bufs=2 * GROUP))
         psum = stack.enter_context(tc.psum_pool(name="psum", bufs=3))
 
-        kT = keep.tile([P, NH, S], BF16)
-        qT = keep.tile([P, NH, S], BF16)
-        half_k_sq_rows = keep.tile([P, NH, S], F32)
-        cos_k_rows = keep.tile([P, NH, S], F32)
-        v_codes = keep.tile([P, NH * D], U32, align_bytes=64)
-        v_scales = keep.tile([P, NH * D], U8, align_bytes=64)
-        row_sum = keep.tile([P, NH * NT], F32)
-
-        with tc.tile_pool(name="prep", bufs=1) as prep:
-            sw_bf = prep.tile([P, 3], BF16)
-            nc.scalar.dma_start(out=sw_bf[:], in_=scoring_weights.partition_broadcast(P))
-            bv_bf = prep.tile([P, HID], BF16)
-            nc.scalar.dma_start(out=bv_bf[:], in_=bv.partition_broadcast(P))
-            k_sb = prep.tile([P, NH * NT, D], BF16)
-            nc.sync.dma_start(out=k_sb[:], in_=k.rearrange("b h (t p) d -> p (b h t) d", p=P))
-            q_sb = prep.tile([P, NH * NT, D], BF16)
+        sw_bf = keep.tile([P, 3], BF16)
+        nc.scalar.dma_start(out=sw_bf[:], in_=scoring_weights.partition_broadcast(P))
+        k_rows = {}
+        q_rows = {}
+        for group in range(N_GROUPS):
+            heads = slice(group * GROUP, (group + 1) * GROUP)
+            k_rows[group] = work.tile([P, GC, D], BF16, name="k_rows", bufs=N_GROUPS)
+            nc.sync.dma_start(out=k_rows[group][:], in_=k[0, heads].rearrange("h (t p) d -> p (h t) d", p=P))
+            q_rows[group] = work.tile([P, GC, D], BF16, name="q_rows", bufs=N_GROUPS)
             nc.sync.dma_start(
-                out=q_sb[:].rearrange("p (h t) d -> p h (t d)", t=NT),
-                in_=q.rearrange("b h (p t) d -> p (b h) (t d)", t=NT),
+                out=q_rows[group][:].rearrange("p (h t) d -> p h (t d)", t=NT),
+                in_=q[0, heads].rearrange("h (p t) d -> p h (t d)", t=NT),
             )
-            value_sb = prep.tile([P, PACK, HID], BF16)
-            nc.sync.dma_start(
-                out=value_sb[:].rearrange("p (u e) c -> p u (e c)", e=2),
-                in_=value.rearrange("b (u p e) c -> p (b u) (e c)", u=2, e=2),
-            )
-            wv_sb = prep.tile([P, N_PASS, NH, K_PASS], BF16)
-            wv_passes = Wv.rearrange("(h p) (g c) -> p g h c", p=P, g=N_PASS)
-            for g in range(N_PASS):
-                nc.sync.dma_start(out=wv_sb[:, g, :, :], in_=wv_passes[:, g, :, :])
+        value_sb = keep.tile([P, PACK, HID], BF16)
+        nc.sync.dma_start(
+            out=value_sb[:].rearrange("p (u e) c -> p u (e c)", e=2),
+            in_=value.rearrange("b (u p e) c -> p (b u) (e c)", u=2, e=2),
+        )
+        wv_sb = keep.tile([P, N_PASS, NH, K_PASS], BF16)
+        wv_passes = Wv.rearrange("(h p) (g c) -> p g h c", p=P, g=N_PASS)
+        for g in range(N_PASS):
+            nc.sync.dma_start(out=wv_sb[:, g, :, :], in_=wv_passes[:, g, :, :])
+        bv_bf = keep.tile([P, HID], BF16)
+        nc.sync.dma_start(out=bv_bf[:], in_=bv.partition_broadcast(P))
 
-            ident_b = keep.tile([P, P], BF16)
-            make_identity(nc, ident_b[:])
-            ident_f = keep.tile([P, P], F32)
-            make_identity(nc, ident_f[:])
+        ident_b = keep.tile([P, P], BF16)
+        make_identity(nc, ident_b[:])
+        ident_f = keep.tile([P, P], F32)
+        make_identity(nc, ident_f[:])
 
-            sw = prep.tile([P, 3], F32)
-            nc.vector.tensor_copy(out=sw[:], in_=sw_bf[:])
-            neg_sw_max = prep.tile([P, 1], F32)
-            nc.vector.tensor_reduce(out=neg_sw_max[:], in_=sw[:], axis=AX.X, op=ALU.max, negate=True)
-            sw_exp = prep.tile([P, 3], F32)
-            sw_sum = prep.tile([P, 1], F32)
-            nc.scalar.activation(
-                out=sw_exp[:], in_=sw[:], func=ACT.Exp, bias=neg_sw_max[:], accum_out=sw_sum[:]
-            )
-            sw_rsum = prep.tile([P, 1], F32)
-            nc.vector.reciprocal(out=sw_rsum[:], in_=sw_sum[:])
-            w = prep.tile([P, 3], F32)
-            nc.vector.tensor_scalar_mul(out=w[:], in0=sw_exp[:], scalar1=sw_rsum[:])
+        sw = keep.tile([P, 3], F32)
+        nc.vector.tensor_copy(out=sw[:], in_=sw_bf[:])
+        neg_sw_max = keep.tile([P, 1], F32)
+        nc.vector.tensor_reduce(out=neg_sw_max[:], in_=sw[:], axis=AX.X, op=ALU.max, negate=True)
+        sw_exp = keep.tile([P, 3], F32)
+        sw_sum = keep.tile([P, 1], F32)
+        nc.scalar.activation(out=sw_exp[:], in_=sw[:], func=ACT.Exp, bias=neg_sw_max[:], accum_out=sw_sum[:])
+        sw_rsum = keep.tile([P, 1], F32)
+        nc.vector.reciprocal(out=sw_rsum[:], in_=sw_sum[:])
+        w = keep.tile([P, 3], F32)
+        nc.vector.tensor_scalar_mul(out=w[:], in0=sw_exp[:], scalar1=sw_rsum[:])
 
-            def squared_norms(rows_sb, name):
-                squares = prep.tile([P, NH * NT, D], BF16, name=name + "_squares")
-                sums = keep.tile([P, NH * NT], F32, name=name + "_sq")
-                for c in range(NH * NT):
-                    nc.scalar.activation(
-                        out=squares[:, c, :], in_=rows_sb[:, c, :], func=ACT.Square, accum_out=sums[:, c : c + 1]
-                    )
-                return sums
-
-            def transpose_heads(rows_sb, flipped_sb):
-                for h0 in range(0, NH, 2):
-                    flipped = psum.tile([P, 2, S], BF16, tag="flip", name="head_flipped")
-                    for a in range(2):
-                        for t in range(NT):
-                            nc.tensor.transpose(
-                                out=flipped[:, a, t * P : (t + 1) * P],
-                                in_=rows_sb[:, (h0 + a) * NT + t, :],
-                                identity=ident_b[:],
-                            )
-                    nc.vector.tensor_copy(out=flipped_sb[:, h0 : h0 + 2, :], in_=flipped[:])
-
-            k_sq = squared_norms(k_sb, "k")
-            transpose_heads(k_sb, kT)
-            q_sq = squared_norms(q_sb, "q")
-            transpose_heads(q_sb, qT)
-
-            def group_pass(block_of, n_blocks, grouped):
-                for b0 in range(0, n_blocks, 2):
-                    flipped = psum.tile([P, 2, 2 * P], F32, tag="flip", name="pass_flipped")
-                    for a in range(2):
-                        words = block_of(b0 + a).bitcast(F32)
-                        for u in range(2):
-                            nc.tensor.transpose(
-                                out=flipped[:, u, a * P : (a + 1) * P],
-                                in_=words[:, u * P : (u + 1) * P],
-                                identity=ident_f[:],
-                            )
-                    nc.scalar.copy(
-                        out=grouped[:, b0 * P : (b0 + 2) * P, :], in_=flipped[:].rearrange("p u r -> p r u")
-                    )
-
-            def quantise_pass(grouped, codes, scales):
-                nc.vector.quantize_mx(
-                    out=codes.bitcast(FP8X4), scales=scales, in_=grouped.rearrange("p r u -> p (r u)").bitcast(BF16)
-                )
-
-            value_grouped = prep.tile([P, N_PASS, S, 2], F32, align_bytes=64)
-            value_codes = prep.tile([P, N_PASS, S], U32, align_bytes=64)
-            value_scales = prep.tile([P, N_PASS, S], U8, align_bytes=64)
-            wv_grouped = prep.tile([P, N_PASS, HID, 2], F32, align_bytes=64)
-            wv_codes = prep.tile([P, N_PASS, HID], U32, align_bytes=64)
-            wv_scales = prep.tile([P, N_PASS, HID], U8, align_bytes=64)
-
-            for g in range(N_PASS):
-                group_pass(
-                    lambda b: value_sb[:, b, g * K_PASS : (g + 1) * K_PASS], PACK, value_grouped[:, g, :, :]
-                )
-            for g in range(N_PASS):
-                quantise_pass(value_grouped[:, g, :, :], value_codes[:, g, :], value_scales[:, g, :])
-            group_pass(lambda b: wv_sb[:, 0, b, :], NH, wv_grouped[:, 0, :, :])
-
-            def floored_norm(sums, name):
-                floored = prep.tile([P, NH * NT], F32, name=name + "_floored")
-                nc.vector.tensor_scalar_max(out=floored[:], in0=sums[:], scalar1=NORM_SQ_FLOOR)
-                norm = prep.tile([P, NH * NT], F32, name=name + "_norm")
-                nc.scalar.activation(out=norm[:], in_=floored[:], func=ACT.Sqrt)
-                return norm
-
-            k_norm = floored_norm(k_sq, "k")
-            q_norm = floored_norm(q_sq, "q")
-            half_k_sq = prep.tile([P, NH * NT], F32)
-            nc.vector.tensor_scalar_mul(out=half_k_sq[:], in0=k_sq[:], scalar1=0.5)
-            half_q_sq = keep.tile([P, NH * NT], F32)
-            nc.vector.tensor_scalar_mul(out=half_q_sq[:], in0=q_sq[:], scalar1=0.5)
-            k_rnorm = prep.tile([P, NH * NT], F32)
-            nc.vector.reciprocal(out=k_rnorm[:], in_=k_norm[:])
-            cos_k = prep.tile([P, NH * NT], F32)
-            nc.vector.tensor_scalar_mul(out=cos_k[:], in0=k_rnorm[:], scalar1=w[:, 1:2])
-            q_rnorm = keep.tile([P, NH * NT], F32)
-            nc.vector.reciprocal(out=q_rnorm[:], in_=q_norm[:])
-            dot_q = keep.tile([P, NH * NT], F32)
-            nc.vector.tensor_scalar_mul(out=dot_q[:], in0=q_norm[:], scalar1=w[:, 0:1])
-            euc_q = prep.tile([P, NH * NT], F32)
-            nc.vector.tensor_scalar_mul(out=euc_q[:], in0=q_norm[:], scalar1=w[:, 2:3])
-            sqrt_scale = keep.tile([P, NH * NT], F32)
-            nc.vector.scalar_tensor_tensor(
-                out=sqrt_scale[:], in0=euc_q[:], scalar=-2.0, in1=euc_q[:], op0=ALU.mult, op1=ALU.mult
-            )
-
-            quantise_pass(wv_grouped[:, 0, :, :], wv_codes[:, 0, :], wv_scales[:, 0, :])
-            group_pass(lambda b: wv_sb[:, 1, b, :], NH, wv_grouped[:, 1, :, :])
-            quantise_pass(wv_grouped[:, 1, :, :], wv_codes[:, 1, :], wv_scales[:, 1, :])
-
-            v_grouped = prep.tile([P, NH, D, PACK], BF16, align_bytes=64)
-            for h in range(NH):
-                head = slice(h * D, (h + 1) * D)
-                vp = psum.tile([P, PACK, D], F32, tag="acc", bufs=2, name="vp")
-                for t in range(PACK):
-                    block = slice(t * P, (t + 1) * P)
-                    for g in range(N_PASS):
-                        nc.tensor.matmul_mx(
-                            out=vp[:, t, :],
-                            lhsT=value_codes[:, g, block].bitcast(FP8X4),
-                            lhsT_scale=value_scales[:, g, block],
-                            rhs=wv_codes[:, g, head].bitcast(FP8X4),
-                            rhs_scale=wv_scales[:, g, head],
-                            start=(g == 0),
-                            stop=(g == N_PASS - 1),
-                        )
-                nc.vector.tensor_tensor(
-                    out=v_grouped[:, h, :, :],
-                    in0=vp[:].rearrange("p t d -> p d t"),
-                    in1=bv_bf[:, head].unsqueeze(2).to_broadcast([P, D, PACK]),
-                    op=ALU.add,
-                )
-
-            for h in range(NH):
-                for column_tile, rows in ((half_k_sq, half_k_sq_rows), (cos_k, cos_k_rows)):
-                    spread = psum.tile([P, S], F32, tag="flip", name="spread")
-                    for t in range(NT):
-                        c = h * NT + t
-                        nc.tensor.transpose(
-                            out=spread[:, t * P : (t + 1) * P],
-                            in_=column_tile[:, c : c + 1].to_broadcast([P, P]),
-                            identity=ident_f[:],
-                        )
-                    nc.scalar.copy(out=rows[:, h, :], in_=spread[:])
-
-            nc.vector.quantize_mx(
-                out=v_codes[:].bitcast(FP8X4), scales=v_scales[:], in_=v_grouped[:].rearrange("p h d t -> p (h d t)")
-            )
-
-        work = stack.enter_context(tc.tile_pool(name="work", bufs=2 * GROUP, reuse_waits="tile"))
-        out_rows = out.rearrange("b (p t) c -> p (b t) c", t=NT)
+        KEYS, QUERIES = 0, 1
+        flipped_sb = {}
+        key_rows = {}
+        half_sq = {}
+        rnorm = {}
+        dot_q = {}
+        sqrt_scale = {}
         neg_half_d2 = {}
         mixed = {}
         e_grouped = {}
+        row_sum = keep.tile([P, NH * NT], F32)
+        out_rows = out.rearrange("b (p t) c -> p (b t) c", t=NT)
 
         def heads_of(group):
             return range(group * GROUP, (group + 1) * GROUP)
 
+        def small(name, shape):
+            return work.tile(shape, F32, name=name, bufs=N_GROUPS)
+
+        sq = {}
+        cos_k = {}
+
+        def square_and_transpose(group):
+            both = (k_rows[group], q_rows[group])
+            squares = work.tile([P, 2, GC, D], BF16, name="squares", bufs=1)
+            sq[group] = small("sq", [P, 2, GC])
+            for side in (KEYS, QUERIES):
+                for c in range(GC):
+                    nc.scalar.activation(
+                        out=squares[:, side, c, :],
+                        in_=both[side][:, c, :],
+                        func=ACT.Square,
+                        accum_out=sq[group][:, side, c : c + 1],
+                    )
+            flipped_sb[group] = work.tile([P, 2, GROUP, S], BF16, name="flipped_sb", bufs=2)
+            for side in (KEYS, QUERIES):
+                flipped = psum.tile([P, GROUP, S], BF16, tag="flip", name="flipped")
+                for c in range(GC):
+                    nc.tensor.transpose(
+                        out=flipped[:, c // NT, (c % NT) * P : (c % NT + 1) * P],
+                        in_=both[side][:, c, :],
+                        identity=ident_b[:],
+                    )
+                nc.vector.tensor_copy(out=flipped_sb[group][:, side, :, :], in_=flipped[:])
+
+        def norm_scalars(group):
+            floored = small("floored", [P, 2, GC])
+            nc.vector.tensor_scalar_max(out=floored[:], in0=sq[group][:], scalar1=NORM_SQ_FLOOR)
+            norm = small("norm", [P, 2, GC])
+            nc.scalar.activation(out=norm[:], in_=floored[:], func=ACT.Sqrt)
+            rnorm[group] = small("rnorm", [P, 2, GC])
+            nc.vector.reciprocal(out=rnorm[group][:], in_=norm[:])
+            half_sq[group] = small("half_sq", [P, 2, GC])
+            nc.vector.tensor_scalar_mul(out=half_sq[group][:], in0=sq[group][:], scalar1=0.5)
+            cos_k[group] = small("cos_k", [P, GC])
+            nc.vector.tensor_scalar_mul(out=cos_k[group][:], in0=rnorm[group][:, KEYS, :], scalar1=w[:, 1:2])
+            dot_q[group] = small("dot_q", [P, GC])
+            nc.vector.tensor_scalar_mul(out=dot_q[group][:], in0=norm[:, QUERIES, :], scalar1=w[:, 0:1])
+            euc_q = small("euc_q", [P, GC])
+            nc.vector.tensor_scalar_mul(out=euc_q[:], in0=norm[:, QUERIES, :], scalar1=w[:, 2:3])
+            sqrt_scale[group] = small("sqrt_scale", [P, GC])
+            nc.vector.scalar_tensor_tensor(
+                out=sqrt_scale[group][:], in0=euc_q[:], scalar=-2.0, in1=euc_q[:], op0=ALU.mult, op1=ALU.mult
+            )
+
+        def spread_keys(group):
+            key_rows[group] = work.tile([P, 2, GROUP, S], F32, name="key_rows", bufs=2)
+            for a in range(GROUP):
+                for which, columns in enumerate((half_sq[group][:, KEYS, :], cos_k[group][:])):
+                    spread = psum.tile([P, S], F32, tag="flip", name="spread")
+                    for t in range(NT):
+                        c = a * NT + t
+                        nc.tensor.transpose(
+                            out=spread[:, t * P : (t + 1) * P],
+                            in_=columns[:, c : c + 1].to_broadcast([P, P]),
+                            identity=ident_f[:],
+                        )
+                    nc.scalar.copy(out=key_rows[group][:, which, a, :], in_=spread[:])
+
         def scores(group):
-            for h in heads_of(group):
+            for a, h in enumerate(heads_of(group)):
                 neg_half_d2[h] = work.tile([P, NT, S], F32, name="neg_half_d2")
                 mixed[h] = work.tile([P, NT, S], F32, name="mixed", bufs=3 * GROUP)
                 for t in range(NT):
-                    c = h * NT + t
+                    c = a * NT + t
                     dot = psum.tile([P, S], F32, tag="dot")
                     nc.tensor.matmul(
-                        out=dot[:], lhsT=qT[:, h, t * P : (t + 1) * P], rhs=kT[:, h, :], start=True, stop=True
+                        out=dot[:],
+                        lhsT=flipped_sb[group][:, QUERIES, a, t * P : (t + 1) * P],
+                        rhs=flipped_sb[group][:, KEYS, a, :],
+                        start=True,
+                        stop=True,
                     )
                     nc.vector.scalar_tensor_tensor(
                         out=neg_half_d2[h][:, t, :],
                         in0=dot[:],
-                        scalar=half_q_sq[:, c : c + 1],
-                        in1=half_k_sq_rows[:, h, :],
+                        scalar=half_sq[group][:, QUERIES, c : c + 1],
+                        in1=key_rows[group][:, 0, a, :],
                         op0=ALU.subtract,
                         op1=ALU.subtract,
                     )
                     nc.vector.scalar_tensor_tensor(
                         out=mixed[h][:, t, :],
-                        in0=cos_k_rows[:, h, :],
-                        scalar=dot_q[:, c : c + 1],
+                        in0=key_rows[group][:, 1, a, :],
+                        scalar=dot_q[group][:, c : c + 1],
                         in1=dot[:],
                         op0=ALU.add,
                         op1=ALU.mult,
@@ -257,41 +194,44 @@ def tile_adaptiveattention_pa_kernel(tc, q, k, value, Wv, bv, scoring_weights, o
                 nc.vector.tensor_scalar_min(out=neg_half_d2[h][:], in0=neg_half_d2[h][:], scalar1=-0.5 * D2_EPS)
 
         def distances(group):
-            for h in heads_of(group):
+            for a, h in enumerate(heads_of(group)):
                 for t in range(NT):
-                    c = h * NT + t
+                    c = a * NT + t
                     nc.scalar.activation(
                         out=neg_half_d2[h][:, t, :],
                         in_=neg_half_d2[h][:, t, :],
                         func=ACT.Sqrt,
-                        scale=sqrt_scale[:, c : c + 1],
+                        scale=sqrt_scale[group][:, c : c + 1],
                     )
                 nc.gpsimd.tensor_tensor(out=mixed[h][:], in0=mixed[h][:], in1=neg_half_d2[h][:], op=ALU.subtract)
 
         def exponentials(group):
             exp_bias = {}
             e = {}
-            for h in heads_of(group):
+            for a, h in enumerate(heads_of(group)):
                 neg_max = work.tile([P, NT], F32, name="neg_max")
                 nc.vector.tensor_reduce(out=neg_max[:], in_=mixed[h][:], axis=AX.X, op=ALU.max, negate=True)
                 exp_bias[h] = work.tile([P, NT], F32, name="exp_bias")
                 nc.vector.tensor_tensor(
-                    out=exp_bias[h][:], in0=neg_max[:], in1=q_rnorm[:, h * NT : (h + 1) * NT], op=ALU.mult
+                    out=exp_bias[h][:],
+                    in0=neg_max[:],
+                    in1=rnorm[group][:, QUERIES, a * NT : (a + 1) * NT],
+                    op=ALU.mult,
                 )
-            for h in heads_of(group):
-                e[h] = work.tile([P, NT, S], BF16, name="e")
+            for a, h in enumerate(heads_of(group)):
+                e[h] = work.tile([P, NT, S], BF16, name="e", bufs=GROUP)
                 for t in range(NT):
-                    c = h * NT + t
+                    c = a * NT + t
                     nc.scalar.activation(
                         out=e[h][:, t, :],
                         in_=mixed[h][:, t, :],
                         func=ACT.Exp,
-                        scale=q_rnorm[:, c : c + 1],
+                        scale=rnorm[group][:, QUERIES, c : c + 1],
                         bias=exp_bias[h][:, t : t + 1],
-                        accum_out=row_sum[:, c : c + 1],
+                        accum_out=row_sum[:, h * NT + t : h * NT + t + 1],
                     )
             for h in heads_of(group):
-                e_grouped[h] = work.tile([P, NT, P, 2], F32, name="e_grouped", align_bytes=64)
+                e_grouped[h] = work.tile([P, NT, P, 2], F32, name="e_grouped", bufs=GROUP + 1, align_bytes=64)
                 for t0 in range(0, NT, 2):
                     e_flipped = psum.tile([P, 2, 2, P], F32, tag="flip", name="e_flipped")
                     for a in range(2):
@@ -308,8 +248,8 @@ def tile_adaptiveattention_pa_kernel(tc, q, k, value, Wv, bv, scoring_weights, o
             e_codes = {}
             e_scales = {}
             for h in heads_of(group):
-                e_codes[h] = work.tile([P, S], U32, name="e_codes", align_bytes=64)
-                e_scales[h] = work.tile([P, S], U8, name="e_scales", align_bytes=64)
+                e_codes[h] = work.tile([P, S], U32, name="e_codes", bufs=GROUP, align_bytes=64)
+                e_scales[h] = work.tile([P, S], U8, name="e_scales", bufs=GROUP, align_bytes=64)
                 nc.vector.quantize_mx(
                     out=e_codes[h][:].bitcast(FP8X4),
                     scales=e_scales[h][:],
@@ -331,16 +271,93 @@ def tile_adaptiveattention_pa_kernel(tc, q, k, value, Wv, bv, scoring_weights, o
                     )
                 row_rsum = work.tile([P, NT], F32, name="row_rsum")
                 nc.vector.reciprocal(out=row_rsum[:], in_=row_sum[:, h * NT : (h + 1) * NT])
-                result = work.tile([P, NT, D], F32, name="result")
+                result = work.tile([P, NT, D], F32, name="result", bufs=GROUP)
                 nc.vector.tensor_tensor(
                     out=result[:], in0=ctx[:], in1=row_rsum[:].unsqueeze(2).to_broadcast([P, NT, D]), op=ALU.mult
                 )
                 nc.sync.dma_start(out=out_rows[:, :, head], in_=result[:])
 
+        value_codes = keep.tile([P, N_PASS, S], U32, align_bytes=64)
+        value_scales = keep.tile([P, N_PASS, S], U8, align_bytes=64)
+        wv_codes = keep.tile([P, N_PASS, HID], U32, align_bytes=64)
+        wv_scales = keep.tile([P, N_PASS, HID], U8, align_bytes=64)
+        v_codes = keep.tile([P, NH * D], U32, align_bytes=64)
+        v_scales = keep.tile([P, NH * D], U8, align_bytes=64)
+
+        def quantise_pass(block_of, n_blocks, codes, scales):
+            grouped = work.tile([P, HID, 2], F32, name="grouped", bufs=1, align_bytes=64)
+            for b0 in range(0, n_blocks, 2):
+                flipped = psum.tile([P, 2, 2 * P], F32, tag="flip", name="pass_flipped")
+                for a in range(2):
+                    words = block_of(b0 + a).bitcast(F32)
+                    for u in range(2):
+                        nc.tensor.transpose(
+                            out=flipped[:, u, a * P : (a + 1) * P],
+                            in_=words[:, u * P : (u + 1) * P],
+                            identity=ident_f[:],
+                        )
+                nc.scalar.copy(out=grouped[:, b0 * P : (b0 + 2) * P, :], in_=flipped[:].rearrange("p u r -> p r u"))
+            nc.vector.quantize_mx(
+                out=codes.bitcast(FP8X4),
+                scales=scales,
+                in_=grouped[:, 0 : n_blocks * P, :].rearrange("p r u -> p (r u)").bitcast(BF16),
+            )
+
+        def quantise_value_and_wv():
+            for g in range(N_PASS):
+                quantise_pass(
+                    lambda b: value_sb[:, b, g * K_PASS : (g + 1) * K_PASS],
+                    PACK,
+                    value_codes[:, g, :],
+                    value_scales[:, g, :],
+                )
+            for g in range(N_PASS):
+                quantise_pass(lambda b: wv_sb[:, g, b, :], NH, wv_codes[:, g, :], wv_scales[:, g, :])
+
+        def project():
+            v_grouped = work.tile([P, NH, D, PACK], BF16, bufs=1, align_bytes=64)
+            for h in range(NH):
+                head = slice(h * D, (h + 1) * D)
+                vp = psum.tile([P, PACK, D], F32, tag="acc", bufs=2, name="vp")
+                for t in range(PACK):
+                    block = slice(t * P, (t + 1) * P)
+                    for g in range(N_PASS):
+                        nc.tensor.matmul_mx(
+                            out=vp[:, t, :],
+                            lhsT=value_codes[:, g, block].bitcast(FP8X4),
+                            lhsT_scale=value_scales[:, g, block],
+                            rhs=wv_codes[:, g, head].bitcast(FP8X4),
+                            rhs_scale=wv_scales[:, g, head],
+                            start=(g == 0),
+                            stop=(g == N_PASS - 1),
+                        )
+                nc.vector.tensor_tensor(
+                    out=v_grouped[:, h, :, :],
+                    in0=vp[:].rearrange("p t d -> p d t"),
+                    in1=bv_bf[:, head].unsqueeze(2).to_broadcast([P, D, PACK]),
+                    op=ALU.add,
+                )
+            nc.vector.quantize_mx(
+                out=v_codes[:].bitcast(FP8X4), scales=v_scales[:], in_=v_grouped[:].rearrange("p h d t -> p (h d t)")
+            )
+
+        fill_in = (quantise_value_and_wv, project)
+        square_and_transpose(0)
+        norm_scalars(0)
+        spread_keys(0)
         for step in range(N_GROUPS + 2):
+            if step + 1 < N_GROUPS:
+                square_and_transpose(step + 1)
             if step < N_GROUPS:
                 scores(step)
+            if step + 1 < N_GROUPS:
+                norm_scalars(step + 1)
+            if step < N_GROUPS:
                 distances(step)
+            if step + 1 < N_GROUPS:
+                spread_keys(step + 1)
+            if step < len(fill_in):
+                fill_in[step]()
             if 1 <= step <= N_GROUPS:
                 exponentials(step - 1)
             if step >= 2:

@@ -191,7 +191,14 @@ def tile_adaptiveattention_pa_kernel(tc, q, k, value, Wv, bv, scoring_weights, o
                         op0=ALU.add,
                         op1=ALU.mult,
                     )
-                nc.vector.tensor_scalar_min(out=neg_half_d2[h][:], in0=neg_half_d2[h][:], scalar1=-0.5 * D2_EPS)
+                nc.gpsimd.tensor_scalar(
+                    out=neg_half_d2[h][:],
+                    in0=neg_half_d2[h][:],
+                    scalar1=-0.5 * D2_EPS,
+                    scalar2=-3.0e38,
+                    op0=ALU.min,
+                    op1=ALU.max,
+                )
 
         def distances(group):
             for a, h in enumerate(heads_of(group)):

@@ -81,6 +81,12 @@ def tile_adaptiveattention_pa_kernel(tc, q, k, value, Wv, bv, scoring_weights, o
         nc.vector.reciprocal(out=sw_rsum[:], in_=sw_sum[:])
         w = keep.tile([P, 3], F32)
         nc.vector.tensor_scalar_mul(out=w[:], in0=sw_exp[:], scalar1=sw_rsum[:])
+        euc_scale = keep.tile([P, 1], F32)
+        nc.vector.scalar_tensor_tensor(
+            out=euc_scale[:], in0=w[:, 2:3], scalar=-2.0, in1=w[:, 2:3], op0=ALU.mult, op1=ALU.mult
+        )
+        norm_floor = keep.tile([P, 1], F32)
+        nc.vector.memset(norm_floor[:], NORM_SQ_FLOOR)
 
         KEYS, QUERIES = 0, 1
         flipped_sb = {}
@@ -128,24 +134,20 @@ def tile_adaptiveattention_pa_kernel(tc, q, k, value, Wv, bv, scoring_weights, o
                 nc.vector.tensor_copy(out=flipped_sb[group][:, side, :, :], in_=flipped[:])
 
         def norm_scalars(group):
-            floored = small("floored", [P, 2, GC])
-            nc.vector.tensor_scalar_max(out=floored[:], in0=sq[group][:], scalar1=NORM_SQ_FLOOR)
+            half_sq[group] = small("half_sq", [P, 2, GC])
+            nc.scalar.activation(out=half_sq[group][:], in_=sq[group][:], func=ACT.Copy, scale=0.5)
             norm = small("norm", [P, 2, GC])
-            nc.scalar.activation(out=norm[:], in_=floored[:], func=ACT.Sqrt)
+            nc.scalar.activation(out=norm[:], in_=sq[group][:], func=ACT.Sqrt, bias=norm_floor[:])
             rnorm[group] = small("rnorm", [P, 2, GC])
             nc.vector.reciprocal(out=rnorm[group][:], in_=norm[:])
-            half_sq[group] = small("half_sq", [P, 2, GC])
-            nc.vector.tensor_scalar_mul(out=half_sq[group][:], in0=sq[group][:], scalar1=0.5)
-            cos_k[group] = small("cos_k", [P, GC])
-            nc.vector.tensor_scalar_mul(out=cos_k[group][:], in0=rnorm[group][:, KEYS, :], scalar1=w[:, 1:2])
             dot_q[group] = small("dot_q", [P, GC])
-            nc.vector.tensor_scalar_mul(out=dot_q[group][:], in0=norm[:, QUERIES, :], scalar1=w[:, 0:1])
-            euc_q = small("euc_q", [P, GC])
-            nc.vector.tensor_scalar_mul(out=euc_q[:], in0=norm[:, QUERIES, :], scalar1=w[:, 2:3])
+            nc.scalar.activation(out=dot_q[group][:], in_=norm[:, QUERIES, :], func=ACT.Copy, scale=w[:, 0:1])
             sqrt_scale[group] = small("sqrt_scale", [P, GC])
-            nc.vector.scalar_tensor_tensor(
-                out=sqrt_scale[group][:], in0=euc_q[:], scalar=-2.0, in1=euc_q[:], op0=ALU.mult, op1=ALU.mult
+            nc.scalar.activation(
+                out=sqrt_scale[group][:], in_=sq[group][:, QUERIES, :], func=ACT.Copy, scale=euc_scale[:]
             )
+            cos_k[group] = small("cos_k", [P, GC])
+            nc.scalar.activation(out=cos_k[group][:], in_=rnorm[group][:, KEYS, :], func=ACT.Copy, scale=w[:, 1:2])
 
         def spread_keys(group):
             key_rows[group] = work.tile([P, 2, GROUP, S], F32, name="key_rows", bufs=2)
@@ -219,12 +221,14 @@ def tile_adaptiveattention_pa_kernel(tc, q, k, value, Wv, bv, scoring_weights, o
                 neg_max = work.tile([P, NT], F32, name="neg_max")
                 nc.vector.tensor_reduce(out=neg_max[:], in_=mixed[h][:], axis=AX.X, op=ALU.max, negate=True)
                 exp_bias[h] = work.tile([P, NT], F32, name="exp_bias")
-                nc.vector.tensor_tensor(
-                    out=exp_bias[h][:],
-                    in0=neg_max[:],
-                    in1=rnorm[group][:, QUERIES, a * NT : (a + 1) * NT],
-                    op=ALU.mult,
-                )
+                for t in range(NT):
+                    c = a * NT + t
+                    nc.scalar.activation(
+                        out=exp_bias[h][:, t : t + 1],
+                        in_=neg_max[:, t : t + 1],
+                        func=ACT.Copy,
+                        scale=rnorm[group][:, QUERIES, c : c + 1],
+                    )
             for a, h in enumerate(heads_of(group)):
                 e[h] = work.tile([P, NT, S], BF16, name="e", bufs=GROUP)
                 for t in range(NT):

@@ -28,40 +28,50 @@ NORM_SQ_FLOOR = 1e-24
 FLOPS = 2 * S * HID * HID + 2 * 2 * NH * S * S * D
 
 
-GROUP = 2
-N_GROUPS = NH // GROUP
-GC = GROUP * NT
+BATCHES = ((0,), (1,), (2, 3), (4, 5), (6, 7))
+BATCH_OF = {h: (i, a) for i, batch in enumerate(BATCHES) for a, h in enumerate(batch)}
+KEYS, QUERIES = 0, 1
 
 
 def tile_adaptiveattention_pa_kernel(tc, q, k, value, Wv, bv, scoring_weights, out):
     nc = tc.nc
     with ExitStack() as stack:
         keep = stack.enter_context(tc.tile_pool(name="keep", bufs=1))
-        work = stack.enter_context(tc.tile_pool(name="work", bufs=2 * GROUP))
+        work = stack.enter_context(tc.tile_pool(name="work", bufs=2))
         psum = stack.enter_context(tc.psum_pool(name="psum", bufs=3))
+        engine = mybir.EngineType
+        stack.enter_context(tc.manual_schedule(engines={engine.DVE, engine.Activation, engine.Pool, engine.SP}))
 
         sw_bf = keep.tile([P, 3], BF16)
         nc.scalar.dma_start(out=sw_bf[:], in_=scoring_weights.partition_broadcast(P))
         k_rows = {}
         q_rows = {}
-        for group in range(N_GROUPS):
-            heads = slice(group * GROUP, (group + 1) * GROUP)
-            k_rows[group] = work.tile([P, GC, D], BF16, name="k_rows", bufs=N_GROUPS)
-            nc.sync.dma_start(out=k_rows[group][:], in_=k[0, heads].rearrange("h (t p) d -> p (h t) d", p=P))
-            q_rows[group] = work.tile([P, GC, D], BF16, name="q_rows", bufs=N_GROUPS)
+
+        def load_batch(i):
+            heads = slice(BATCHES[i][0], BATCHES[i][-1] + 1)
+            n = len(BATCHES[i]) * NT
+            k_rows[i] = keep.tile([P, n, D], BF16, name="k_rows%d" % i)
+            nc.sync.dma_start(out=k_rows[i][:], in_=k[0, heads].rearrange("h (t p) d -> p (h t) d", p=P))
+            q_rows[i] = keep.tile([P, n, D], BF16, name="q_rows%d" % i)
             nc.sync.dma_start(
-                out=q_rows[group][:].rearrange("p (h t) d -> p h (t d)", t=NT),
+                out=q_rows[i][:].rearrange("p (h t) d -> p h (t d)", t=NT),
                 in_=q[0, heads].rearrange("h (p t) d -> p h (t d)", t=NT),
             )
+
+        load_batch(0)
+        load_batch(1)
         value_sb = keep.tile([P, PACK, HID], BF16)
         nc.sync.dma_start(
             out=value_sb[:].rearrange("p (u e) c -> p u (e c)", e=2),
             in_=value.rearrange("b (u p e) c -> p (b u) (e c)", u=2, e=2),
         )
+        load_batch(2)
         wv_sb = keep.tile([P, N_PASS, NH, K_PASS], BF16)
         wv_passes = Wv.rearrange("(h p) (g c) -> p g h c", p=P, g=N_PASS)
         for g in range(N_PASS):
             nc.sync.dma_start(out=wv_sb[:, g, :, :], in_=wv_passes[:, g, :, :])
+        for i in range(3, len(BATCHES)):
+            load_batch(i)
         bv_bf = keep.tile([P, HID], BF16)
         nc.sync.dma_start(out=bv_bf[:], in_=bv.partition_broadcast(P))
 
@@ -87,206 +97,258 @@ def tile_adaptiveattention_pa_kernel(tc, q, k, value, Wv, bv, scoring_weights, o
         )
         norm_floor = keep.tile([P, 1], F32)
         nc.vector.memset(norm_floor[:], NORM_SQ_FLOOR)
+        unused = keep.tile([P, 3], F32)
+        nc.scalar.activation(out=unused[:], in_=sw_exp[:], func=ACT.Sqrt)
 
-        KEYS, QUERIES = 0, 1
         flipped_sb = {}
         key_rows = {}
-        half_sq = {}
+        sq = {}
+        norm = {}
         rnorm = {}
+        key_columns = {}
+        half_sq = {}
+        for i in range(len(BATCHES)):
+            key_columns[i] = keep.tile([P, P], F32, name="key_columns%d" % i)
+            nc.gpsimd.memset(key_columns[i][:], 0.0)
         dot_q = {}
         sqrt_scale = {}
         neg_half_d2 = {}
         mixed = {}
+        neg_max = {}
+        exp_bias = {}
+        e = {}
         e_grouped = {}
+        e_codes = {}
+        e_scales = {}
+        context = {}
         row_sum = keep.tile([P, NH * NT], F32)
         out_rows = out.rearrange("b (p t) c -> p (b t) c", t=NT)
 
-        def heads_of(group):
-            return range(group * GROUP, (group + 1) * GROUP)
+        def small(name, i, columns):
+            return keep.tile([P, columns], F32, name="%s%d" % (name, i))
 
-        def small(name, shape):
-            return work.tile(shape, F32, name=name, bufs=N_GROUPS)
-
-        sq = {}
-        cos_k = {}
-
-        def square_and_transpose(group):
-            both = (k_rows[group], q_rows[group])
-            squares = work.tile([P, 2, GC, D], BF16, name="squares", bufs=1)
-            sq[group] = small("sq", [P, 2, GC])
+        def squares(i, vector_sides=()):
+            n = len(BATCHES[i]) * NT
+            sq[i] = keep.tile([P, 2, n], F32, name="sq%d" % i)
             for side in (KEYS, QUERIES):
-                for c in range(GC):
+                rows = (k_rows, q_rows)[side][i]
+                if side in vector_sides:
+                    products = work.tile([P, n, D], F32, name="products", bufs=1)
+                    nc.vector.tensor_tensor(out=products[:], in0=rows[:], in1=rows[:], op=ALU.mult)
+                    nc.vector.tensor_reduce(out=sq[i][:, side, :], in_=products[:], axis=AX.X, op=ALU.add)
+                    continue
+                unused_squares = work.tile([P, n, D], BF16, name="unused_squares%d" % n, bufs=1)
+                for c in range(n):
                     nc.scalar.activation(
-                        out=squares[:, side, c, :],
-                        in_=both[side][:, c, :],
+                        out=unused_squares[:, c, :],
+                        in_=rows[:, c, :],
                         func=ACT.Square,
-                        accum_out=sq[group][:, side, c : c + 1],
+                        accum_out=sq[i][:, side, c : c + 1],
                     )
-            flipped_sb[group] = work.tile([P, 2, GROUP, S], BF16, name="flipped_sb", bufs=2)
-            for side in (KEYS, QUERIES):
-                flipped = psum.tile([P, GROUP, S], BF16, tag="flip", name="flipped")
-                for c in range(GC):
-                    nc.tensor.transpose(
-                        out=flipped[:, c // NT, (c % NT) * P : (c % NT + 1) * P],
-                        in_=both[side][:, c, :],
-                        identity=ident_b[:],
-                    )
-                nc.vector.tensor_copy(out=flipped_sb[group][:, side, :, :], in_=flipped[:])
 
-        def norm_scalars(group):
-            half_sq[group] = small("half_sq", [P, 2, GC])
-            nc.scalar.activation(out=half_sq[group][:], in_=sq[group][:], func=ACT.Copy, scale=0.5)
-            norm = small("norm", [P, 2, GC])
-            nc.scalar.activation(out=norm[:], in_=sq[group][:], func=ACT.Sqrt, bias=norm_floor[:])
-            rnorm[group] = small("rnorm", [P, 2, GC])
-            nc.vector.reciprocal(out=rnorm[group][:], in_=norm[:])
-            dot_q[group] = small("dot_q", [P, GC])
-            nc.scalar.activation(out=dot_q[group][:], in_=norm[:, QUERIES, :], func=ACT.Copy, scale=w[:, 0:1])
-            sqrt_scale[group] = small("sqrt_scale", [P, GC])
+        def flip_rows(i, side, copy):
+            n = len(BATCHES[i]) * NT
+            if side == KEYS:
+                flipped_sb[i] = keep.tile([P, 2, n // NT, S], BF16, name="flipped_sb%d" % i)
+            rows = (k_rows, q_rows)[side][i]
+            flipped = psum.tile([P, n * P], BF16, tag="flip", name="flipped")
+            for c in range(n):
+                nc.tensor.transpose(out=flipped[:, c * P : (c + 1) * P], in_=rows[:, c, :], identity=ident_b[:])
+            copy(out=flipped_sb[i][:, side, :, :].rearrange("p a s -> p (a s)"), in_=flipped[:])
+
+        def norm_scalars(i):
+            n = len(BATCHES[i]) * NT
+            norm[i] = keep.tile([P, 2, n], F32, name="norm%d" % i)
+            nc.scalar.activation(out=norm[i][:], in_=sq[i][:], func=ACT.Sqrt, bias=norm_floor[:])
+            nc.scalar.activation(out=key_columns[i][:, 0:n], in_=sq[i][:, KEYS, :], func=ACT.Copy, scale=0.5)
+            half_sq[i] = small("half_sq", i, n)
+            nc.scalar.activation(out=half_sq[i][:], in_=sq[i][:, QUERIES, :], func=ACT.Copy, scale=0.5)
+            dot_q[i] = small("dot_q", i, n)
+            nc.scalar.activation(out=dot_q[i][:], in_=norm[i][:, QUERIES, :], func=ACT.Copy, scale=w[:, 0:1])
+            sqrt_scale[i] = small("sqrt_scale", i, n)
+            nc.scalar.activation(out=sqrt_scale[i][:], in_=sq[i][:, QUERIES, :], func=ACT.Copy, scale=euc_scale[:])
+
+        def norm_inverses(i):
+            n = len(BATCHES[i]) * NT
+            rnorm[i] = keep.tile([P, 2, n], F32, name="rnorm%d" % i)
+            nc.vector.reciprocal(out=rnorm[i][:], in_=norm[i][:])
             nc.scalar.activation(
-                out=sqrt_scale[group][:], in_=sq[group][:, QUERIES, :], func=ACT.Copy, scale=euc_scale[:]
+                out=key_columns[i][:, n : 2 * n], in_=rnorm[i][:, KEYS, :], func=ACT.Copy, scale=w[:, 1:2]
             )
-            cos_k[group] = small("cos_k", [P, GC])
-            nc.scalar.activation(out=cos_k[group][:], in_=rnorm[group][:, KEYS, :], func=ACT.Copy, scale=w[:, 1:2])
 
-        def spread_keys(group):
-            key_rows[group] = work.tile([P, 2, GROUP, S], F32, name="key_rows", bufs=2)
-            for a in range(GROUP):
-                for which, columns in enumerate((half_sq[group][:, KEYS, :], cos_k[group][:])):
+        def spread_keys(i, copiers):
+            heads = len(BATCHES[i])
+            n = heads * NT
+            key_rows[i] = work.tile([P, 2, heads, S], F32, name="key_rows%d" % heads, bufs=2)
+            for a in range(heads):
+                for which in range(2):
                     spread = psum.tile([P, S], F32, tag="flip", name="spread")
                     for t in range(NT):
-                        c = a * NT + t
+                        c = which * n + a * NT + t
                         nc.tensor.transpose(
                             out=spread[:, t * P : (t + 1) * P],
-                            in_=columns[:, c : c + 1].to_broadcast([P, P]),
+                            in_=key_columns[i][:, c : c + 1].to_broadcast([P, P]),
                             identity=ident_f[:],
                         )
-                    nc.scalar.copy(out=key_rows[group][:, which, a, :], in_=spread[:])
+                    copiers[which](out=key_rows[i][:, which, a, :], in_=spread[:])
 
-        def scores(group):
-            for a, h in enumerate(heads_of(group)):
-                neg_half_d2[h] = work.tile([P, NT, S], F32, name="neg_half_d2")
-                mixed[h] = work.tile([P, NT, S], F32, name="mixed", bufs=3 * GROUP)
-                for t in range(NT):
-                    c = a * NT + t
-                    dot = psum.tile([P, S], F32, tag="dot")
-                    nc.tensor.matmul(
-                        out=dot[:],
-                        lhsT=flipped_sb[group][:, QUERIES, a, t * P : (t + 1) * P],
-                        rhs=flipped_sb[group][:, KEYS, a, :],
-                        start=True,
-                        stop=True,
-                    )
-                    nc.vector.scalar_tensor_tensor(
-                        out=neg_half_d2[h][:, t, :],
-                        in0=dot[:],
-                        scalar=half_sq[group][:, QUERIES, c : c + 1],
-                        in1=key_rows[group][:, 0, a, :],
-                        op0=ALU.subtract,
-                        op1=ALU.subtract,
-                    )
-                    nc.vector.scalar_tensor_tensor(
-                        out=mixed[h][:, t, :],
-                        in0=key_rows[group][:, 1, a, :],
-                        scalar=dot_q[group][:, c : c + 1],
-                        in1=dot[:],
-                        op0=ALU.add,
-                        op1=ALU.mult,
-                    )
-                nc.gpsimd.tensor_scalar(
-                    out=neg_half_d2[h][:],
-                    in0=neg_half_d2[h][:],
-                    scalar1=-0.5 * D2_EPS,
-                    scalar2=-3.0e38,
-                    op0=ALU.min,
-                    op1=ALU.max,
+        def park_keys(i):
+            heads = len(BATCHES[i])
+            n = heads * NT
+            turned = psum.tile([P, P], F32, tag="flip", name="turned")
+            nc.tensor.transpose(out=turned[:], in_=key_columns[i][:], identity=ident_f[:])
+            parked = work.tile([P, P], F32, name="parked", bufs=2)
+            nc.scalar.copy(out=parked[:], in_=turned[:])
+            rest = out[0, 2 * i : 2 * i + 2, :]
+            nc.sync.dma_start(out=rest.rearrange("w (c j) -> (w c) j", j=P), in_=parked[0 : 2 * n, :])
+            key_rows[i] = work.tile([P, 2, heads, S], F32, name="key_rows%d" % heads, bufs=2)
+            for which in range(2):
+                nc.sync.dma_start(
+                    out=key_rows[i][:, which, :, :].rearrange("p a j -> p (a j)"),
+                    in_=rest[which, :].partition_broadcast(P),
                 )
 
-        def distances(group):
-            for a, h in enumerate(heads_of(group)):
-                for t in range(NT):
-                    c = a * NT + t
-                    nc.scalar.activation(
-                        out=neg_half_d2[h][:, t, :],
-                        in_=neg_half_d2[h][:, t, :],
-                        func=ACT.Sqrt,
-                        scale=sqrt_scale[group][:, c : c + 1],
-                    )
-                nc.gpsimd.tensor_tensor(out=mixed[h][:], in0=mixed[h][:], in1=neg_half_d2[h][:], op=ALU.subtract)
-
-        def exponentials(group):
-            exp_bias = {}
-            e = {}
-            for a, h in enumerate(heads_of(group)):
-                neg_max = work.tile([P, NT], F32, name="neg_max")
-                nc.vector.tensor_reduce(out=neg_max[:], in_=mixed[h][:], axis=AX.X, op=ALU.max, negate=True)
-                exp_bias[h] = work.tile([P, NT], F32, name="exp_bias")
-                for t in range(NT):
-                    c = a * NT + t
-                    nc.scalar.activation(
-                        out=exp_bias[h][:, t : t + 1],
-                        in_=neg_max[:, t : t + 1],
-                        func=ACT.Copy,
-                        scale=rnorm[group][:, QUERIES, c : c + 1],
-                    )
-            for a, h in enumerate(heads_of(group)):
-                e[h] = work.tile([P, NT, S], BF16, name="e", bufs=GROUP)
-                for t in range(NT):
-                    c = a * NT + t
-                    nc.scalar.activation(
-                        out=e[h][:, t, :],
-                        in_=mixed[h][:, t, :],
-                        func=ACT.Exp,
-                        scale=rnorm[group][:, QUERIES, c : c + 1],
-                        bias=exp_bias[h][:, t : t + 1],
-                        accum_out=row_sum[:, h * NT + t : h * NT + t + 1],
-                    )
-            for h in heads_of(group):
-                e_grouped[h] = work.tile([P, NT, P, 2], F32, name="e_grouped", bufs=GROUP + 1, align_bytes=64)
-                for t0 in range(0, NT, 2):
-                    e_flipped = psum.tile([P, 2, 2, P], F32, tag="flip", name="e_flipped")
-                    for a in range(2):
-                        words = e[h][:, t0 + a, :].bitcast(F32)
-                        for u in range(2):
-                            nc.tensor.transpose(
-                                out=e_flipped[:, a, u, :], in_=words[:, u * P : (u + 1) * P], identity=ident_f[:]
-                            )
-                    nc.scalar.copy(
-                        out=e_grouped[h][:, t0 : t0 + 2, :, :], in_=e_flipped[:].rearrange("p a u i -> p a i u")
-                    )
-
-        def context(group):
-            e_codes = {}
-            e_scales = {}
-            for h in heads_of(group):
-                e_codes[h] = work.tile([P, S], U32, name="e_codes", bufs=GROUP, align_bytes=64)
-                e_scales[h] = work.tile([P, S], U8, name="e_scales", bufs=GROUP, align_bytes=64)
-                nc.vector.quantize_mx(
-                    out=e_codes[h][:].bitcast(FP8X4),
-                    scales=e_scales[h][:],
-                    in_=e_grouped[h][:].rearrange("p t i u -> p (t i u)").bitcast(BF16),
+        def dots(h, tiles=range(NT)):
+            i, a = BATCH_OF[h]
+            if 0 in tiles:
+                neg_half_d2[h] = work.tile([P, NT, S], F32, name="neg_half_d2", bufs=3)
+                mixed[h] = work.tile([P, NT, S], F32, name="mixed", bufs=5)
+            for t in tiles:
+                c = a * NT + t
+                dot = psum.tile([P, S], F32, tag="dot")
+                nc.tensor.matmul(
+                    out=dot[:],
+                    lhsT=flipped_sb[i][:, QUERIES, a, t * P : (t + 1) * P],
+                    rhs=flipped_sb[i][:, KEYS, a, :],
+                    start=True,
+                    stop=True,
                 )
-            for h in heads_of(group):
-                head = slice(h * D, (h + 1) * D)
-                ctx = psum.tile([P, NT, D], F32, tag="acc", bufs=2, name="ctx")
-                for t in range(NT):
-                    block = slice(t * P, (t + 1) * P)
-                    nc.tensor.matmul_mx(
-                        out=ctx[:, t, :],
-                        lhsT=e_codes[h][:, block].bitcast(FP8X4),
-                        lhsT_scale=e_scales[h][:, block],
-                        rhs=v_codes[:, head].bitcast(FP8X4),
-                        rhs_scale=v_scales[:, head],
-                        start=True,
-                        stop=True,
-                    )
-                row_rsum = work.tile([P, NT], F32, name="row_rsum")
-                nc.vector.reciprocal(out=row_rsum[:], in_=row_sum[:, h * NT : (h + 1) * NT])
-                result = work.tile([P, NT, D], F32, name="result", bufs=GROUP)
-                nc.vector.tensor_tensor(
-                    out=result[:], in0=ctx[:], in1=row_rsum[:].unsqueeze(2).to_broadcast([P, NT, D]), op=ALU.mult
+                nc.vector.scalar_tensor_tensor(
+                    out=mixed[h][:, t, :],
+                    in0=key_rows[i][:, 1, a, :],
+                    scalar=dot_q[i][:, c : c + 1],
+                    in1=dot[:],
+                    op0=ALU.add,
+                    op1=ALU.mult,
                 )
-                nc.sync.dma_start(out=out_rows[:, :, head], in_=result[:])
+                nc.vector.scalar_tensor_tensor(
+                    out=neg_half_d2[h][:, t, :],
+                    in0=dot[:],
+                    scalar=half_sq[i][:, c : c + 1],
+                    in1=key_rows[i][:, 0, a, :],
+                    op0=ALU.subtract,
+                    op1=ALU.subtract,
+                )
+
+        def floor(h, tiles=slice(0, NT), engine=None):
+            (engine or nc.gpsimd).tensor_scalar(
+                out=neg_half_d2[h][:, tiles, :],
+                in0=neg_half_d2[h][:, tiles, :],
+                scalar1=-0.5 * D2_EPS,
+                scalar2=-3.0e38,
+                op0=ALU.min,
+                op1=ALU.max,
+            )
+
+        def roots(h, tiles=range(NT)):
+            i, a = BATCH_OF[h]
+            for t in tiles:
+                c = a * NT + t
+                nc.scalar.activation(
+                    out=neg_half_d2[h][:, t, :],
+                    in_=neg_half_d2[h][:, t, :],
+                    func=ACT.Sqrt,
+                    scale=sqrt_scale[i][:, c : c + 1],
+                )
+
+        def subtract(h, tiles=slice(0, NT), engine=None):
+            (engine or nc.gpsimd).tensor_tensor(
+                out=mixed[h][:, tiles, :], in0=mixed[h][:, tiles, :], in1=neg_half_d2[h][:, tiles, :], op=ALU.subtract
+            )
+
+        def maxima(h, tiles=slice(0, NT)):
+            if tiles.start == 0:
+                neg_max[h] = work.tile([P, NT], F32, name="neg_max", bufs=4)
+            nc.vector.tensor_reduce(
+                out=neg_max[h][:, tiles], in_=mixed[h][:, tiles, :], axis=AX.X, op=ALU.max, negate=True
+            )
+
+        def biases(h, engine=None):
+            i, a = BATCH_OF[h]
+            exp_bias[h] = work.tile([P, NT], F32, name="exp_bias", bufs=4)
+            (engine or nc.gpsimd).tensor_tensor(
+                out=exp_bias[h][:],
+                in0=neg_max[h][:],
+                in1=rnorm[i][:, QUERIES, a * NT : (a + 1) * NT],
+                op=ALU.mult,
+            )
+
+        def exponentials(h, tiles=range(NT)):
+            i, a = BATCH_OF[h]
+            if 0 in tiles:
+                e[h] = work.tile([P, NT, S], BF16, name="e", bufs=3)
+            for t in tiles:
+                c = a * NT + t
+                nc.scalar.activation(
+                    out=e[h][:, t, :],
+                    in_=mixed[h][:, t, :],
+                    func=ACT.Exp,
+                    scale=rnorm[i][:, QUERIES, c : c + 1],
+                    bias=exp_bias[h][:, t : t + 1],
+                    accum_out=row_sum[:, h * NT + t : h * NT + t + 1],
+                )
+
+        def flip_e(h, halves=(0, 1), copiers=None):
+            copiers = copiers or (nc.scalar.copy,)
+            if 0 in halves:
+                e_grouped[h] = work.tile([P, NT, P, 2], F32, name="e_grouped", bufs=4, align_bytes=64)
+            for half in halves:
+                t0 = 2 * half
+                e_flipped = psum.tile([P, 2, 2, P], F32, tag="flip", name="e_flipped")
+                for b in range(2):
+                    words = e[h][:, t0 + b, :].bitcast(F32)
+                    for u in range(2):
+                        nc.tensor.transpose(
+                            out=e_flipped[:, b, u, :], in_=words[:, u * P : (u + 1) * P], identity=ident_f[:]
+                        )
+                copiers[half % len(copiers)](
+                    out=e_grouped[h][:, t0 : t0 + 2, :, :], in_=e_flipped[:].rearrange("p a u i -> p a i u")
+                )
+
+        def quantise_e(h, tiles=slice(0, NT)):
+            if tiles.start == 0:
+                e_codes[h] = work.tile([P, NT, P], U32, name="e_codes", bufs=2, align_bytes=64)
+                e_scales[h] = work.tile([P, NT, P], U8, name="e_scales", bufs=2, align_bytes=64)
+            nc.vector.quantize_mx(
+                out=e_codes[h][:, tiles, :].rearrange("p t i -> p (t i)").bitcast(FP8X4),
+                scales=e_scales[h][:, tiles, :].rearrange("p t i -> p (t i)"),
+                in_=e_grouped[h][:, tiles, :, :].rearrange("p t i u -> p (t i u)").bitcast(BF16),
+            )
+
+        def contract(h, tiles=range(NT)):
+            head = slice(h * D, (h + 1) * D)
+            if 0 in tiles:
+                context[h] = psum.tile([P, NT, D], F32, tag="acc", bufs=2, name="ctx")
+            for t in tiles:
+                nc.tensor.matmul_mx(
+                    out=context[h][:, t, :],
+                    lhsT=e_codes[h][:, t, :].bitcast(FP8X4),
+                    lhsT_scale=e_scales[h][:, t, :],
+                    rhs=v_codes[:, head].bitcast(FP8X4),
+                    rhs_scale=v_scales[:, head],
+                    start=True,
+                    stop=True,
+                )
+
+        def normalise(h):
+            head = slice(h * D, (h + 1) * D)
+            row_rsum = work.tile([P, NT], F32, name="row_rsum")
+            nc.vector.reciprocal(out=row_rsum[:], in_=row_sum[:, h * NT : (h + 1) * NT])
+            result = work.tile([P, NT, D], F32, name="result", bufs=2)
+            nc.vector.tensor_tensor(
+                out=result[:], in0=context[h][:], in1=row_rsum[:].unsqueeze(2).to_broadcast([P, NT, D]), op=ALU.mult
+            )
+            nc.sync.dma_start(out=out_rows[:, :, head], in_=result[:])
 
         value_codes = keep.tile([P, N_PASS, S], U32, align_bytes=64)
         value_scales = keep.tile([P, N_PASS, S], U8, align_bytes=64)
@@ -294,9 +356,9 @@ def tile_adaptiveattention_pa_kernel(tc, q, k, value, Wv, bv, scoring_weights, o
         wv_scales = keep.tile([P, N_PASS, HID], U8, align_bytes=64)
         v_codes = keep.tile([P, NH * D], U32, align_bytes=64)
         v_scales = keep.tile([P, NH * D], U8, align_bytes=64)
+        grouped = {}
 
-        def quantise_pass(block_of, n_blocks, codes, scales):
-            grouped = work.tile([P, HID, 2], F32, name="grouped", bufs=1, align_bytes=64)
+        def flip_pass(into, block_of, n_blocks, copy):
             for b0 in range(0, n_blocks, 2):
                 flipped = psum.tile([P, 2, 2 * P], F32, tag="flip", name="pass_flipped")
                 for a in range(2):
@@ -307,69 +369,155 @@ def tile_adaptiveattention_pa_kernel(tc, q, k, value, Wv, bv, scoring_weights, o
                             in_=words[:, u * P : (u + 1) * P],
                             identity=ident_f[:],
                         )
-                nc.scalar.copy(out=grouped[:, b0 * P : (b0 + 2) * P, :], in_=flipped[:].rearrange("p u r -> p r u"))
+                copy(out=into[:, b0 * P : (b0 + 2) * P, :], in_=flipped[:].rearrange("p u r -> p r u"))
+
+        def flip_value(g, copy):
+            if g == 0:
+                grouped["value"] = work.tile([P, N_PASS, S, 2], F32, name="grouped", bufs=2, align_bytes=64)
+            flip_pass(grouped["value"][:, g, :, :], lambda b: value_sb[:, b, g * K_PASS : (g + 1) * K_PASS], PACK, copy)
+
+        def quantise_value():
             nc.vector.quantize_mx(
-                out=codes.bitcast(FP8X4),
-                scales=scales,
-                in_=grouped[:, 0 : n_blocks * P, :].rearrange("p r u -> p (r u)").bitcast(BF16),
+                out=value_codes[:].rearrange("p g r -> p (g r)").bitcast(FP8X4),
+                scales=value_scales[:].rearrange("p g r -> p (g r)"),
+                in_=grouped["value"][:].rearrange("p g r u -> p (g r u)").bitcast(BF16),
             )
 
-        def quantise_value_and_wv():
-            for g in range(N_PASS):
-                quantise_pass(
-                    lambda b: value_sb[:, b, g * K_PASS : (g + 1) * K_PASS],
-                    PACK,
-                    value_codes[:, g, :],
-                    value_scales[:, g, :],
-                )
-            for g in range(N_PASS):
-                quantise_pass(lambda b: wv_sb[:, g, b, :], NH, wv_codes[:, g, :], wv_scales[:, g, :])
+        def flip_wv(g, copy):
+            grouped[g] = work.tile([P, HID, 2], F32, name="grouped", bufs=2, align_bytes=64)
+            flip_pass(grouped[g], lambda b: wv_sb[:, g, b, :], NH, copy)
 
-        def project():
-            v_grouped = work.tile([P, NH, D, PACK], BF16, bufs=1, align_bytes=64)
-            for h in range(NH):
-                head = slice(h * D, (h + 1) * D)
-                vp = psum.tile([P, PACK, D], F32, tag="acc", bufs=2, name="vp")
-                for t in range(PACK):
-                    block = slice(t * P, (t + 1) * P)
-                    for g in range(N_PASS):
-                        nc.tensor.matmul_mx(
-                            out=vp[:, t, :],
-                            lhsT=value_codes[:, g, block].bitcast(FP8X4),
-                            lhsT_scale=value_scales[:, g, block],
-                            rhs=wv_codes[:, g, head].bitcast(FP8X4),
-                            rhs_scale=wv_scales[:, g, head],
-                            start=(g == 0),
-                            stop=(g == N_PASS - 1),
-                        )
-                nc.vector.tensor_tensor(
-                    out=v_grouped[:, h, :, :],
-                    in0=vp[:].rearrange("p t d -> p d t"),
-                    in1=bv_bf[:, head].unsqueeze(2).to_broadcast([P, D, PACK]),
-                    op=ALU.add,
-                )
+        def quantise_wv(g):
+            nc.vector.quantize_mx(
+                out=wv_codes[:, g, :].bitcast(FP8X4),
+                scales=wv_scales[:, g, :],
+                in_=grouped[g][:].rearrange("p r u -> p (r u)").bitcast(BF16),
+            )
+
+        v_grouped = keep.tile([P, NH, D, PACK], BF16, align_bytes=64)
+
+        def project(h):
+            head = slice(h * D, (h + 1) * D)
+            vp = psum.tile([P, PACK, D], F32, tag="acc", bufs=2, name="vp")
+            for t in range(PACK):
+                block = slice(t * P, (t + 1) * P)
+                for g in range(N_PASS):
+                    nc.tensor.matmul_mx(
+                        out=vp[:, t, :],
+                        lhsT=value_codes[:, g, block].bitcast(FP8X4),
+                        lhsT_scale=value_scales[:, g, block],
+                        rhs=wv_codes[:, g, head].bitcast(FP8X4),
+                        rhs_scale=wv_scales[:, g, head],
+                        start=(g == 0),
+                        stop=(g == N_PASS - 1),
+                    )
+            nc.vector.tensor_tensor(
+                out=v_grouped[:, h, :, :],
+                in0=vp[:].rearrange("p t d -> p d t"),
+                in1=bv_bf[:, head].unsqueeze(2).to_broadcast([P, D, PACK]),
+                op=ALU.add,
+            )
+
+        def quantise_v():
             nc.vector.quantize_mx(
                 out=v_codes[:].bitcast(FP8X4), scales=v_scales[:], in_=v_grouped[:].rearrange("p h d t -> p (h d t)")
             )
 
-        fill_in = (quantise_value_and_wv, project)
-        square_and_transpose(0)
+        v_copy, s_copy = nc.vector.tensor_copy, nc.scalar.copy
+        squares(0, (KEYS,))
+        flip_rows(0, KEYS, v_copy)
+        flip_rows(0, QUERIES, v_copy)
         norm_scalars(0)
-        spread_keys(0)
-        for step in range(N_GROUPS + 2):
-            if step + 1 < N_GROUPS:
-                square_and_transpose(step + 1)
-            if step < N_GROUPS:
-                scores(step)
-            if step + 1 < N_GROUPS:
-                norm_scalars(step + 1)
-            if step < N_GROUPS:
-                distances(step)
-            if step + 1 < N_GROUPS:
-                spread_keys(step + 1)
-            if step < len(fill_in):
-                fill_in[step]()
-            if 1 <= step <= N_GROUPS:
-                exponentials(step - 1)
-            if step >= 2:
-                context(step - 2)
+        norm_inverses(0)
+        spread_keys(0, (v_copy, v_copy))
+        squares(1)
+        norm_scalars(1)
+        squares(2)
+        norm_scalars(2)
+        for h in range(NH):
+            last = h == NH - 1
+            if last:
+                dots(h, (0, 1))
+                floor(h, slice(0, 2))
+                dots(h, (2, 3))
+            else:
+                dots(h)
+            if h == 0:
+                norm_inverses(2)
+                park_keys(2)
+                flip_rows(1, KEYS, v_copy)
+                flip_rows(1, QUERIES, v_copy)
+                norm_inverses(1)
+                spread_keys(1, (v_copy, v_copy))
+                flip_value(0, s_copy)
+                flip_value(1, s_copy)
+            if h == 1:
+                quantise_value()
+            if 2 <= h <= 3:
+                quantise_wv(h - 2)
+            if h == 4:
+                quantise_v()
+            if 5 <= h:
+                quantise_e(h - 5)
+            if last:
+                floor(h, slice(2, 4))
+            else:
+                floor(h)
+            if h >= 1:
+                subtract(h - 1)
+            if h >= 5:
+                contract(h - 5)
+            if h >= 2:
+                maxima(h - 2)
+                biases(h - 2)
+            if h >= 5:
+                normalise(h - 5)
+            if h == 3:
+                for i in range(8):
+                    project(i)
+            if h in (2, 3):
+                i = 1 + h
+                norm_inverses(i)
+                park_keys(i)
+            roots(h)
+            if h < 3:
+                flip_rows(h + 2, KEYS, s_copy)
+                flip_rows(h + 2, QUERIES, s_copy)
+            if h < N_PASS:
+                flip_wv(h, s_copy)
+            if h in (0, 1):
+                squares(3 + h)
+                norm_scalars(3 + h)
+            if h >= 2 and h % 2 == 0:
+                heads = (0,) if h == 2 else (h - 3, h - 2)
+                for i in heads:
+                    exponentials(i)
+                for i in heads:
+                    flip_e(i)
+        exponentials(5)
+        quantise_e(3)
+        contract(3)
+        for t in (0, 2):
+            subtract(7, slice(t, t + 2), nc.vector)
+        normalise(3)
+        maxima(6)
+        biases(6)
+        maxima(7)
+        biases(7)
+        flip_e(5, copiers=(v_copy,))
+        quantise_e(4)
+        contract(4)
+        normalise(4)
+        exponentials(6)
+        quantise_e(5)
+        contract(5)
+        flip_e(6, copiers=(v_copy,))
+        normalise(5)
+        quantise_e(6)
+        contract(6)
+        exponentials(7)
+        normalise(6)
+        flip_e(7, copiers=(v_copy, s_copy))
+        quantise_e(7)
+        contract(7)
+        normalise(7)

@@ -23,6 +23,7 @@ K_PASS = P * PACK
 N_PASS = HID // K_PASS
 WORDS = K_PASS // 2
 D2_EPS = 1e-12
+LOG2_E = 1.4426950408889634
 NORM_SQ_FLOOR = 1e-24
 
 FLOPS = 2 * S * HID * HID + 2 * 2 * NH * S * S * D
@@ -39,8 +40,7 @@ def tile_adaptiveattention_pa_kernel(tc, q, k, value, Wv, bv, scoring_weights, o
         keep = stack.enter_context(tc.tile_pool(name="keep", bufs=1))
         work = stack.enter_context(tc.tile_pool(name="work", bufs=2))
         psum = stack.enter_context(tc.psum_pool(name="psum", bufs=3))
-        engine = mybir.EngineType
-        stack.enter_context(tc.manual_schedule(engines={engine.DVE, engine.Activation, engine.Pool, engine.SP}))
+        stack.enter_context(tc.manual_schedule(engines={mybir.EngineType.DVE, mybir.EngineType.Activation, mybir.EngineType.Pool, mybir.EngineType.SP}))
 
         sw_bf = keep.tile([P, 3], BF16)
         nc.scalar.dma_start(out=sw_bf[:], in_=scoring_weights.partition_broadcast(P))
@@ -75,30 +75,48 @@ def tile_adaptiveattention_pa_kernel(tc, q, k, value, Wv, bv, scoring_weights, o
         bv_bf = keep.tile([P, HID], BF16)
         nc.sync.dma_start(out=bv_bf[:], in_=bv.partition_broadcast(P))
 
+        ones = keep.tile([P, 1], F32)
+        nc.vector.memset(ones[:], 1.0)
+        unused = keep.tile([P, 1], F32)
+        nc.scalar.activation(out=unused[:], in_=ones[:], func=ACT.Sqrt)
         ident_b = keep.tile([P, P], BF16)
         make_identity(nc, ident_b[:])
         ident_f = keep.tile([P, P], F32)
         make_identity(nc, ident_f[:])
 
-        sw = keep.tile([P, 3], F32)
-        nc.vector.tensor_copy(out=sw[:], in_=sw_bf[:])
-        neg_sw_max = keep.tile([P, 1], F32)
-        nc.vector.tensor_reduce(out=neg_sw_max[:], in_=sw[:], axis=AX.X, op=ALU.max, negate=True)
-        sw_exp = keep.tile([P, 3], F32)
-        sw_sum = keep.tile([P, 1], F32)
-        nc.scalar.activation(out=sw_exp[:], in_=sw[:], func=ACT.Exp, bias=neg_sw_max[:], accum_out=sw_sum[:])
-        sw_rsum = keep.tile([P, 1], F32)
-        nc.vector.reciprocal(out=sw_rsum[:], in_=sw_sum[:])
         w = keep.tile([P, 3], F32)
-        nc.vector.tensor_scalar_mul(out=w[:], in0=sw_exp[:], scalar1=sw_rsum[:])
         euc_scale = keep.tile([P, 1], F32)
-        nc.vector.scalar_tensor_tensor(
-            out=euc_scale[:], in0=w[:, 2:3], scalar=-2.0, in1=w[:, 2:3], op0=ALU.mult, op1=ALU.mult
-        )
+
+        def mixing_powers():
+            neg_sw_max = keep.tile([P, 1], F32)
+            nc.vector.tensor_reduce(out=neg_sw_max[:], in_=sw_bf[:], axis=AX.X, op=ALU.max, negate=True)
+            sw_log2 = keep.tile([P, 3], F32)
+            nc.vector.tensor_scalar(
+                out=sw_log2[:],
+                in0=sw_bf[:],
+                scalar1=neg_sw_max[:],
+                scalar2=LOG2_E,
+                op0=ALU.add,
+                op1=ALU.mult,
+            )
+            two = keep.tile([P, 3], F32)
+            nc.gpsimd.memset(two[:], 2.0)
+            sw_exp = keep.tile([P, 3], F32)
+            nc.gpsimd.tensor_tensor(out=sw_exp[:], in0=two[:], in1=sw_log2[:], op=ALU.pow)
+            return sw_exp
+
+        def mixing_weights(sw_exp):
+            sw_sum = keep.tile([P, 1], F32)
+            nc.vector.tensor_reduce(out=sw_sum[:], in_=sw_exp[:], axis=AX.X, op=ALU.add)
+            sw_rsum = keep.tile([P, 1], F32)
+            nc.vector.reciprocal(out=sw_rsum[:], in_=sw_sum[:])
+            nc.vector.tensor_scalar_mul(out=w[:], in0=sw_exp[:], scalar1=sw_rsum[:])
+            nc.vector.scalar_tensor_tensor(
+                out=euc_scale[:], in0=w[:, 2:3], scalar=-2.0, in1=w[:, 2:3], op0=ALU.mult, op1=ALU.mult
+            )
+
         norm_floor = keep.tile([P, 1], F32)
         nc.vector.memset(norm_floor[:], NORM_SQ_FLOOR)
-        unused = keep.tile([P, 3], F32)
-        nc.scalar.activation(out=unused[:], in_=sw_exp[:], func=ACT.Sqrt)
 
         flipped_sb = {}
         key_rows = {}
@@ -109,7 +127,7 @@ def tile_adaptiveattention_pa_kernel(tc, q, k, value, Wv, bv, scoring_weights, o
         half_sq = {}
         for i in range(len(BATCHES)):
             key_columns[i] = keep.tile([P, P], F32, name="key_columns%d" % i)
-            nc.gpsimd.memset(key_columns[i][:], 0.0)
+            nc.vector.memset(key_columns[i][:], 0.0)
         dot_q = {}
         sqrt_scale = {}
         neg_half_d2 = {}
@@ -127,16 +145,11 @@ def tile_adaptiveattention_pa_kernel(tc, q, k, value, Wv, bv, scoring_weights, o
         def small(name, i, columns):
             return keep.tile([P, columns], F32, name="%s%d" % (name, i))
 
-        def squares(i, vector_sides=()):
+        def squares(i):
             n = len(BATCHES[i]) * NT
             sq[i] = keep.tile([P, 2, n], F32, name="sq%d" % i)
             for side in (KEYS, QUERIES):
                 rows = (k_rows, q_rows)[side][i]
-                if side in vector_sides:
-                    products = work.tile([P, n, D], F32, name="products", bufs=1)
-                    nc.vector.tensor_tensor(out=products[:], in0=rows[:], in1=rows[:], op=ALU.mult)
-                    nc.vector.tensor_reduce(out=sq[i][:, side, :], in_=products[:], axis=AX.X, op=ALU.add)
-                    continue
                 unused_squares = work.tile([P, n, D], BF16, name="unused_squares%d" % n, bufs=1)
                 for c in range(n):
                     nc.scalar.activation(
@@ -144,6 +157,22 @@ def tile_adaptiveattention_pa_kernel(tc, q, k, value, Wv, bv, scoring_weights, o
                         in_=rows[:, c, :],
                         func=ACT.Square,
                         accum_out=sq[i][:, side, c : c + 1],
+                    )
+
+        def squares_of_flipped(i):
+            n = len(BATCHES[i]) * NT
+            sq[i] = psum.tile([P, 2, n], F32, tag="acc", bufs=2, name="sq")
+            for side in (KEYS, QUERIES):
+                products = work.tile([P, n * P], F32, name="flipped_squares", bufs=2)
+                rows = flipped_sb[i][:, side, :, :].rearrange("p a s -> p (a s)")
+                nc.gpsimd.tensor_tensor(out=products[:], in0=rows, in1=rows, op=ALU.mult)
+                for c in range(n):
+                    nc.tensor.matmul(
+                        out=sq[i][:, side, c : c + 1],
+                        lhsT=products[:, c * P : (c + 1) * P],
+                        rhs=ones[:],
+                        start=True,
+                        stop=True,
                     )
 
         def flip_rows(i, side, copy):
@@ -163,6 +192,9 @@ def tile_adaptiveattention_pa_kernel(tc, q, k, value, Wv, bv, scoring_weights, o
             nc.scalar.activation(out=key_columns[i][:, 0:n], in_=sq[i][:, KEYS, :], func=ACT.Copy, scale=0.5)
             half_sq[i] = small("half_sq", i, n)
             nc.scalar.activation(out=half_sq[i][:], in_=sq[i][:, QUERIES, :], func=ACT.Copy, scale=0.5)
+
+        def norm_products(i):
+            n = len(BATCHES[i]) * NT
             dot_q[i] = small("dot_q", i, n)
             nc.scalar.activation(out=dot_q[i][:], in_=norm[i][:, QUERIES, :], func=ACT.Copy, scale=w[:, 0:1])
             sqrt_scale[i] = small("sqrt_scale", i, n)
@@ -182,7 +214,7 @@ def tile_adaptiveattention_pa_kernel(tc, q, k, value, Wv, bv, scoring_weights, o
             key_rows[i] = work.tile([P, 2, heads, S], F32, name="key_rows%d" % heads, bufs=2)
             for a in range(heads):
                 for which in range(2):
-                    spread = psum.tile([P, S], F32, tag="flip", name="spread")
+                    spread = psum.tile([P, S], F32, tag="dot", name="spread")
                     for t in range(NT):
                         c = which * n + a * NT + t
                         nc.tensor.transpose(
@@ -195,7 +227,7 @@ def tile_adaptiveattention_pa_kernel(tc, q, k, value, Wv, bv, scoring_weights, o
         def park_keys(i):
             heads = len(BATCHES[i])
             n = heads * NT
-            turned = psum.tile([P, P], F32, tag="flip", name="turned")
+            turned = psum.tile([P, P], F32, tag="acc", bufs=2, name="turned")
             nc.tensor.transpose(out=turned[:], in_=key_columns[i][:], identity=ident_f[:])
             parked = work.tile([P, P], F32, name="parked", bufs=2)
             nc.scalar.copy(out=parked[:], in_=turned[:])
@@ -301,7 +333,7 @@ def tile_adaptiveattention_pa_kernel(tc, q, k, value, Wv, bv, scoring_weights, o
         def flip_e(h, halves=(0, 1), copiers=None):
             copiers = copiers or (nc.scalar.copy,)
             if 0 in halves:
-                e_grouped[h] = work.tile([P, NT, P, 2], F32, name="e_grouped", bufs=4, align_bytes=64)
+                e_grouped[h] = work.tile([P, NT, P, 2], F32, name="e_grouped", bufs=3, align_bytes=64)
             for half in halves:
                 t0 = 2 * half
                 e_flipped = psum.tile([P, 2, 2, P], F32, tag="flip", name="e_flipped")
@@ -340,11 +372,18 @@ def tile_adaptiveattention_pa_kernel(tc, q, k, value, Wv, bv, scoring_weights, o
                     stop=True,
                 )
 
-        def normalise(h):
+        def normalise(h, on_scalar=False):
             head = slice(h * D, (h + 1) * D)
             row_rsum = work.tile([P, NT], F32, name="row_rsum")
             nc.vector.reciprocal(out=row_rsum[:], in_=row_sum[:, h * NT : (h + 1) * NT])
-            result = work.tile([P, NT, D], F32, name="result", bufs=2)
+            result = work.tile([P, NT, D], F32, name="result", bufs=3)
+            if on_scalar:
+                for t in range(NT):
+                    nc.scalar.activation(
+                        out=result[:, t, :], in_=context[h][:, t, :], func=ACT.Copy, scale=row_rsum[:, t : t + 1]
+                    )
+                nc.sync.dma_start(out=out_rows[:, :, head], in_=result[:])
+                return
             nc.vector.tensor_tensor(
                 out=result[:], in0=context[h][:], in1=row_rsum[:].unsqueeze(2).to_broadcast([P, NT, D]), op=ALU.mult
             )
@@ -394,10 +433,11 @@ def tile_adaptiveattention_pa_kernel(tc, q, k, value, Wv, bv, scoring_weights, o
                 in_=grouped[g][:].rearrange("p r u -> p (r u)").bitcast(BF16),
             )
 
-        v_grouped = keep.tile([P, NH, D, PACK], BF16, align_bytes=64)
 
         def project(h):
             head = slice(h * D, (h + 1) * D)
+            if h == 0:
+                grouped["v"] = work.tile([P, NH, D, PACK], BF16, name="grouped", bufs=2, align_bytes=64)
             vp = psum.tile([P, PACK, D], F32, tag="acc", bufs=2, name="vp")
             for t in range(PACK):
                 block = slice(t * P, (t + 1) * P)
@@ -412,7 +452,7 @@ def tile_adaptiveattention_pa_kernel(tc, q, k, value, Wv, bv, scoring_weights, o
                         stop=(g == N_PASS - 1),
                     )
             nc.vector.tensor_tensor(
-                out=v_grouped[:, h, :, :],
+                out=grouped["v"][:, h, :, :],
                 in0=vp[:].rearrange("p t d -> p d t"),
                 in1=bv_bf[:, head].unsqueeze(2).to_broadcast([P, D, PACK]),
                 op=ALU.add,
@@ -420,104 +460,158 @@ def tile_adaptiveattention_pa_kernel(tc, q, k, value, Wv, bv, scoring_weights, o
 
         def quantise_v():
             nc.vector.quantize_mx(
-                out=v_codes[:].bitcast(FP8X4), scales=v_scales[:], in_=v_grouped[:].rearrange("p h d t -> p (h d t)")
+                out=v_codes[:].bitcast(FP8X4), scales=v_scales[:], in_=grouped["v"][:].rearrange("p h d t -> p (h d t)")
             )
 
         v_copy, s_copy = nc.vector.tensor_copy, nc.scalar.copy
-        squares(0, (KEYS,))
+        sw_exp = mixing_powers()
+        squares(0)
         flip_rows(0, KEYS, v_copy)
         flip_rows(0, QUERIES, v_copy)
         norm_scalars(0)
+        mixing_weights(sw_exp)
+        norm_products(0)
         norm_inverses(0)
-        spread_keys(0, (v_copy, v_copy))
-        squares(1)
+        flip_rows(1, KEYS, v_copy)
+        flip_rows(1, QUERIES, v_copy)
+        spread_keys(0, (s_copy, v_copy))
+        squares_of_flipped(1)
+        flip_rows(2, KEYS, s_copy)
+        flip_rows(2, QUERIES, s_copy)
+        squares_of_flipped(2)
         norm_scalars(1)
-        squares(2)
+        norm_products(1)
+        dots(0, (0, 1))
+        norm_inverses(1)
+        dots(0, (2, 3))
+        spread_keys(1, (s_copy, s_copy))
+        flip_value(0, s_copy)
         norm_scalars(2)
-        for h in range(NH):
-            last = h == NH - 1
-            if last:
-                dots(h, (0, 1))
-                floor(h, slice(0, 2))
-                dots(h, (2, 3))
-            else:
-                dots(h)
-            if h == 0:
-                norm_inverses(2)
-                park_keys(2)
-                flip_rows(1, KEYS, v_copy)
-                flip_rows(1, QUERIES, v_copy)
-                norm_inverses(1)
-                spread_keys(1, (v_copy, v_copy))
-                flip_value(0, s_copy)
-                flip_value(1, s_copy)
-            if h == 1:
-                quantise_value()
-            if 2 <= h <= 3:
-                quantise_wv(h - 2)
-            if h == 4:
-                quantise_v()
-            if 5 <= h:
-                quantise_e(h - 5)
-            if last:
-                floor(h, slice(2, 4))
-            else:
-                floor(h)
-            if h >= 1:
-                subtract(h - 1)
-            if h >= 5:
-                contract(h - 5)
-            if h >= 2:
-                maxima(h - 2)
-                biases(h - 2)
-            if h >= 5:
-                normalise(h - 5)
-            if h == 3:
-                for i in range(8):
-                    project(i)
-            if h in (2, 3):
-                i = 1 + h
-                norm_inverses(i)
-                park_keys(i)
-            roots(h)
-            if h < 3:
-                flip_rows(h + 2, KEYS, s_copy)
-                flip_rows(h + 2, QUERIES, s_copy)
-            if h < N_PASS:
-                flip_wv(h, s_copy)
-            if h in (0, 1):
-                squares(3 + h)
-                norm_scalars(3 + h)
-            if h >= 2 and h % 2 == 0:
-                heads = (0,) if h == 2 else (h - 3, h - 2)
-                for i in heads:
-                    exponentials(i)
-                for i in heads:
-                    flip_e(i)
+        norm_products(2)
+        flip_value(1, s_copy)
+        floor(0)
+        dots(1, (0, 1))
+        norm_inverses(2)
+        roots(0)
+        squares(3)
+        norm_scalars(3)
+        norm_products(3)
+        flip_wv(0, s_copy)
+        dots(1, (2, 3))
+        quantise_value()
+        spread_keys(2, (v_copy, v_copy))
+        floor(1)
+        subtract(0)
+        dots(2, (0, 1))
+        norm_inverses(3)
+        park_keys(3)
+        roots(1)
+        flip_wv(1, s_copy)
+        flip_rows(3, KEYS, s_copy)
+        flip_rows(3, QUERIES, s_copy)
+        squares(4)
+        norm_scalars(4)
+        norm_products(4)
+        dots(2, (2, 3))
+        quantise_wv(0)
+        floor(2)
+        subtract(1)
+        maxima(0)
+        biases(0)
+        dots(3, (0, 1))
+        roots(2)
+        flip_rows(4, KEYS, s_copy)
+        flip_rows(4, QUERIES, s_copy)
+        dots(3, (2, 3))
+        quantise_wv(1)
+        floor(3)
+        subtract(2)
+        maxima(1)
+        biases(1)
+        project(0)
+        project(1)
+        project(2)
+        project(3)
+        dots(4, (0, 1))
+        norm_inverses(4)
+        park_keys(4)
+        roots(3)
+        exponentials(0)
+        exponentials(1)
+        flip_e(0)
+        flip_e(1)
+        dots(4, (2, 3))
+        floor(4)
+        subtract(3)
+        maxima(2)
+        biases(2)
+        project(4)
+        project(5)
+        project(6)
+        project(7)
+        dots(5, (0, 1))
+        roots(4)
+        dots(5, (2, 3))
+        quantise_v()
+        quantise_e(0)
+        floor(5)
+        subtract(4)
+        contract(0)
+        maxima(3)
+        biases(3)
+        normalise(0)
+        dots(6, (0, 1))
+        roots(5)
+        exponentials(2)
+        exponentials(3)
+        flip_e(2)
+        flip_e(3)
+        dots(6, (2, 3))
+        quantise_e(1)
+        floor(6)
+        subtract(5)
+        contract(1)
+        maxima(4)
+        biases(4)
+        normalise(1)
+        dots(7, (0, 1))
+        floor(7, slice(0, 2))
+        roots(6)
+        dots(7, (2, 3))
+        quantise_e(2)
+        floor(7, slice(2, 4))
+        subtract(6)
+        contract(2)
+        maxima(5)
+        biases(5)
+        normalise(2)
+        roots(7)
+        exponentials(4)
         exponentials(5)
         quantise_e(3)
         contract(3)
-        for t in (0, 2):
-            subtract(7, slice(t, t + 2), nc.vector)
-        normalise(3)
+        subtract(7, slice(0, 2), nc.vector)
+        subtract(7, slice(2, 4), nc.vector)
         maxima(6)
         biases(6)
         maxima(7)
         biases(7)
-        flip_e(5, copiers=(v_copy,))
-        quantise_e(4)
-        contract(4)
-        normalise(4)
         exponentials(6)
+        exponentials(7)
+        flip_e(4, copiers=(v_copy,))
+        quantise_e(4)
+        normalise(3)
+        contract(4)
+        flip_e(5, copiers=(v_copy,))
         quantise_e(5)
         contract(5)
-        flip_e(6, copiers=(v_copy,))
-        normalise(5)
+        normalise(4)
+        flip_e(6, copiers=(s_copy,))
         quantise_e(6)
         contract(6)
-        exponentials(7)
-        normalise(6)
-        flip_e(7, copiers=(v_copy, s_copy))
+        normalise(5)
+        flip_e(7, copiers=(s_copy,))
         quantise_e(7)
         contract(7)
+        normalise(6, True)
         normalise(7)

@@ -31,6 +31,7 @@ FLOPS = 2 * S * HID * HID + 2 * 2 * NH * S * S * D
 
 BATCHES = ((0,), (1,), (2, 3), (4, 5), (6, 7))
 BATCH_OF = {h: (i, a) for i, batch in enumerate(BATCHES) for a, h in enumerate(batch)}
+KEEP, KEEP_E = 0, 0
 KEYS, QUERIES = 0, 1
 
 
@@ -75,10 +76,12 @@ def tile_adaptiveattention_pa_kernel(tc, q, k, value, Wv, bv, scoring_weights, o
         bv_bf = keep.tile([P, HID], BF16)
         nc.sync.dma_start(out=bv_bf[:], in_=bv.partition_broadcast(P))
 
-        ones = keep.tile([P, 1], F32)
+        zeros = keep.tile([P, P], F32)
+        nc.vector.memset(zeros[:], 0.0)
+        ones = keep.tile([P, 64], F32)
         nc.vector.memset(ones[:], 1.0)
         unused = keep.tile([P, 1], F32)
-        nc.scalar.activation(out=unused[:], in_=ones[:], func=ACT.Sqrt)
+        nc.scalar.activation(out=unused[:], in_=ones[:, 0:1], func=ACT.Sqrt)
         ident_b = keep.tile([P, P], BF16)
         make_identity(nc, ident_b[:])
         ident_f = keep.tile([P, P], F32)
@@ -145,9 +148,18 @@ def tile_adaptiveattention_pa_kernel(tc, q, k, value, Wv, bv, scoring_weights, o
         def small(name, i, columns):
             return keep.tile([P, columns], F32, name="%s%d" % (name, i))
 
+        def keep_clock(bank):
+            nc.tensor.matmul(out=bank, lhsT=ident_f[:], rhs=ident_f[:, 0 : bank.shape[1]], start=True, stop=True)
+
+        def warm_up(n):
+            warm = psum.tile([P, P], F32, tag="dot", name="warm")
+            for i in range(n):
+                nc.tensor.matmul(out=warm[:], lhsT=zeros[:], rhs=zeros[:], start=True, stop=True)
+
         def squares(i):
             n = len(BATCHES[i]) * NT
-            sq[i] = keep.tile([P, 2, n], F32, name="sq%d" % i)
+            sq_tile = keep.tile([P, 2, n], F32, name="sq%d" % i)
+            sq[i] = sq_tile[:]
             for side in (KEYS, QUERIES):
                 rows = (k_rows, q_rows)[side][i]
                 unused_squares = work.tile([P, n, D], BF16, name="unused_squares%d" % n, bufs=1)
@@ -161,14 +173,15 @@ def tile_adaptiveattention_pa_kernel(tc, q, k, value, Wv, bv, scoring_weights, o
 
         def squares_of_flipped(i):
             n = len(BATCHES[i]) * NT
-            sq[i] = psum.tile([P, 2, n], F32, tag="acc", bufs=2, name="sq")
+            sums = psum.tile([P, 2, n + 64 - 1], F32, tag="acc", bufs=2, name="sums")
+            sq[i] = sums[:, :, 0:n]
             for side in (KEYS, QUERIES):
                 products = work.tile([P, n * P], F32, name="flipped_squares", bufs=2)
                 rows = flipped_sb[i][:, side, :, :].rearrange("p a s -> p (a s)")
                 nc.gpsimd.tensor_tensor(out=products[:], in0=rows, in1=rows, op=ALU.mult)
                 for c in range(n):
                     nc.tensor.matmul(
-                        out=sq[i][:, side, c : c + 1],
+                        out=sums[:, side, c : c + 64],
                         lhsT=products[:, c * P : (c + 1) * P],
                         rhs=ones[:],
                         start=True,
@@ -188,7 +201,7 @@ def tile_adaptiveattention_pa_kernel(tc, q, k, value, Wv, bv, scoring_weights, o
         def norm_scalars(i):
             n = len(BATCHES[i]) * NT
             norm[i] = keep.tile([P, 2, n], F32, name="norm%d" % i)
-            nc.scalar.activation(out=norm[i][:], in_=sq[i][:], func=ACT.Sqrt, bias=norm_floor[:])
+            nc.scalar.activation(out=norm[i][:], in_=sq[i], func=ACT.Sqrt, bias=norm_floor[:])
             nc.scalar.activation(out=key_columns[i][:, 0:n], in_=sq[i][:, KEYS, :], func=ACT.Copy, scale=0.5)
             half_sq[i] = small("half_sq", i, n)
             nc.scalar.activation(out=half_sq[i][:], in_=sq[i][:, QUERIES, :], func=ACT.Copy, scale=0.5)
@@ -214,7 +227,7 @@ def tile_adaptiveattention_pa_kernel(tc, q, k, value, Wv, bv, scoring_weights, o
             key_rows[i] = work.tile([P, 2, heads, S], F32, name="key_rows%d" % heads, bufs=2)
             for a in range(heads):
                 for which in range(2):
-                    spread = psum.tile([P, S], F32, tag="dot", name="spread")
+                    spread = psum.tile([P, S], F32, tag="flip", name="spread")
                     for t in range(NT):
                         c = which * n + a * NT + t
                         nc.tensor.transpose(
@@ -240,6 +253,20 @@ def tile_adaptiveattention_pa_kernel(tc, q, k, value, Wv, bv, scoring_weights, o
                     in_=rest[which, :].partition_broadcast(P),
                 )
 
+        dot = {}
+
+        def multiply(h, tiles):
+            i, a = BATCH_OF[h]
+            for t in tiles:
+                dot[h, t] = psum.tile([P, S], F32, tag="dot", name="dot")
+                nc.tensor.matmul(
+                    out=dot[h, t][:],
+                    lhsT=flipped_sb[i][:, QUERIES, a, t * P : (t + 1) * P],
+                    rhs=flipped_sb[i][:, KEYS, a, :],
+                    start=True,
+                    stop=True,
+                )
+
         def dots(h, tiles=range(NT)):
             i, a = BATCH_OF[h]
             if 0 in tiles:
@@ -247,25 +274,19 @@ def tile_adaptiveattention_pa_kernel(tc, q, k, value, Wv, bv, scoring_weights, o
                 mixed[h] = work.tile([P, NT, S], F32, name="mixed", bufs=5)
             for t in tiles:
                 c = a * NT + t
-                dot = psum.tile([P, S], F32, tag="dot")
-                nc.tensor.matmul(
-                    out=dot[:],
-                    lhsT=flipped_sb[i][:, QUERIES, a, t * P : (t + 1) * P],
-                    rhs=flipped_sb[i][:, KEYS, a, :],
-                    start=True,
-                    stop=True,
-                )
+                if (h, t) not in dot:
+                    multiply(h, (t,))
                 nc.vector.scalar_tensor_tensor(
                     out=mixed[h][:, t, :],
                     in0=key_rows[i][:, 1, a, :],
                     scalar=dot_q[i][:, c : c + 1],
-                    in1=dot[:],
+                    in1=dot[h, t][:],
                     op0=ALU.add,
                     op1=ALU.mult,
                 )
                 nc.vector.scalar_tensor_tensor(
                     out=neg_half_d2[h][:, t, :],
-                    in0=dot[:],
+                    in0=dot[h, t][:],
                     scalar=half_sq[i][:, c : c + 1],
                     in1=key_rows[i][:, 0, a, :],
                     op0=ALU.subtract,
@@ -337,6 +358,8 @@ def tile_adaptiveattention_pa_kernel(tc, q, k, value, Wv, bv, scoring_weights, o
             for half in halves:
                 t0 = 2 * half
                 e_flipped = psum.tile([P, 2, 2, P], F32, tag="flip", name="e_flipped")
+                if KEEP_E:
+                    keep_clock(e_flipped[:, 0, 0, 0:KEEP_E])
                 for b in range(2):
                     words = e[h][:, t0 + b, :].bitcast(F32)
                     for u in range(2):
@@ -464,6 +487,7 @@ def tile_adaptiveattention_pa_kernel(tc, q, k, value, Wv, bv, scoring_weights, o
             )
 
         v_copy, s_copy = nc.vector.tensor_copy, nc.scalar.copy
+        warm_up(5)
         sw_exp = mixing_powers()
         squares(0)
         flip_rows(0, KEYS, v_copy)
@@ -476,22 +500,23 @@ def tile_adaptiveattention_pa_kernel(tc, q, k, value, Wv, bv, scoring_weights, o
         flip_rows(1, QUERIES, v_copy)
         spread_keys(0, (s_copy, v_copy))
         squares_of_flipped(1)
-        flip_rows(2, KEYS, s_copy)
-        flip_rows(2, QUERIES, s_copy)
-        squares_of_flipped(2)
+        squares(2)
+        norm_scalars(2)
+        norm_products(2)
         norm_scalars(1)
         norm_products(1)
         dots(0, (0, 1))
         norm_inverses(1)
+        norm_inverses(2)
+        park_keys(2)
         dots(0, (2, 3))
         spread_keys(1, (s_copy, s_copy))
+        flip_rows(2, KEYS, s_copy)
+        flip_rows(2, QUERIES, s_copy)
         flip_value(0, s_copy)
-        norm_scalars(2)
-        norm_products(2)
         flip_value(1, s_copy)
         floor(0)
         dots(1, (0, 1))
-        norm_inverses(2)
         roots(0)
         squares(3)
         norm_scalars(3)
@@ -499,7 +524,6 @@ def tile_adaptiveattention_pa_kernel(tc, q, k, value, Wv, bv, scoring_weights, o
         flip_wv(0, s_copy)
         dots(1, (2, 3))
         quantise_value()
-        spread_keys(2, (v_copy, v_copy))
         floor(1)
         subtract(0)
         dots(2, (0, 1))

@@ -23,6 +23,7 @@ K_PASS = P * PACK
 N_PASS = HID // K_PASS
 WORDS = K_PASS // 2
 D2_EPS = 1e-12
+SQRT_HALF = 0.7071067811865476
 LOG2_E = 1.4426950408889634
 NORM_SQ_FLOOR = 1e-24
 
@@ -52,34 +53,30 @@ def tile_adaptiveattention_pa_kernel(tc, q, k, value, Wv, bv, scoring_weights, o
             heads = slice(BATCHES[i][0], BATCHES[i][-1] + 1)
             n = len(BATCHES[i]) * NT
             k_rows[i] = keep.tile([P, n, D], BF16, name="k_rows%d" % i)
-            nc.sync.dma_start(out=k_rows[i][:], in_=k[0, heads].rearrange("h (t p) d -> p (h t) d", p=P))
             q_rows[i] = keep.tile([P, n, D], BF16, name="q_rows%d" % i)
-            nc.sync.dma_start(
-                out=q_rows[i][:].rearrange("p (h t) d -> p h (t d)", t=NT),
-                in_=q[0, heads].rearrange("h (p t) d -> p h (t d)", t=NT),
-            )
+            for rows, source in ((k_rows[i], k), (q_rows[i], q)):
+                nc.sync.dma_start(
+                    out=rows[:].rearrange("p (h t) d -> p h (t d)", t=NT),
+                    in_=source[0, heads].rearrange("h (p t) d -> p h (t d)", t=NT),
+                )
 
-        load_batch(0)
-        load_batch(1)
         value_sb = keep.tile([P, PACK, HID], BF16)
-        nc.sync.dma_start(
-            out=value_sb[:].rearrange("p (u e) c -> p u (e c)", e=2),
-            in_=value.rearrange("b (u p e) c -> p (b u) (e c)", u=2, e=2),
-        )
-        load_batch(2)
         wv_sb = keep.tile([P, N_PASS, NH, K_PASS], BF16)
         wv_passes = Wv.rearrange("(h p) (g c) -> p g h c", p=P, g=N_PASS)
-        for g in range(N_PASS):
-            nc.sync.dma_start(out=wv_sb[:, g, :, :], in_=wv_passes[:, g, :, :])
-        for i in range(3, len(BATCHES)):
-            load_batch(i)
         bv_bf = keep.tile([P, HID], BF16)
+        load_batch(0)
+        load_batch(1)
+        load_batch(2)
+        nc.sync.dma_start(out=value_sb[:], in_=value.rearrange("b (p v) c -> p (b v) c", v=PACK))
+        nc.sync.dma_start(out=wv_sb[:, 0, :, :], in_=wv_passes[:, 0, :, :])
+        load_batch(3)
+        nc.sync.dma_start(out=wv_sb[:, 1, :, :], in_=wv_passes[:, 1, :, :])
+        load_batch(4)
         nc.sync.dma_start(out=bv_bf[:], in_=bv.partition_broadcast(P))
-
         zeros = keep.tile([P, P], F32)
         nc.vector.memset(zeros[:], 0.0)
         ones = keep.tile([P, 64], F32)
-        nc.vector.memset(ones[:], 1.0)
+        nc.vector.memset(ones[:], 0.5)
         unused = keep.tile([P, 1], F32)
         nc.scalar.activation(out=unused[:], in_=ones[:, 0:1], func=ACT.Sqrt)
         ident_b = keep.tile([P, P], BF16)
@@ -115,7 +112,7 @@ def tile_adaptiveattention_pa_kernel(tc, q, k, value, Wv, bv, scoring_weights, o
             nc.vector.reciprocal(out=sw_rsum[:], in_=sw_sum[:])
             nc.vector.tensor_scalar_mul(out=w[:], in0=sw_exp[:], scalar1=sw_rsum[:])
             nc.vector.scalar_tensor_tensor(
-                out=euc_scale[:], in0=w[:, 2:3], scalar=-2.0, in1=w[:, 2:3], op0=ALU.mult, op1=ALU.mult
+                out=euc_scale[:], in0=w[:, 2:3], scalar=-4.0, in1=w[:, 2:3], op0=ALU.mult, op1=ALU.mult
             )
 
         norm_floor = keep.tile([P, 1], F32)
@@ -158,23 +155,24 @@ def tile_adaptiveattention_pa_kernel(tc, q, k, value, Wv, bv, scoring_weights, o
 
         def squares(i):
             n = len(BATCHES[i]) * NT
-            sq_tile = keep.tile([P, 2, n], F32, name="sq%d" % i)
-            sq[i] = sq_tile[:]
+            sq[i] = key_columns[i][:, 0 : 2 * n].rearrange("p (f c) -> p f c", f=2)
             for side in (KEYS, QUERIES):
                 rows = (k_rows, q_rows)[side][i]
-                unused_squares = work.tile([P, n, D], BF16, name="unused_squares%d" % n, bufs=1)
+                unused_squares = work.tile([P, 2 * NT, D], BF16, name="unused_squares", bufs=1)
                 for c in range(n):
                     nc.scalar.activation(
                         out=unused_squares[:, c, :],
                         in_=rows[:, c, :],
                         func=ACT.Square,
+                        scale=SQRT_HALF,
                         accum_out=sq[i][:, side, c : c + 1],
                     )
+
+        pending_sums = {}
 
         def squares_of_flipped(i):
             n = len(BATCHES[i]) * NT
             sums = psum.tile([P, 2, n + 64 - 1], F32, tag="acc", bufs=2, name="sums")
-            sq[i] = sums[:, :, 0:n]
             for side in (KEYS, QUERIES):
                 products = work.tile([P, n * P], F32, name="flipped_squares", bufs=2)
                 rows = flipped_sb[i][:, side, :, :].rearrange("p a s -> p (a s)")
@@ -187,6 +185,8 @@ def tile_adaptiveattention_pa_kernel(tc, q, k, value, Wv, bv, scoring_weights, o
                         start=True,
                         stop=True,
                     )
+            sq[i] = key_columns[i][:, 0 : 2 * n].rearrange("p (f c) -> p f c", f=2)
+            pending_sums[i] = sums[:, :, 0:n]
 
         def flip_rows(i, side, copy):
             n = len(BATCHES[i]) * NT
@@ -200,11 +200,11 @@ def tile_adaptiveattention_pa_kernel(tc, q, k, value, Wv, bv, scoring_weights, o
 
         def norm_scalars(i):
             n = len(BATCHES[i]) * NT
+            if i in pending_sums:
+                nc.scalar.copy(out=sq[i], in_=pending_sums[i])
             norm[i] = keep.tile([P, 2, n], F32, name="norm%d" % i)
-            nc.scalar.activation(out=norm[i][:], in_=sq[i], func=ACT.Sqrt, bias=norm_floor[:])
-            nc.scalar.activation(out=key_columns[i][:, 0:n], in_=sq[i][:, KEYS, :], func=ACT.Copy, scale=0.5)
-            half_sq[i] = small("half_sq", i, n)
-            nc.scalar.activation(out=half_sq[i][:], in_=sq[i][:, QUERIES, :], func=ACT.Copy, scale=0.5)
+            nc.scalar.activation(out=norm[i][:], in_=sq[i], func=ACT.Sqrt, scale=2.0, bias=norm_floor[:])
+            half_sq[i] = key_columns[i][:, n : 2 * n]
 
         def norm_products(i):
             n = len(BATCHES[i]) * NT
@@ -218,7 +218,7 @@ def tile_adaptiveattention_pa_kernel(tc, q, k, value, Wv, bv, scoring_weights, o
             rnorm[i] = keep.tile([P, 2, n], F32, name="rnorm%d" % i)
             nc.vector.reciprocal(out=rnorm[i][:], in_=norm[i][:])
             nc.scalar.activation(
-                out=key_columns[i][:, n : 2 * n], in_=rnorm[i][:, KEYS, :], func=ACT.Copy, scale=w[:, 1:2]
+                out=key_columns[i][:, 2 * n : 3 * n], in_=rnorm[i][:, KEYS, :], func=ACT.Copy, scale=w[:, 1:2]
             )
 
         def spread_keys(i, copiers):
@@ -229,7 +229,7 @@ def tile_adaptiveattention_pa_kernel(tc, q, k, value, Wv, bv, scoring_weights, o
                 for which in range(2):
                     spread = psum.tile([P, S], F32, tag="flip", name="spread")
                     for t in range(NT):
-                        c = which * n + a * NT + t
+                        c = 2 * which * n + a * NT + t
                         nc.tensor.transpose(
                             out=spread[:, t * P : (t + 1) * P],
                             in_=key_columns[i][:, c : c + 1].to_broadcast([P, P]),
@@ -245,7 +245,11 @@ def tile_adaptiveattention_pa_kernel(tc, q, k, value, Wv, bv, scoring_weights, o
             parked = work.tile([P, P], F32, name="parked", bufs=2)
             nc.scalar.copy(out=parked[:], in_=turned[:])
             rest = out[0, 2 * i : 2 * i + 2, :]
-            nc.sync.dma_start(out=rest.rearrange("w (c j) -> (w c) j", j=P), in_=parked[0 : 2 * n, :])
+            for which in range(2):
+                nc.sync.dma_start(
+                    out=rest[which, :].rearrange("(c j) -> c j", j=P),
+                    in_=parked[2 * which * n : (2 * which + 1) * n, :],
+                )
             key_rows[i] = work.tile([P, 2, heads, S], F32, name="key_rows%d" % heads, bufs=2)
             for which in range(2):
                 nc.sync.dma_start(
@@ -326,10 +330,20 @@ def tile_adaptiveattention_pa_kernel(tc, q, k, value, Wv, bv, scoring_weights, o
                 out=neg_max[h][:, tiles], in_=mixed[h][:, tiles, :], axis=AX.X, op=ALU.max, negate=True
             )
 
-        def biases(h, engine=None):
+        def biases(h, on_scalar=False):
             i, a = BATCH_OF[h]
             exp_bias[h] = work.tile([P, NT], F32, name="exp_bias", bufs=4)
-            (engine or nc.gpsimd).tensor_tensor(
+            if on_scalar:
+                for t in range(NT):
+                    c = a * NT + t
+                    nc.scalar.activation(
+                        out=exp_bias[h][:, t : t + 1],
+                        in_=neg_max[h][:, t : t + 1],
+                        func=ACT.Copy,
+                        scale=rnorm[i][:, QUERIES, c : c + 1],
+                    )
+                return
+            nc.gpsimd.tensor_tensor(
                 out=exp_bias[h][:],
                 in0=neg_max[h][:],
                 in1=rnorm[i][:, QUERIES, a * NT : (a + 1) * NT],
@@ -354,7 +368,10 @@ def tile_adaptiveattention_pa_kernel(tc, q, k, value, Wv, bv, scoring_weights, o
         def flip_e(h, halves=(0, 1), copiers=None):
             copiers = copiers or (nc.scalar.copy,)
             if 0 in halves:
-                e_grouped[h] = work.tile([P, NT, P, 2], F32, name="e_grouped", bufs=3, align_bytes=64)
+                if h % 2 == 0:
+                    e_pair = work.tile([P, 2, NT, P, 2], F32, name="e_grouped", bufs=2, align_bytes=64)
+                    e_grouped[h], e_grouped[h + 1] = e_pair[:, 0], e_pair[:, 1]
+                    pair_words[h] = e_pair
             for half in halves:
                 t0 = 2 * half
                 e_flipped = psum.tile([P, 2, 2, P], F32, tag="flip", name="e_flipped")
@@ -370,15 +387,24 @@ def tile_adaptiveattention_pa_kernel(tc, q, k, value, Wv, bv, scoring_weights, o
                     out=e_grouped[h][:, t0 : t0 + 2, :, :], in_=e_flipped[:].rearrange("p a u i -> p a i u")
                 )
 
-        def quantise_e(h, tiles=slice(0, NT)):
-            if tiles.start == 0:
-                e_codes[h] = work.tile([P, NT, P], U32, name="e_codes", bufs=2, align_bytes=64)
-                e_scales[h] = work.tile([P, NT, P], U8, name="e_scales", bufs=2, align_bytes=64)
+        pair_words = {}
+
+        def quantise_e(h, heads=1):
+            if h % 2 == 0:
+                codes = work.tile([P, 2, NT, P], U32, name="e_codes", bufs=2, align_bytes=64)
+                scales = work.tile([P, 2, NT, P], U8, name="e_scales", bufs=2, align_bytes=64)
+                for i in range(2):
+                    e_codes[h + i], e_scales[h + i] = codes[:, i], scales[:, i]
+                pair_codes[h] = codes, scales
+            codes, scales = pair_codes[h - h % 2]
+            members = slice(h % 2, h % 2 + heads)
             nc.vector.quantize_mx(
-                out=e_codes[h][:, tiles, :].rearrange("p t i -> p (t i)").bitcast(FP8X4),
-                scales=e_scales[h][:, tiles, :].rearrange("p t i -> p (t i)"),
-                in_=e_grouped[h][:, tiles, :, :].rearrange("p t i u -> p (t i u)").bitcast(BF16),
+                out=codes[:, members].rearrange("p h t i -> p (h t i)").bitcast(FP8X4),
+                scales=scales[:, members].rearrange("p h t i -> p (h t i)"),
+                in_=pair_words[h - h % 2][:, members].rearrange("p h t i u -> p (h t i u)").bitcast(BF16),
             )
+
+        pair_codes = {}
 
         def contract(h, tiles=range(NT)):
             head = slice(h * D, (h + 1) * D)
@@ -420,7 +446,7 @@ def tile_adaptiveattention_pa_kernel(tc, q, k, value, Wv, bv, scoring_weights, o
         v_scales = keep.tile([P, NH * D], U8, align_bytes=64)
         grouped = {}
 
-        def flip_pass(into, block_of, n_blocks, copy):
+        def flip_pass(into, block_of, n_blocks, copy, apart=1):
             for b0 in range(0, n_blocks, 2):
                 flipped = psum.tile([P, 2, 2 * P], F32, tag="flip", name="pass_flipped")
                 for a in range(2):
@@ -431,12 +457,15 @@ def tile_adaptiveattention_pa_kernel(tc, q, k, value, Wv, bv, scoring_weights, o
                             in_=words[:, u * P : (u + 1) * P],
                             identity=ident_f[:],
                         )
-                copy(out=into[:, b0 * P : (b0 + 2) * P, :], in_=flipped[:].rearrange("p u r -> p r u"))
+                copy(
+                    out=into[:, b0 * P : (b0 + 2) * P, :].rearrange("p (e n) u -> p e n u", e=apart),
+                    in_=flipped[:].rearrange("p u (n e) -> p e n u", e=apart),
+                )
 
         def flip_value(g, copy):
             if g == 0:
                 grouped["value"] = work.tile([P, N_PASS, S, 2], F32, name="grouped", bufs=2, align_bytes=64)
-            flip_pass(grouped["value"][:, g, :, :], lambda b: value_sb[:, b, g * K_PASS : (g + 1) * K_PASS], PACK, copy)
+            flip_pass(grouped["value"][:, g, :, :], lambda b: value_sb[:, b, g * K_PASS : (g + 1) * K_PASS], PACK, copy, 2)
 
         def quantise_value():
             nc.vector.quantize_mx(
@@ -577,13 +606,10 @@ def tile_adaptiveattention_pa_kernel(tc, q, k, value, Wv, bv, scoring_weights, o
         roots(4)
         dots(5, (2, 3))
         quantise_v()
-        quantise_e(0)
         floor(5)
         subtract(4)
-        contract(0)
         maxima(3)
         biases(3)
-        normalise(0)
         dots(6, (0, 1))
         roots(5)
         exponentials(2)
@@ -591,29 +617,31 @@ def tile_adaptiveattention_pa_kernel(tc, q, k, value, Wv, bv, scoring_weights, o
         flip_e(2)
         flip_e(3)
         dots(6, (2, 3))
-        quantise_e(1)
+        quantise_e(0, 2)
         floor(6)
         subtract(5)
+        contract(0)
         contract(1)
         maxima(4)
         biases(4)
-        normalise(1)
+        normalise(0)
         dots(7, (0, 1))
+        normalise(1)
         floor(7, slice(0, 2))
         roots(6)
         dots(7, (2, 3))
-        quantise_e(2)
+        quantise_e(2, 2)
         floor(7, slice(2, 4))
         subtract(6)
         contract(2)
+        contract(3)
         maxima(5)
         biases(5)
         normalise(2)
+        normalise(3)
         roots(7)
         exponentials(4)
         exponentials(5)
-        quantise_e(3)
-        contract(3)
         subtract(7, slice(0, 2), nc.vector)
         subtract(7, slice(2, 4), nc.vector)
         maxima(6)
@@ -624,7 +652,6 @@ def tile_adaptiveattention_pa_kernel(tc, q, k, value, Wv, bv, scoring_weights, o
         exponentials(7)
         flip_e(4, copiers=(v_copy,))
         quantise_e(4)
-        normalise(3)
         contract(4)
         flip_e(5, copiers=(v_copy,))
         quantise_e(5)

@@ -70,9 +70,12 @@ def tile_adaptiveattention_pa_kernel(tc, q, k, value, Wv, bv, scoring_weights, o
         nc.sync.dma_start(out=value_sb[:], in_=value.rearrange("b (p v) c -> p (b v) c", v=PACK))
         nc.sync.dma_start(out=wv_sb[:, 0, :, :], in_=wv_passes[:, 0, :, :])
         load_batch(3)
-        nc.sync.dma_start(out=wv_sb[:, 1, :, :], in_=wv_passes[:, 1, :, :])
-        load_batch(4)
-        nc.sync.dma_start(out=bv_bf[:], in_=bv.partition_broadcast(P))
+
+        def late_loads():
+            nc.sync.dma_start(out=wv_sb[:, 1, :, :], in_=wv_passes[:, 1, :, :])
+            load_batch(4)
+            nc.sync.dma_start(out=bv_bf[:], in_=bv.partition_broadcast(P))
+
         zeros = keep.tile([P, P], F32)
         nc.vector.memset(zeros[:], 0.0)
         ones = keep.tile([P, 64], F32)
@@ -251,11 +254,10 @@ def tile_adaptiveattention_pa_kernel(tc, q, k, value, Wv, bv, scoring_weights, o
                     in_=parked[2 * which * n : (2 * which + 1) * n, :],
                 )
             key_rows[i] = work.tile([P, 2, heads, S], F32, name="key_rows%d" % heads, bufs=2)
-            for which in range(2):
-                nc.sync.dma_start(
-                    out=key_rows[i][:, which, :, :].rearrange("p a j -> p (a j)"),
-                    in_=rest[which, :].partition_broadcast(P),
-                )
+            nc.sync.dma_start(
+                out=key_rows[i][:].rearrange("p w a j -> p (w a j)"),
+                in_=rest.rearrange("w j -> (w j)").partition_broadcast(P),
+            )
 
         dot = {}
 
@@ -538,6 +540,7 @@ def tile_adaptiveattention_pa_kernel(tc, q, k, value, Wv, bv, scoring_weights, o
         norm_inverses(1)
         norm_inverses(2)
         park_keys(2)
+        late_loads()
         dots(0, (2, 3))
         spread_keys(1, (s_copy, s_copy))
         flip_rows(2, KEYS, s_copy)

@@ -11,6 +11,7 @@ FP8X4 = mybir.dt.float8_e4m3fn_x4
 ALU = mybir.AluOpType
 ACT = mybir.ActivationFunctionType
 AX = mybir.AxisListType
+ENGINE = mybir.EngineType
 
 P = 128
 NH = 8
@@ -21,19 +22,19 @@ NT = S // P
 PACK = 4
 K_PASS = P * PACK
 N_PASS = HID // K_PASS
-WORDS = K_PASS // 2
 D2_EPS = 1e-12
+NORM_SQ_FLOOR = 1e-24
 SQRT_HALF = 0.7071067811865476
 LOG2_E = 1.4426950408889634
-NORM_SQ_FLOOR = 1e-24
-
-FLOPS = 2 * S * HID * HID + 2 * 2 * NH * S * S * D
-
+SUM_COLUMNS = 64
+WARM_UP = 5
 
 BATCHES = ((0,), (1,), (2, 3), (4, 5), (6, 7))
 BATCH_OF = {h: (i, a) for i, batch in enumerate(BATCHES) for a, h in enumerate(batch)}
-KEEP, KEEP_E = 0, 0
+PARKED = (2, 3, 4)
 KEYS, QUERIES = 0, 1
+ALL = slice(0, NT)
+FIRST, SECOND = slice(0, NT // 2), slice(NT // 2, NT)
 
 
 def tile_adaptiveattention_pa_kernel(tc, q, k, value, Wv, bv, scoring_weights, out):
@@ -42,7 +43,7 @@ def tile_adaptiveattention_pa_kernel(tc, q, k, value, Wv, bv, scoring_weights, o
         keep = stack.enter_context(tc.tile_pool(name="keep", bufs=1))
         work = stack.enter_context(tc.tile_pool(name="work", bufs=2))
         psum = stack.enter_context(tc.psum_pool(name="psum", bufs=3))
-        stack.enter_context(tc.manual_schedule(engines={mybir.EngineType.DVE, mybir.EngineType.Activation, mybir.EngineType.Pool, mybir.EngineType.SP}))
+        stack.enter_context(tc.manual_schedule(engines={ENGINE.DVE, ENGINE.Activation, ENGINE.Pool, ENGINE.SP}))
 
         sw_bf = keep.tile([P, 3], BF16)
         nc.scalar.dma_start(out=sw_bf[:], in_=scoring_weights.partition_broadcast(P))
@@ -64,28 +65,33 @@ def tile_adaptiveattention_pa_kernel(tc, q, k, value, Wv, bv, scoring_weights, o
         wv_sb = keep.tile([P, N_PASS, NH, K_PASS], BF16)
         wv_passes = Wv.rearrange("(h p) (g c) -> p g h c", p=P, g=N_PASS)
         bv_bf = keep.tile([P, HID], BF16)
-        load_batch(0)
-        load_batch(1)
-        load_batch(2)
-        nc.sync.dma_start(out=value_sb[:], in_=value.rearrange("b (p v) c -> p (b v) c", v=PACK))
-        nc.sync.dma_start(out=wv_sb[:, 0, :, :], in_=wv_passes[:, 0, :, :])
-        load_batch(3)
 
-        def late_loads():
-            nc.sync.dma_start(out=wv_sb[:, 1, :, :], in_=wv_passes[:, 1, :, :])
+        def load_wv(g):
+            nc.sync.dma_start(out=wv_sb[:, g, :, :], in_=wv_passes[:, g, :, :])
+
+        def load_late():
+            load_wv(1)
             load_batch(4)
             nc.sync.dma_start(out=bv_bf[:], in_=bv.partition_broadcast(P))
 
+        for i in (0, 1, 2):
+            load_batch(i)
+        nc.sync.dma_start(out=value_sb[:], in_=value.rearrange("b (p v) c -> p (b v) c", v=PACK))
+        load_batch(3)
+        load_wv(0)
+
         zeros = keep.tile([P, P], F32)
         nc.vector.memset(zeros[:], 0.0)
-        ones = keep.tile([P, 64], F32)
-        nc.vector.memset(ones[:], 0.5)
+        halves = keep.tile([P, SUM_COLUMNS], F32)
+        nc.vector.memset(halves[:], 0.5)
         unused = keep.tile([P, 1], F32)
-        nc.scalar.activation(out=unused[:], in_=ones[:, 0:1], func=ACT.Sqrt)
+        nc.scalar.activation(out=unused[:], in_=halves[:, 0:1], func=ACT.Sqrt)
         ident_b = keep.tile([P, P], BF16)
         make_identity(nc, ident_b[:])
         ident_f = keep.tile([P, P], F32)
         make_identity(nc, ident_f[:])
+        norm_floor = keep.tile([P, 1], F32)
+        nc.vector.memset(norm_floor[:], NORM_SQ_FLOOR)
 
         w = keep.tile([P, 3], F32)
         euc_scale = keep.tile([P, 1], F32)
@@ -95,12 +101,7 @@ def tile_adaptiveattention_pa_kernel(tc, q, k, value, Wv, bv, scoring_weights, o
             nc.vector.tensor_reduce(out=neg_sw_max[:], in_=sw_bf[:], axis=AX.X, op=ALU.max, negate=True)
             sw_log2 = keep.tile([P, 3], F32)
             nc.vector.tensor_scalar(
-                out=sw_log2[:],
-                in0=sw_bf[:],
-                scalar1=neg_sw_max[:],
-                scalar2=LOG2_E,
-                op0=ALU.add,
-                op1=ALU.mult,
+                out=sw_log2[:], in0=sw_bf[:], scalar1=neg_sw_max[:], scalar2=LOG2_E, op0=ALU.add, op1=ALU.mult
             )
             two = keep.tile([P, 3], F32)
             nc.gpsimd.memset(two[:], 2.0)
@@ -118,49 +119,34 @@ def tile_adaptiveattention_pa_kernel(tc, q, k, value, Wv, bv, scoring_weights, o
                 out=euc_scale[:], in0=w[:, 2:3], scalar=-4.0, in1=w[:, 2:3], op0=ALU.mult, op1=ALU.mult
             )
 
-        norm_floor = keep.tile([P, 1], F32)
-        nc.vector.memset(norm_floor[:], NORM_SQ_FLOOR)
-
-        flipped_sb = {}
+        columns = {}
+        for i, batch in enumerate(BATCHES):
+            columns[i] = keep.tile([P, P if i in PARKED else 3 * len(batch) * NT], F32, name="columns%d" % i)
+            if i in PARKED:
+                nc.vector.memset(columns[i][:], 0.0)
+        flipped_rows = {}
         key_rows = {}
-        sq = {}
+        sums = {}
         norm = {}
         rnorm = {}
-        key_columns = {}
-        half_sq = {}
-        for i in range(len(BATCHES)):
-            key_columns[i] = keep.tile([P, P], F32, name="key_columns%d" % i)
-            nc.vector.memset(key_columns[i][:], 0.0)
         dot_q = {}
         sqrt_scale = {}
-        neg_half_d2 = {}
-        mixed = {}
-        neg_max = {}
-        exp_bias = {}
-        e = {}
-        e_grouped = {}
-        e_codes = {}
-        e_scales = {}
-        context = {}
-        row_sum = keep.tile([P, NH * NT], F32)
-        out_rows = out.rearrange("b (p t) c -> p (b t) c", t=NT)
 
-        def small(name, i, columns):
-            return keep.tile([P, columns], F32, name="%s%d" % (name, i))
+        def tiles_of(i):
+            return len(BATCHES[i]) * NT
 
-        def keep_clock(bank):
-            nc.tensor.matmul(out=bank, lhsT=ident_f[:], rhs=ident_f[:, 0 : bank.shape[1]], start=True, stop=True)
+        def half_norms_sq(i):
+            n = tiles_of(i)
+            return columns[i][:, 0 : 2 * n].rearrange("p (f c) -> p f c", f=2)
 
-        def warm_up(n):
+        def warm_up():
             warm = psum.tile([P, P], F32, tag="dot", name="warm")
-            for i in range(n):
+            for i in range(WARM_UP):
                 nc.tensor.matmul(out=warm[:], lhsT=zeros[:], rhs=zeros[:], start=True, stop=True)
 
         def squares(i):
-            n = len(BATCHES[i]) * NT
-            sq[i] = key_columns[i][:, 0 : 2 * n].rearrange("p (f c) -> p f c", f=2)
-            for side in (KEYS, QUERIES):
-                rows = (k_rows, q_rows)[side][i]
+            n = tiles_of(i)
+            for side, rows in ((KEYS, k_rows[i]), (QUERIES, q_rows[i])):
                 unused_squares = work.tile([P, 2 * NT, D], BF16, name="unused_squares", bufs=1)
                 for c in range(n):
                     nc.scalar.activation(
@@ -168,139 +154,140 @@ def tile_adaptiveattention_pa_kernel(tc, q, k, value, Wv, bv, scoring_weights, o
                         in_=rows[:, c, :],
                         func=ACT.Square,
                         scale=SQRT_HALF,
-                        accum_out=sq[i][:, side, c : c + 1],
+                        accum_out=half_norms_sq(i)[:, side, c : c + 1],
                     )
 
-        pending_sums = {}
-
         def squares_of_flipped(i):
-            n = len(BATCHES[i]) * NT
-            sums = psum.tile([P, 2, n + 64 - 1], F32, tag="acc", bufs=2, name="sums")
+            n = tiles_of(i)
+            spread_sums = psum.tile([P, 2, n + SUM_COLUMNS - 1], F32, tag="acc", bufs=2, name="sums")
             for side in (KEYS, QUERIES):
                 products = work.tile([P, n * P], F32, name="flipped_squares", bufs=2)
-                rows = flipped_sb[i][:, side, :, :].rearrange("p a s -> p (a s)")
+                rows = flipped_rows[i][:, side, :, :].rearrange("p a s -> p (a s)")
                 nc.gpsimd.tensor_tensor(out=products[:], in0=rows, in1=rows, op=ALU.mult)
                 for c in range(n):
                     nc.tensor.matmul(
-                        out=sums[:, side, c : c + 64],
+                        out=spread_sums[:, side, c : c + SUM_COLUMNS],
                         lhsT=products[:, c * P : (c + 1) * P],
-                        rhs=ones[:],
+                        rhs=halves[:],
                         start=True,
                         stop=True,
                     )
-            sq[i] = key_columns[i][:, 0 : 2 * n].rearrange("p (f c) -> p f c", f=2)
-            pending_sums[i] = sums[:, :, 0:n]
+            sums[i] = spread_sums[:, :, 0:n]
 
-        def flip_rows(i, side, copy):
-            n = len(BATCHES[i]) * NT
-            if side == KEYS:
-                flipped_sb[i] = keep.tile([P, 2, n // NT, S], BF16, name="flipped_sb%d" % i)
-            rows = (k_rows, q_rows)[side][i]
-            flipped = psum.tile([P, n * P], BF16, tag="flip", name="flipped")
-            for c in range(n):
-                nc.tensor.transpose(out=flipped[:, c * P : (c + 1) * P], in_=rows[:, c, :], identity=ident_b[:])
-            copy(out=flipped_sb[i][:, side, :, :].rearrange("p a s -> p (a s)"), in_=flipped[:])
+        def flip_rows(i, copy):
+            n = tiles_of(i)
+            flipped_rows[i] = keep.tile([P, 2, n // NT, S], BF16, name="flipped_rows%d" % i)
+            for side, rows in ((KEYS, k_rows[i]), (QUERIES, q_rows[i])):
+                flipped = psum.tile([P, n * P], BF16, tag="flip", name="flipped")
+                for c in range(n):
+                    nc.tensor.transpose(out=flipped[:, c * P : (c + 1) * P], in_=rows[:, c, :], identity=ident_b[:])
+                copy(out=flipped_rows[i][:, side, :, :].rearrange("p a s -> p (a s)"), in_=flipped[:])
 
-        def norm_scalars(i):
-            n = len(BATCHES[i]) * NT
-            if i in pending_sums:
-                nc.scalar.copy(out=sq[i], in_=pending_sums[i])
+        def norms(i):
+            n = tiles_of(i)
+            if i in sums:
+                nc.scalar.copy(out=half_norms_sq(i), in_=sums[i])
             norm[i] = keep.tile([P, 2, n], F32, name="norm%d" % i)
-            nc.scalar.activation(out=norm[i][:], in_=sq[i], func=ACT.Sqrt, scale=2.0, bias=norm_floor[:])
-            half_sq[i] = key_columns[i][:, n : 2 * n]
+            nc.scalar.activation(
+                out=norm[i][:], in_=half_norms_sq(i), func=ACT.Sqrt, scale=2.0, bias=norm_floor[:]
+            )
 
         def norm_products(i):
-            n = len(BATCHES[i]) * NT
-            dot_q[i] = small("dot_q", i, n)
+            n = tiles_of(i)
+            dot_q[i] = keep.tile([P, n], F32, name="dot_q%d" % i)
             nc.scalar.activation(out=dot_q[i][:], in_=norm[i][:, QUERIES, :], func=ACT.Copy, scale=w[:, 0:1])
-            sqrt_scale[i] = small("sqrt_scale", i, n)
-            nc.scalar.activation(out=sqrt_scale[i][:], in_=sq[i][:, QUERIES, :], func=ACT.Copy, scale=euc_scale[:])
+            sqrt_scale[i] = keep.tile([P, n], F32, name="sqrt_scale%d" % i)
+            nc.scalar.activation(
+                out=sqrt_scale[i][:], in_=half_norms_sq(i)[:, QUERIES, :], func=ACT.Copy, scale=euc_scale[:]
+            )
 
         def norm_inverses(i):
-            n = len(BATCHES[i]) * NT
+            n = tiles_of(i)
             rnorm[i] = keep.tile([P, 2, n], F32, name="rnorm%d" % i)
             nc.vector.reciprocal(out=rnorm[i][:], in_=norm[i][:])
             nc.scalar.activation(
-                out=key_columns[i][:, 2 * n : 3 * n], in_=rnorm[i][:, KEYS, :], func=ACT.Copy, scale=w[:, 1:2]
+                out=columns[i][:, 2 * n : 3 * n], in_=rnorm[i][:, KEYS, :], func=ACT.Copy, scale=w[:, 1:2]
             )
+
+        def key_rows_tile(i):
+            heads = len(BATCHES[i])
+            key_rows[i] = work.tile([P, heads, 2, S], F32, name="key_rows%d" % heads, bufs=2)
 
         def spread_keys(i, copiers):
-            heads = len(BATCHES[i])
-            n = heads * NT
-            key_rows[i] = work.tile([P, 2, heads, S], F32, name="key_rows%d" % heads, bufs=2)
-            for a in range(heads):
-                for which in range(2):
-                    spread = psum.tile([P, S], F32, tag="flip", name="spread")
-                    for t in range(NT):
-                        c = 2 * which * n + a * NT + t
-                        nc.tensor.transpose(
-                            out=spread[:, t * P : (t + 1) * P],
-                            in_=key_columns[i][:, c : c + 1].to_broadcast([P, P]),
-                            identity=ident_f[:],
-                        )
-                    copiers[which](out=key_rows[i][:, which, a, :], in_=spread[:])
+            n = tiles_of(i)
+            key_rows_tile(i)
+            for which in range(2):
+                spread = psum.tile([P, S], F32, tag="flip", name="spread")
+                for t in range(NT):
+                    c = 2 * which * n + t
+                    nc.tensor.transpose(
+                        out=spread[:, t * P : (t + 1) * P],
+                        in_=columns[i][:, c : c + 1].to_broadcast([P, P]),
+                        identity=ident_f[:],
+                    )
+                copiers[which](out=key_rows[i][:, 0, which, :], in_=spread[:])
 
         def park_keys(i):
-            heads = len(BATCHES[i])
-            n = heads * NT
+            n = tiles_of(i)
             turned = psum.tile([P, P], F32, tag="acc", bufs=2, name="turned")
-            nc.tensor.transpose(out=turned[:], in_=key_columns[i][:], identity=ident_f[:])
-            parked = work.tile([P, P], F32, name="parked", bufs=2)
+            nc.tensor.transpose(out=turned[:], in_=columns[i][:], identity=ident_f[:])
+            parked = work.tile([P, P], F32, name="parked", bufs=1)
             nc.scalar.copy(out=parked[:], in_=turned[:])
-            rest = out[0, 2 * i : 2 * i + 2, :]
-            for which in range(2):
+            rest = out[0, 2 * i : 2 * i + len(BATCHES[i]), :]
+            heads = range(len(BATCHES[i]))
+            for a in heads:
+                for which in range(2):
+                    start = 2 * which * n + a * NT
+                    nc.sync.dma_start(
+                        out=rest[a, which * S : (which + 1) * S].rearrange("(c j) -> c j", j=P),
+                        in_=parked[start : start + NT, :],
+                    )
+            key_rows_tile(i)
+            for a in heads:
                 nc.sync.dma_start(
-                    out=rest[which, :].rearrange("(c j) -> c j", j=P),
-                    in_=parked[2 * which * n : (2 * which + 1) * n, :],
+                    out=key_rows[i][:, a, :, :].rearrange("p w j -> p (w j)"), in_=rest[a, :].partition_broadcast(P)
                 )
-            key_rows[i] = work.tile([P, 2, heads, S], F32, name="key_rows%d" % heads, bufs=2)
-            nc.sync.dma_start(
-                out=key_rows[i][:].rearrange("p w a j -> p (w a j)"),
-                in_=rest.rearrange("w j -> (w j)").partition_broadcast(P),
-            )
 
-        dot = {}
+        neg_half_d2 = {}
+        mixed = {}
+        neg_max = {}
+        exp_bias = {}
 
-        def multiply(h, tiles):
+        def scores(h, tiles):
             i, a = BATCH_OF[h]
-            for t in tiles:
-                dot[h, t] = psum.tile([P, S], F32, tag="dot", name="dot")
+            n = tiles_of(i)
+            if tiles == FIRST:
+                neg_half_d2[h] = work.tile([P, NT, S], F32, name="neg_half_d2", bufs=3)
+                mixed[h] = work.tile([P, NT, S], F32, name="mixed", bufs=5)
+            for t in range(tiles.start, tiles.stop):
+                c = a * NT + t
+                dot = psum.tile([P, S], F32, tag="dot", name="dot")
                 nc.tensor.matmul(
-                    out=dot[h, t][:],
-                    lhsT=flipped_sb[i][:, QUERIES, a, t * P : (t + 1) * P],
-                    rhs=flipped_sb[i][:, KEYS, a, :],
+                    out=dot[:],
+                    lhsT=flipped_rows[i][:, QUERIES, a, t * P : (t + 1) * P],
+                    rhs=flipped_rows[i][:, KEYS, a, :],
                     start=True,
                     stop=True,
                 )
-
-        def dots(h, tiles=range(NT)):
-            i, a = BATCH_OF[h]
-            if 0 in tiles:
-                neg_half_d2[h] = work.tile([P, NT, S], F32, name="neg_half_d2", bufs=3)
-                mixed[h] = work.tile([P, NT, S], F32, name="mixed", bufs=5)
-            for t in tiles:
-                c = a * NT + t
-                if (h, t) not in dot:
-                    multiply(h, (t,))
                 nc.vector.scalar_tensor_tensor(
                     out=mixed[h][:, t, :],
-                    in0=key_rows[i][:, 1, a, :],
+                    in0=key_rows[i][:, a, 1, :],
                     scalar=dot_q[i][:, c : c + 1],
-                    in1=dot[h, t][:],
+                    in1=dot[:],
                     op0=ALU.add,
                     op1=ALU.mult,
                 )
                 nc.vector.scalar_tensor_tensor(
                     out=neg_half_d2[h][:, t, :],
-                    in0=dot[h, t][:],
-                    scalar=half_sq[i][:, c : c + 1],
-                    in1=key_rows[i][:, 0, a, :],
+                    in0=dot[:],
+                    scalar=columns[i][:, n + c : n + c + 1],
+                    in1=key_rows[i][:, a, 0, :],
                     op0=ALU.subtract,
                     op1=ALU.subtract,
                 )
 
-        def floor(h, tiles=slice(0, NT), engine=None):
-            (engine or nc.gpsimd).tensor_scalar(
+        def floor(h, tiles=ALL):
+            nc.gpsimd.tensor_scalar(
                 out=neg_half_d2[h][:, tiles, :],
                 in0=neg_half_d2[h][:, tiles, :],
                 scalar1=-0.5 * D2_EPS,
@@ -309,9 +296,9 @@ def tile_adaptiveattention_pa_kernel(tc, q, k, value, Wv, bv, scoring_weights, o
                 op1=ALU.max,
             )
 
-        def roots(h, tiles=range(NT)):
+        def roots(h):
             i, a = BATCH_OF[h]
-            for t in tiles:
+            for t in range(NT):
                 c = a * NT + t
                 nc.scalar.activation(
                     out=neg_half_d2[h][:, t, :],
@@ -320,31 +307,16 @@ def tile_adaptiveattention_pa_kernel(tc, q, k, value, Wv, bv, scoring_weights, o
                     scale=sqrt_scale[i][:, c : c + 1],
                 )
 
-        def subtract(h, tiles=slice(0, NT), engine=None):
-            (engine or nc.gpsimd).tensor_tensor(
+        def subtract(h, tiles=ALL, engine=nc.gpsimd):
+            engine.tensor_tensor(
                 out=mixed[h][:, tiles, :], in0=mixed[h][:, tiles, :], in1=neg_half_d2[h][:, tiles, :], op=ALU.subtract
             )
 
-        def maxima(h, tiles=slice(0, NT)):
-            if tiles.start == 0:
-                neg_max[h] = work.tile([P, NT], F32, name="neg_max", bufs=4)
-            nc.vector.tensor_reduce(
-                out=neg_max[h][:, tiles], in_=mixed[h][:, tiles, :], axis=AX.X, op=ALU.max, negate=True
-            )
-
-        def biases(h, on_scalar=False):
+        def maxima(h):
             i, a = BATCH_OF[h]
+            neg_max[h] = work.tile([P, NT], F32, name="neg_max", bufs=4)
+            nc.vector.tensor_reduce(out=neg_max[h][:], in_=mixed[h][:], axis=AX.X, op=ALU.max, negate=True)
             exp_bias[h] = work.tile([P, NT], F32, name="exp_bias", bufs=4)
-            if on_scalar:
-                for t in range(NT):
-                    c = a * NT + t
-                    nc.scalar.activation(
-                        out=exp_bias[h][:, t : t + 1],
-                        in_=neg_max[h][:, t : t + 1],
-                        func=ACT.Copy,
-                        scale=rnorm[i][:, QUERIES, c : c + 1],
-                    )
-                return
             nc.gpsimd.tensor_tensor(
                 out=exp_bias[h][:],
                 in0=neg_max[h][:],
@@ -352,11 +324,18 @@ def tile_adaptiveattention_pa_kernel(tc, q, k, value, Wv, bv, scoring_weights, o
                 op=ALU.mult,
             )
 
-        def exponentials(h, tiles=range(NT)):
+        e = {}
+        e_words = {}
+        e_codes = {}
+        e_scales = {}
+        context = {}
+        row_sum = keep.tile([P, NH * NT], F32)
+        out_rows = out.rearrange("b (p t) c -> p (b t) c", t=NT)
+
+        def exponentials(h):
             i, a = BATCH_OF[h]
-            if 0 in tiles:
-                e[h] = work.tile([P, NT, S], BF16, name="e", bufs=3)
-            for t in tiles:
+            e[h] = work.tile([P, NT, S], BF16, name="e", bufs=3)
+            for t in range(NT):
                 c = a * NT + t
                 nc.scalar.activation(
                     out=e[h][:, t, :],
@@ -367,74 +346,54 @@ def tile_adaptiveattention_pa_kernel(tc, q, k, value, Wv, bv, scoring_weights, o
                     accum_out=row_sum[:, h * NT + t : h * NT + t + 1],
                 )
 
-        def flip_e(h, halves=(0, 1), copiers=None):
-            copiers = copiers or (nc.scalar.copy,)
-            if 0 in halves:
-                if h % 2 == 0:
-                    e_pair = work.tile([P, 2, NT, P, 2], F32, name="e_grouped", bufs=2, align_bytes=64)
-                    e_grouped[h], e_grouped[h + 1] = e_pair[:, 0], e_pair[:, 1]
-                    pair_words[h] = e_pair
-            for half in halves:
-                t0 = 2 * half
-                e_flipped = psum.tile([P, 2, 2, P], F32, tag="flip", name="e_flipped")
-                if KEEP_E:
-                    keep_clock(e_flipped[:, 0, 0, 0:KEEP_E])
+        def flip_e(h, copy):
+            pair, member = h // 2, h % 2
+            if member == 0:
+                e_words[pair] = work.tile([P, 2, NT, P, 2], F32, name="e_words", bufs=2, align_bytes=64)
+            for t0 in range(0, NT, 2):
+                flipped = psum.tile([P, 2, 2, P], F32, tag="flip", name="e_flipped")
                 for b in range(2):
                     words = e[h][:, t0 + b, :].bitcast(F32)
                     for u in range(2):
                         nc.tensor.transpose(
-                            out=e_flipped[:, b, u, :], in_=words[:, u * P : (u + 1) * P], identity=ident_f[:]
+                            out=flipped[:, b, u, :], in_=words[:, u * P : (u + 1) * P], identity=ident_f[:]
                         )
-                copiers[half % len(copiers)](
-                    out=e_grouped[h][:, t0 : t0 + 2, :, :], in_=e_flipped[:].rearrange("p a u i -> p a i u")
+                copy(
+                    out=e_words[pair][:, member, t0 : t0 + 2, :, :], in_=flipped[:].rearrange("p a u i -> p a i u")
                 )
 
-        pair_words = {}
-
-        def quantise_e(h, heads=1):
-            if h % 2 == 0:
-                codes = work.tile([P, 2, NT, P], U32, name="e_codes", bufs=2, align_bytes=64)
-                scales = work.tile([P, 2, NT, P], U8, name="e_scales", bufs=2, align_bytes=64)
-                for i in range(2):
-                    e_codes[h + i], e_scales[h + i] = codes[:, i], scales[:, i]
-                pair_codes[h] = codes, scales
-            codes, scales = pair_codes[h - h % 2]
-            members = slice(h % 2, h % 2 + heads)
+        def quantise_e(h, heads):
+            pair, member = h // 2, h % 2
+            if member == 0:
+                e_codes[pair] = work.tile([P, 2, NT, P], U32, name="e_codes", bufs=2, align_bytes=64)
+                e_scales[pair] = work.tile([P, 2, NT, P], U8, name="e_scales", bufs=2, align_bytes=64)
+            members = slice(member, member + heads)
             nc.vector.quantize_mx(
-                out=codes[:, members].rearrange("p h t i -> p (h t i)").bitcast(FP8X4),
-                scales=scales[:, members].rearrange("p h t i -> p (h t i)"),
-                in_=pair_words[h - h % 2][:, members].rearrange("p h t i u -> p (h t i u)").bitcast(BF16),
+                out=e_codes[pair][:, members].rearrange("p h t i -> p (h t i)").bitcast(FP8X4),
+                scales=e_scales[pair][:, members].rearrange("p h t i -> p (h t i)"),
+                in_=e_words[pair][:, members].rearrange("p h t i u -> p (h t i u)").bitcast(BF16),
             )
 
-        pair_codes = {}
-
-        def contract(h, tiles=range(NT)):
+        def contract(h):
+            pair, member = h // 2, h % 2
             head = slice(h * D, (h + 1) * D)
-            if 0 in tiles:
-                context[h] = psum.tile([P, NT, D], F32, tag="acc", bufs=2, name="ctx")
-            for t in tiles:
+            context[h] = psum.tile([P, NT, D], F32, tag="acc", bufs=2, name="context")
+            for t in range(NT):
                 nc.tensor.matmul_mx(
                     out=context[h][:, t, :],
-                    lhsT=e_codes[h][:, t, :].bitcast(FP8X4),
-                    lhsT_scale=e_scales[h][:, t, :],
+                    lhsT=e_codes[pair][:, member, t, :].bitcast(FP8X4),
+                    lhsT_scale=e_scales[pair][:, member, t, :],
                     rhs=v_codes[:, head].bitcast(FP8X4),
                     rhs_scale=v_scales[:, head],
                     start=True,
                     stop=True,
                 )
 
-        def normalise(h, on_scalar=False):
+        def normalise(h):
             head = slice(h * D, (h + 1) * D)
             row_rsum = work.tile([P, NT], F32, name="row_rsum")
             nc.vector.reciprocal(out=row_rsum[:], in_=row_sum[:, h * NT : (h + 1) * NT])
-            result = work.tile([P, NT, D], F32, name="result", bufs=3)
-            if on_scalar:
-                for t in range(NT):
-                    nc.scalar.activation(
-                        out=result[:, t, :], in_=context[h][:, t, :], func=ACT.Copy, scale=row_rsum[:, t : t + 1]
-                    )
-                nc.sync.dma_start(out=out_rows[:, :, head], in_=result[:])
-                return
+            result = work.tile([P, NT, D], F32, name="result", bufs=4)
             nc.vector.tensor_tensor(
                 out=result[:], in0=context[h][:], in1=row_rsum[:].unsqueeze(2).to_broadcast([P, NT, D]), op=ALU.mult
             )
@@ -444,54 +403,54 @@ def tile_adaptiveattention_pa_kernel(tc, q, k, value, Wv, bv, scoring_weights, o
         value_scales = keep.tile([P, N_PASS, S], U8, align_bytes=64)
         wv_codes = keep.tile([P, N_PASS, HID], U32, align_bytes=64)
         wv_scales = keep.tile([P, N_PASS, HID], U8, align_bytes=64)
-        v_codes = keep.tile([P, NH * D], U32, align_bytes=64)
-        v_scales = keep.tile([P, NH * D], U8, align_bytes=64)
-        grouped = {}
+        v_codes = keep.tile([P, HID], U32, align_bytes=64)
+        v_scales = keep.tile([P, HID], U8, align_bytes=64)
+        words_of = {}
 
-        def flip_pass(into, block_of, n_blocks, copy, apart=1):
+        def flip_pass(into, block_of, n_blocks, apart=1):
             for b0 in range(0, n_blocks, 2):
                 flipped = psum.tile([P, 2, 2 * P], F32, tag="flip", name="pass_flipped")
-                for a in range(2):
-                    words = block_of(b0 + a).bitcast(F32)
+                for b in range(2):
+                    words = block_of(b0 + b).bitcast(F32)
                     for u in range(2):
                         nc.tensor.transpose(
-                            out=flipped[:, u, a * P : (a + 1) * P],
+                            out=flipped[:, u, b * P : (b + 1) * P],
                             in_=words[:, u * P : (u + 1) * P],
                             identity=ident_f[:],
                         )
-                copy(
+                nc.scalar.copy(
                     out=into[:, b0 * P : (b0 + 2) * P, :].rearrange("p (e n) u -> p e n u", e=apart),
                     in_=flipped[:].rearrange("p u (n e) -> p e n u", e=apart),
                 )
 
-        def flip_value(g, copy):
-            if g == 0:
-                grouped["value"] = work.tile([P, N_PASS, S, 2], F32, name="grouped", bufs=2, align_bytes=64)
-            flip_pass(grouped["value"][:, g, :, :], lambda b: value_sb[:, b, g * K_PASS : (g + 1) * K_PASS], PACK, copy, 2)
+        def flip_value():
+            words_of["value"] = work.tile([P, N_PASS, S, 2], F32, name="words", bufs=2, align_bytes=64)
+            for g in range(N_PASS):
+                features = slice(g * K_PASS, (g + 1) * K_PASS)
+                flip_pass(words_of["value"][:, g, :, :], lambda v: value_sb[:, v, features], PACK, apart=2)
 
         def quantise_value():
             nc.vector.quantize_mx(
                 out=value_codes[:].rearrange("p g r -> p (g r)").bitcast(FP8X4),
                 scales=value_scales[:].rearrange("p g r -> p (g r)"),
-                in_=grouped["value"][:].rearrange("p g r u -> p (g r u)").bitcast(BF16),
+                in_=words_of["value"][:].rearrange("p g r u -> p (g r u)").bitcast(BF16),
             )
 
-        def flip_wv(g, copy):
-            grouped[g] = work.tile([P, HID, 2], F32, name="grouped", bufs=2, align_bytes=64)
-            flip_pass(grouped[g], lambda b: wv_sb[:, g, b, :], NH, copy)
+        def flip_wv(g):
+            words_of[g] = work.tile([P, HID, 2], F32, name="words", bufs=2, align_bytes=64)
+            flip_pass(words_of[g], lambda h: wv_sb[:, g, h, :], NH)
 
         def quantise_wv(g):
             nc.vector.quantize_mx(
                 out=wv_codes[:, g, :].bitcast(FP8X4),
                 scales=wv_scales[:, g, :],
-                in_=grouped[g][:].rearrange("p r u -> p (r u)").bitcast(BF16),
+                in_=words_of[g][:].rearrange("p r u -> p (r u)").bitcast(BF16),
             )
-
 
         def project(h):
             head = slice(h * D, (h + 1) * D)
             if h == 0:
-                grouped["v"] = work.tile([P, NH, D, PACK], BF16, name="grouped", bufs=2, align_bytes=64)
+                words_of["v"] = work.tile([P, NH, D, PACK], BF16, name="words", bufs=2, align_bytes=64)
             vp = psum.tile([P, PACK, D], F32, tag="acc", bufs=2, name="vp")
             for t in range(PACK):
                 block = slice(t * P, (t + 1) * P)
@@ -506,7 +465,7 @@ def tile_adaptiveattention_pa_kernel(tc, q, k, value, Wv, bv, scoring_weights, o
                         stop=(g == N_PASS - 1),
                     )
             nc.vector.tensor_tensor(
-                out=grouped["v"][:, h, :, :],
+                out=words_of["v"][:, h, :, :],
                 in0=vp[:].rearrange("p t d -> p d t"),
                 in1=bv_bf[:, head].unsqueeze(2).to_broadcast([P, D, PACK]),
                 op=ALU.add,
@@ -514,158 +473,116 @@ def tile_adaptiveattention_pa_kernel(tc, q, k, value, Wv, bv, scoring_weights, o
 
         def quantise_v():
             nc.vector.quantize_mx(
-                out=v_codes[:].bitcast(FP8X4), scales=v_scales[:], in_=grouped["v"][:].rearrange("p h d t -> p (h d t)")
+                out=v_codes[:].bitcast(FP8X4),
+                scales=v_scales[:],
+                in_=words_of["v"][:].rearrange("p h d t -> p (h d t)"),
             )
 
         v_copy, s_copy = nc.vector.tensor_copy, nc.scalar.copy
-        warm_up(5)
+
+        warm_up()
         sw_exp = mixing_powers()
         squares(0)
-        flip_rows(0, KEYS, v_copy)
-        flip_rows(0, QUERIES, v_copy)
-        norm_scalars(0)
+        flip_rows(0, v_copy)
+        norms(0)
         mixing_weights(sw_exp)
         norm_products(0)
         norm_inverses(0)
-        flip_rows(1, KEYS, v_copy)
-        flip_rows(1, QUERIES, v_copy)
-        spread_keys(0, (s_copy, v_copy))
+        flip_rows(1, v_copy)
+        spread_keys(0, (v_copy, v_copy))
         squares_of_flipped(1)
         squares(2)
-        norm_scalars(2)
-        norm_products(2)
-        norm_scalars(1)
-        norm_products(1)
-        dots(0, (0, 1))
-        norm_inverses(1)
-        norm_inverses(2)
-        park_keys(2)
-        late_loads()
-        dots(0, (2, 3))
-        spread_keys(1, (s_copy, s_copy))
-        flip_rows(2, KEYS, s_copy)
-        flip_rows(2, QUERIES, s_copy)
-        flip_value(0, s_copy)
-        flip_value(1, s_copy)
-        floor(0)
-        dots(1, (0, 1))
-        roots(0)
-        squares(3)
-        norm_scalars(3)
-        norm_products(3)
-        flip_wv(0, s_copy)
-        dots(1, (2, 3))
-        quantise_value()
-        floor(1)
-        subtract(0)
-        dots(2, (0, 1))
-        norm_inverses(3)
-        park_keys(3)
-        roots(1)
-        flip_wv(1, s_copy)
-        flip_rows(3, KEYS, s_copy)
-        flip_rows(3, QUERIES, s_copy)
-        squares(4)
-        norm_scalars(4)
-        norm_products(4)
-        dots(2, (2, 3))
-        quantise_wv(0)
-        floor(2)
-        subtract(1)
-        maxima(0)
-        biases(0)
-        dots(3, (0, 1))
-        roots(2)
-        flip_rows(4, KEYS, s_copy)
-        flip_rows(4, QUERIES, s_copy)
-        dots(3, (2, 3))
-        quantise_wv(1)
-        floor(3)
-        subtract(2)
-        maxima(1)
-        biases(1)
-        project(0)
-        project(1)
-        project(2)
-        project(3)
-        dots(4, (0, 1))
-        norm_inverses(4)
-        park_keys(4)
-        roots(3)
-        exponentials(0)
-        exponentials(1)
-        flip_e(0)
-        flip_e(1)
-        dots(4, (2, 3))
-        floor(4)
-        subtract(3)
-        maxima(2)
-        biases(2)
-        project(4)
-        project(5)
-        project(6)
-        project(7)
-        dots(5, (0, 1))
-        roots(4)
-        dots(5, (2, 3))
-        quantise_v()
-        floor(5)
-        subtract(4)
-        maxima(3)
-        biases(3)
-        dots(6, (0, 1))
-        roots(5)
-        exponentials(2)
-        exponentials(3)
-        flip_e(2)
-        flip_e(3)
-        dots(6, (2, 3))
-        quantise_e(0, 2)
-        floor(6)
-        subtract(5)
-        contract(0)
-        contract(1)
-        maxima(4)
-        biases(4)
-        normalise(0)
-        dots(7, (0, 1))
-        normalise(1)
-        floor(7, slice(0, 2))
-        roots(6)
-        dots(7, (2, 3))
-        quantise_e(2, 2)
-        floor(7, slice(2, 4))
-        subtract(6)
-        contract(2)
-        contract(3)
-        maxima(5)
-        biases(5)
-        normalise(2)
-        normalise(3)
-        roots(7)
-        exponentials(4)
-        exponentials(5)
-        subtract(7, slice(0, 2), nc.vector)
-        subtract(7, slice(2, 4), nc.vector)
-        maxima(6)
-        biases(6)
-        maxima(7)
-        biases(7)
-        exponentials(6)
-        exponentials(7)
-        flip_e(4, copiers=(v_copy,))
-        quantise_e(4)
-        contract(4)
-        flip_e(5, copiers=(v_copy,))
-        quantise_e(5)
-        contract(5)
-        normalise(4)
-        flip_e(6, copiers=(s_copy,))
-        quantise_e(6)
-        contract(6)
-        normalise(5)
-        flip_e(7, copiers=(s_copy,))
-        quantise_e(7)
-        contract(7)
-        normalise(6, True)
+        for i in (2, 1):
+            norms(i)
+            norm_products(i)
+
+        def scalar_share(h):
+            roots(h)
+            if h == 0:
+                squares(3)
+                norms(3)
+                norm_products(3)
+                flip_wv(0)
+            if h == 1:
+                flip_rows(3, s_copy)
+                flip_wv(1)
+                squares(4)
+                norms(4)
+                norm_products(4)
+            if h == 2:
+                flip_rows(4, s_copy)
+            if h in (3, 5):
+                pair = (h - 3, h - 2)
+                for i in pair:
+                    exponentials(i)
+                for i in pair:
+                    flip_e(i, s_copy)
+
+        for h in range(NH):
+            last = h == NH - 1
+            scores(h, FIRST)
+            if h == 0:
+                norm_inverses(2)
+                park_keys(2)
+                load_late()
+                norm_inverses(1)
+            if h == 2:
+                norm_inverses(3)
+                park_keys(3)
+            if last:
+                normalise(1)
+                floor(h, FIRST)
+            if h > 0:
+                scalar_share(h - 1)
+            scores(h, SECOND)
+            if h == 0:
+                spread_keys(1, (s_copy, v_copy))
+                flip_rows(2, s_copy)
+                flip_value()
+            if h == 1:
+                quantise_value()
+            if h in (2, 3):
+                quantise_wv(h - 2)
+            if h == 5:
+                quantise_v()
+            pair = (2 * (h - 6), 2 * (h - 6) + 1)
+            if h >= 6:
+                quantise_e(pair[0], 2)
+            floor(h, SECOND if last else ALL)
+            if h > 0:
+                subtract(h - 1)
+            if h >= 6:
+                for i in pair:
+                    contract(i)
+            if h >= 2:
+                maxima(h - 2)
+            if h == 3:
+                for i in range(6):
+                    project(i)
+                norm_inverses(4)
+                park_keys(4)
+            if h == 4:
+                for i in range(6, NH):
+                    project(i)
+            if h == 6:
+                normalise(0)
+            if last:
+                for i in pair:
+                    normalise(i)
+
+        scalar_share(7)
+        for h in (4, 5):
+            exponentials(h)
+        subtract(7, FIRST)
+        subtract(7, SECOND, nc.vector)
+        for h in (6, 7):
+            maxima(h)
+        for h in (6, 7):
+            exponentials(h)
+        for h in range(4, NH):
+            flip_e(h, v_copy if h < 6 else s_copy)
+            quantise_e(h, 1)
+            contract(h)
+            if h > 4:
+                normalise(h - 1)
         normalise(7)

from contextlib import ExitStack

import concourse.mybir as mybir
from concourse.masks import make_identity

F32 = mybir.dt.float32
BF16 = mybir.dt.bfloat16
U32 = mybir.dt.uint32
U8 = mybir.dt.uint8
FP8X4 = mybir.dt.float8_e4m3fn_x4
ALU = mybir.AluOpType
ACT = mybir.ActivationFunctionType
AX = mybir.AxisListType
ENGINE = mybir.EngineType

P = 128
NH = 8
S = 512
D = 128
HID = NH * D
NT = S // P
PACK = 4
K_PASS = P * PACK
N_PASS = HID // K_PASS
D2_EPS = 1e-12
NORM_SQ_FLOOR = 1e-24
SQRT_HALF = 0.7071067811865476
LOG2_E = 1.4426950408889634
SUM_COLUMNS = 64
WARM_UP = 5

BATCHES = ((0,), (1,), (2, 3), (4, 5), (6, 7))
BATCH_OF = {h: (i, a) for i, batch in enumerate(BATCHES) for a, h in enumerate(batch)}
PARKED = (2, 3, 4)
KEYS, QUERIES = 0, 1
ALL = slice(0, NT)
FIRST, SECOND = slice(0, NT // 2), slice(NT // 2, NT)


def tile_adaptiveattention_pa_kernel(tc, q, k, value, Wv, bv, scoring_weights, out):
    nc = tc.nc
    with ExitStack() as stack:
        keep = stack.enter_context(tc.tile_pool(name="keep", bufs=1))
        work = stack.enter_context(tc.tile_pool(name="work", bufs=2))
        psum = stack.enter_context(tc.psum_pool(name="psum", bufs=3))
        stack.enter_context(tc.manual_schedule(engines={ENGINE.DVE, ENGINE.Activation, ENGINE.Pool, ENGINE.SP}))

        sw_bf = keep.tile([P, 3], BF16)
        nc.scalar.dma_start(out=sw_bf[:], in_=scoring_weights.partition_broadcast(P))
        k_rows = {}
        q_rows = {}

        def load_batch(i):
            heads = slice(BATCHES[i][0], BATCHES[i][-1] + 1)
            n = len(BATCHES[i]) * NT
            k_rows[i] = keep.tile([P, n, D], BF16, name="k_rows%d" % i)
            q_rows[i] = keep.tile([P, n, D], BF16, name="q_rows%d" % i)
            for rows, source in ((k_rows[i], k), (q_rows[i], q)):
                nc.sync.dma_start(
                    out=rows[:].rearrange("p (h t) d -> p h (t d)", t=NT),
                    in_=source[0, heads].rearrange("h (p t) d -> p h (t d)", t=NT),
                )

        value_sb = keep.tile([P, PACK, HID], BF16)
        wv_sb = keep.tile([P, N_PASS, NH, K_PASS], BF16)
        wv_passes = Wv.rearrange("(h p) (g c) -> p g h c", p=P, g=N_PASS)
        bv_bf = keep.tile([P, HID], BF16)

        def load_wv(g):
            nc.sync.dma_start(out=wv_sb[:, g, :, :], in_=wv_passes[:, g, :, :])

        def load_late():
            load_wv(1)
            load_batch(4)
            nc.sync.dma_start(out=bv_bf[:], in_=bv.partition_broadcast(P))

        for i in (0, 1, 2):
            load_batch(i)
        nc.sync.dma_start(out=value_sb[:], in_=value.rearrange("b (p v) c -> p (b v) c", v=PACK))
        load_batch(3)
        load_wv(0)

        zeros = keep.tile([P, P], F32)
        nc.vector.memset(zeros[:], 0.0)
        halves = keep.tile([P, SUM_COLUMNS], F32)
        nc.vector.memset(halves[:], 0.5)
        unused = keep.tile([P, 1], F32)
        nc.scalar.activation(out=unused[:], in_=halves[:, 0:1], func=ACT.Sqrt)
        ident_b = keep.tile([P, P], BF16)
        make_identity(nc, ident_b[:])
        ident_f = keep.tile([P, P], F32)
        make_identity(nc, ident_f[:])
        norm_floor = keep.tile([P, 1], F32)
        nc.vector.memset(norm_floor[:], NORM_SQ_FLOOR)

        w = keep.tile([P, 3], F32)
        euc_scale = keep.tile([P, 1], F32)

        def mixing_powers():
            neg_sw_max = keep.tile([P, 1], F32)
            nc.vector.tensor_reduce(out=neg_sw_max[:], in_=sw_bf[:], axis=AX.X, op=ALU.max, negate=True)
            sw_log2 = keep.tile([P, 3], F32)
            nc.vector.tensor_scalar(
                out=sw_log2[:], in0=sw_bf[:], scalar1=neg_sw_max[:], scalar2=LOG2_E, op0=ALU.add, op1=ALU.mult
            )
            two = keep.tile([P, 3], F32)
            nc.gpsimd.memset(two[:], 2.0)
            sw_exp = keep.tile([P, 3], F32)
            nc.gpsimd.tensor_tensor(out=sw_exp[:], in0=two[:], in1=sw_log2[:], op=ALU.pow)
            return sw_exp

        def mixing_weights(sw_exp):
            sw_sum = keep.tile([P, 1], F32)
            nc.vector.tensor_reduce(out=sw_sum[:], in_=sw_exp[:], axis=AX.X, op=ALU.add)
            sw_rsum = keep.tile([P, 1], F32)
            nc.vector.reciprocal(out=sw_rsum[:], in_=sw_sum[:])
            nc.vector.tensor_scalar_mul(out=w[:], in0=sw_exp[:], scalar1=sw_rsum[:])
            nc.vector.scalar_tensor_tensor(
                out=euc_scale[:], in0=w[:, 2:3], scalar=-4.0, in1=w[:, 2:3], op0=ALU.mult, op1=ALU.mult
            )

        columns = {}
        for i, batch in enumerate(BATCHES):
            columns[i] = keep.tile([P, P if i in PARKED else 3 * len(batch) * NT], F32, name="columns%d" % i)
            if i in PARKED:
                nc.vector.memset(columns[i][:], 0.0)
        flipped_rows = {}
        key_rows = {}
        sums = {}
        norm = {}
        rnorm = {}
        dot_q = {}
        sqrt_scale = {}

        def tiles_of(i):
            return len(BATCHES[i]) * NT

        def half_norms_sq(i):
            n = tiles_of(i)
            return columns[i][:, 0 : 2 * n].rearrange("p (f c) -> p f c", f=2)

        def warm_up():
            warm = psum.tile([P, P], F32, tag="dot", name="warm")
            for i in range(WARM_UP):
                nc.tensor.matmul(out=warm[:], lhsT=zeros[:], rhs=zeros[:], start=True, stop=True)

        def squares(i):
            n = tiles_of(i)
            for side, rows in ((KEYS, k_rows[i]), (QUERIES, q_rows[i])):
                unused_squares = work.tile([P, 2 * NT, D], BF16, name="unused_squares", bufs=1)
                for c in range(n):
                    nc.scalar.activation(
                        out=unused_squares[:, c, :],
                        in_=rows[:, c, :],
                        func=ACT.Square,
                        scale=SQRT_HALF,
                        accum_out=half_norms_sq(i)[:, side, c : c + 1],
                    )

        def squares_of_flipped(i):
            n = tiles_of(i)
            spread_sums = psum.tile([P, 2, n + SUM_COLUMNS - 1], F32, tag="acc", bufs=2, name="sums")
            for side in (KEYS, QUERIES):
                products = work.tile([P, n * P], F32, name="flipped_squares", bufs=2)
                rows = flipped_rows[i][:, side, :, :].rearrange("p a s -> p (a s)")
                nc.gpsimd.tensor_tensor(out=products[:], in0=rows, in1=rows, op=ALU.mult)
                for c in range(n):
                    nc.tensor.matmul(
                        out=spread_sums[:, side, c : c + SUM_COLUMNS],
                        lhsT=products[:, c * P : (c + 1) * P],
                        rhs=halves[:],
                        start=True,
                        stop=True,
                    )
            sums[i] = spread_sums[:, :, 0:n]

        def flip_rows(i, copy):
            n = tiles_of(i)
            flipped_rows[i] = keep.tile([P, 2, n // NT, S], BF16, name="flipped_rows%d" % i)
            for side, rows in ((KEYS, k_rows[i]), (QUERIES, q_rows[i])):
                flipped = psum.tile([P, n * P], BF16, tag="flip", name="flipped")
                for c in range(n):
                    nc.tensor.transpose(out=flipped[:, c * P : (c + 1) * P], in_=rows[:, c, :], identity=ident_b[:])
                copy(out=flipped_rows[i][:, side, :, :].rearrange("p a s -> p (a s)"), in_=flipped[:])

        def norms(i):
            n = tiles_of(i)
            if i in sums:
                nc.scalar.copy(out=half_norms_sq(i), in_=sums[i])
            norm[i] = keep.tile([P, 2, n], F32, name="norm%d" % i)
            nc.scalar.activation(
                out=norm[i][:], in_=half_norms_sq(i), func=ACT.Sqrt, scale=2.0, bias=norm_floor[:]
            )

        def norm_products(i):
            n = tiles_of(i)
            dot_q[i] = keep.tile([P, n], F32, name="dot_q%d" % i)
            nc.scalar.activation(out=dot_q[i][:], in_=norm[i][:, QUERIES, :], func=ACT.Copy, scale=w[:, 0:1])
            sqrt_scale[i] = keep.tile([P, n], F32, name="sqrt_scale%d" % i)
            nc.scalar.activation(
                out=sqrt_scale[i][:], in_=half_norms_sq(i)[:, QUERIES, :], func=ACT.Copy, scale=euc_scale[:]
            )

        def norm_inverses(i):
            n = tiles_of(i)
            rnorm[i] = keep.tile([P, 2, n], F32, name="rnorm%d" % i)
            nc.vector.reciprocal(out=rnorm[i][:], in_=norm[i][:])
            nc.scalar.activation(
                out=columns[i][:, 2 * n : 3 * n], in_=rnorm[i][:, KEYS, :], func=ACT.Copy, scale=w[:, 1:2]
            )

        def key_rows_tile(i):
            heads = len(BATCHES[i])
            key_rows[i] = work.tile([P, heads, 2, S], F32, name="key_rows%d" % heads, bufs=2)

        def spread_keys(i, copiers):
            n = tiles_of(i)
            key_rows_tile(i)
            for which in range(2):
                spread = psum.tile([P, S], F32, tag="flip", name="spread")
                for t in range(NT):
                    c = 2 * which * n + t
                    nc.tensor.transpose(
                        out=spread[:, t * P : (t + 1) * P],
                        in_=columns[i][:, c : c + 1].to_broadcast([P, P]),
                        identity=ident_f[:],
                    )
                copiers[which](out=key_rows[i][:, 0, which, :], in_=spread[:])

        def park_keys(i):
            n = tiles_of(i)
            turned = psum.tile([P, P], F32, tag="acc", bufs=2, name="turned")
            nc.tensor.transpose(out=turned[:], in_=columns[i][:], identity=ident_f[:])
            parked = work.tile([P, P], F32, name="parked", bufs=1)
            nc.scalar.copy(out=parked[:], in_=turned[:])
            rest = out[0, 2 * i : 2 * i + len(BATCHES[i]), :]
            heads = range(len(BATCHES[i]))
            for a in heads:
                for which in range(2):
                    start = 2 * which * n + a * NT
                    nc.sync.dma_start(
                        out=rest[a, which * S : (which + 1) * S].rearrange("(c j) -> c j", j=P),
                        in_=parked[start : start + NT, :],
                    )
            key_rows_tile(i)
            for a in heads:
                nc.sync.dma_start(
                    out=key_rows[i][:, a, :, :].rearrange("p w j -> p (w j)"), in_=rest[a, :].partition_broadcast(P)
                )

        neg_half_d2 = {}
        mixed = {}
        neg_max = {}
        exp_bias = {}

        def scores(h, tiles):
            i, a = BATCH_OF[h]
            n = tiles_of(i)
            if tiles == FIRST:
                neg_half_d2[h] = work.tile([P, NT, S], F32, name="neg_half_d2", bufs=3)
                mixed[h] = work.tile([P, NT, S], F32, name="mixed", bufs=5)
            for t in range(tiles.start, tiles.stop):
                c = a * NT + t
                dot = psum.tile([P, S], F32, tag="dot", name="dot")
                nc.tensor.matmul(
                    out=dot[:],
                    lhsT=flipped_rows[i][:, QUERIES, a, t * P : (t + 1) * P],
                    rhs=flipped_rows[i][:, KEYS, a, :],
                    start=True,
                    stop=True,
                )
                nc.vector.scalar_tensor_tensor(
                    out=mixed[h][:, t, :],
                    in0=key_rows[i][:, a, 1, :],
                    scalar=dot_q[i][:, c : c + 1],
                    in1=dot[:],
                    op0=ALU.add,
                    op1=ALU.mult,
                )
                nc.vector.scalar_tensor_tensor(
                    out=neg_half_d2[h][:, t, :],
                    in0=dot[:],
                    scalar=columns[i][:, n + c : n + c + 1],
                    in1=key_rows[i][:, a, 0, :],
                    op0=ALU.subtract,
                    op1=ALU.subtract,
                )

        def floor(h, tiles=ALL):
            nc.gpsimd.tensor_scalar(
                out=neg_half_d2[h][:, tiles, :],
                in0=neg_half_d2[h][:, tiles, :],
                scalar1=-0.5 * D2_EPS,
                scalar2=-3.0e38,
                op0=ALU.min,
                op1=ALU.max,
            )

        def roots(h):
            i, a = BATCH_OF[h]
            for t in range(NT):
                c = a * NT + t
                nc.scalar.activation(
                    out=neg_half_d2[h][:, t, :],
                    in_=neg_half_d2[h][:, t, :],
                    func=ACT.Sqrt,
                    scale=sqrt_scale[i][:, c : c + 1],
                )

        def subtract(h, tiles=ALL, engine=nc.gpsimd):
            engine.tensor_tensor(
                out=mixed[h][:, tiles, :], in0=mixed[h][:, tiles, :], in1=neg_half_d2[h][:, tiles, :], op=ALU.subtract
            )

        def maxima(h):
            i, a = BATCH_OF[h]
            neg_max[h] = work.tile([P, NT], F32, name="neg_max", bufs=4)
            nc.vector.tensor_reduce(out=neg_max[h][:], in_=mixed[h][:], axis=AX.X, op=ALU.max, negate=True)
            exp_bias[h] = work.tile([P, NT], F32, name="exp_bias", bufs=4)
            nc.gpsimd.tensor_tensor(
                out=exp_bias[h][:],
                in0=neg_max[h][:],
                in1=rnorm[i][:, QUERIES, a * NT : (a + 1) * NT],
                op=ALU.mult,
            )

        e = {}
        e_words = {}
        e_codes = {}
        e_scales = {}
        context = {}
        row_sum = keep.tile([P, NH * NT], F32)
        out_rows = out.rearrange("b (p t) c -> p (b t) c", t=NT)

        def exponentials(h):
            i, a = BATCH_OF[h]
            e[h] = work.tile([P, NT, S], BF16, name="e", bufs=3)
            for t in range(NT):
                c = a * NT + t
                nc.scalar.activation(
                    out=e[h][:, t, :],
                    in_=mixed[h][:, t, :],
                    func=ACT.Exp,
                    scale=rnorm[i][:, QUERIES, c : c + 1],
                    bias=exp_bias[h][:, t : t + 1],
                    accum_out=row_sum[:, h * NT + t : h * NT + t + 1],
                )

        def flip_e(h, copy):
            pair, member = h // 2, h % 2
            if member == 0:
                e_words[pair] = work.tile([P, 2, NT, P, 2], F32, name="e_words", bufs=2, align_bytes=64)
            for t0 in range(0, NT, 2):
                flipped = psum.tile([P, 2, 2, P], F32, tag="flip", name="e_flipped")
                for b in range(2):
                    words = e[h][:, t0 + b, :].bitcast(F32)
                    for u in range(2):
                        nc.tensor.transpose(
                            out=flipped[:, b, u, :], in_=words[:, u * P : (u + 1) * P], identity=ident_f[:]
                        )
                copy(
                    out=e_words[pair][:, member, t0 : t0 + 2, :, :], in_=flipped[:].rearrange("p a u i -> p a i u")
                )

        def quantise_e(h, heads):
            pair, member = h // 2, h % 2
            if member == 0:
                e_codes[pair] = work.tile([P, 2, NT, P], U32, name="e_codes", bufs=2, align_bytes=64)
                e_scales[pair] = work.tile([P, 2, NT, P], U8, name="e_scales", bufs=2, align_bytes=64)
            members = slice(member, member + heads)
            nc.vector.quantize_mx(
                out=e_codes[pair][:, members].rearrange("p h t i -> p (h t i)").bitcast(FP8X4),
                scales=e_scales[pair][:, members].rearrange("p h t i -> p (h t i)"),
                in_=e_words[pair][:, members].rearrange("p h t i u -> p (h t i u)").bitcast(BF16),
            )

        def contract(h):
            pair, member = h // 2, h % 2
            head = slice(h * D, (h + 1) * D)
            context[h] = psum.tile([P, NT, D], F32, tag="acc", bufs=2, name="context")
            for t in range(NT):
                nc.tensor.matmul_mx(
                    out=context[h][:, t, :],
                    lhsT=e_codes[pair][:, member, t, :].bitcast(FP8X4),
                    lhsT_scale=e_scales[pair][:, member, t, :],
                    rhs=v_codes[:, head].bitcast(FP8X4),
                    rhs_scale=v_scales[:, head],
                    start=True,
                    stop=True,
                )

        def normalise(h):
            head = slice(h * D, (h + 1) * D)
            row_rsum = work.tile([P, NT], F32, name="row_rsum")
            nc.vector.reciprocal(out=row_rsum[:], in_=row_sum[:, h * NT : (h + 1) * NT])
            result = work.tile([P, NT, D], F32, name="result", bufs=4)
            nc.vector.tensor_tensor(
                out=result[:], in0=context[h][:], in1=row_rsum[:].unsqueeze(2).to_broadcast([P, NT, D]), op=ALU.mult
            )
            nc.sync.dma_start(out=out_rows[:, :, head], in_=result[:])

        value_codes = keep.tile([P, N_PASS, S], U32, align_bytes=64)
        value_scales = keep.tile([P, N_PASS, S], U8, align_bytes=64)
        wv_codes = keep.tile([P, N_PASS, HID], U32, align_bytes=64)
        wv_scales = keep.tile([P, N_PASS, HID], U8, align_bytes=64)
        v_codes = keep.tile([P, HID], U32, align_bytes=64)
        v_scales = keep.tile([P, HID], U8, align_bytes=64)
        words_of = {}

        def flip_pass(into, block_of, n_blocks, apart=1):
            for b0 in range(0, n_blocks, 2):
                flipped = psum.tile([P, 2, 2 * P], F32, tag="flip", name="pass_flipped")
                for b in range(2):
                    words = block_of(b0 + b).bitcast(F32)
                    for u in range(2):
                        nc.tensor.transpose(
                            out=flipped[:, u, b * P : (b + 1) * P],
                            in_=words[:, u * P : (u + 1) * P],
                            identity=ident_f[:],
                        )
                nc.scalar.copy(
                    out=into[:, b0 * P : (b0 + 2) * P, :].rearrange("p (e n) u -> p e n u", e=apart),
                    in_=flipped[:].rearrange("p u (n e) -> p e n u", e=apart),
                )

        def flip_value():
            words_of["value"] = work.tile([P, N_PASS, S, 2], F32, name="words", bufs=2, align_bytes=64)
            for g in range(N_PASS):
                features = slice(g * K_PASS, (g + 1) * K_PASS)
                flip_pass(words_of["value"][:, g, :, :], lambda v: value_sb[:, v, features], PACK, apart=2)

        def quantise_value():
            nc.vector.quantize_mx(
                out=value_codes[:].rearrange("p g r -> p (g r)").bitcast(FP8X4),
                scales=value_scales[:].rearrange("p g r -> p (g r)"),
                in_=words_of["value"][:].rearrange("p g r u -> p (g r u)").bitcast(BF16),
            )

        def flip_wv(g):
            words_of[g] = work.tile([P, HID, 2], F32, name="words", bufs=2, align_bytes=64)
            flip_pass(words_of[g], lambda h: wv_sb[:, g, h, :], NH)

        def quantise_wv(g):
            nc.vector.quantize_mx(
                out=wv_codes[:, g, :].bitcast(FP8X4),
                scales=wv_scales[:, g, :],
                in_=words_of[g][:].rearrange("p r u -> p (r u)").bitcast(BF16),
            )

        def project(h):
            head = slice(h * D, (h + 1) * D)
            if h == 0:
                words_of["v"] = work.tile([P, NH, D, PACK], BF16, name="words", bufs=2, align_bytes=64)
            vp = psum.tile([P, PACK, D], F32, tag="acc", bufs=2, name="vp")
            for t in range(PACK):
                block = slice(t * P, (t + 1) * P)
                for g in range(N_PASS):
                    nc.tensor.matmul_mx(
                        out=vp[:, t, :],
                        lhsT=value_codes[:, g, block].bitcast(FP8X4),
                        lhsT_scale=value_scales[:, g, block],
                        rhs=wv_codes[:, g, head].bitcast(FP8X4),
                        rhs_scale=wv_scales[:, g, head],
                        start=(g == 0),
                        stop=(g == N_PASS - 1),
                    )
            nc.vector.tensor_tensor(
                out=words_of["v"][:, h, :, :],
                in0=vp[:].rearrange("p t d -> p d t"),
                in1=bv_bf[:, head].unsqueeze(2).to_broadcast([P, D, PACK]),
                op=ALU.add,
            )

        def quantise_v():
            nc.vector.quantize_mx(
                out=v_codes[:].bitcast(FP8X4),
                scales=v_scales[:],
                in_=words_of["v"][:].rearrange("p h d t -> p (h d t)"),
            )

        v_copy, s_copy = nc.vector.tensor_copy, nc.scalar.copy

        warm_up()
        sw_exp = mixing_powers()
        squares(0)
        flip_rows(0, v_copy)
        norms(0)
        mixing_weights(sw_exp)
        norm_products(0)
        norm_inverses(0)
        flip_rows(1, v_copy)
        spread_keys(0, (v_copy, v_copy))
        squares_of_flipped(1)
        squares(2)
        for i in (2, 1):
            norms(i)
            norm_products(i)

        def scalar_share(h):
            roots(h)
            if h == 0:
                squares(3)
                norms(3)
                norm_products(3)
                flip_wv(0)
            if h == 1:
                flip_rows(3, s_copy)
                flip_wv(1)
                squares(4)
                norms(4)
                norm_products(4)
            if h == 2:
                flip_rows(4, s_copy)
            if h in (3, 5):
                pair = (h - 3, h - 2)
                for i in pair:
                    exponentials(i)
                for i in pair:
                    flip_e(i, s_copy)

        for h in range(NH):
            last = h == NH - 1
            scores(h, FIRST)
            if h == 0:
                norm_inverses(2)
                park_keys(2)
                load_late()
                norm_inverses(1)
            if h == 2:
                norm_inverses(3)
                park_keys(3)
            if last:
                normalise(1)
                floor(h, FIRST)
            if h > 0:
                scalar_share(h - 1)
            scores(h, SECOND)
            if h == 0:
                spread_keys(1, (s_copy, v_copy))
                flip_rows(2, s_copy)
                flip_value()
            if h == 1:
                quantise_value()
            if h in (2, 3):
                quantise_wv(h - 2)
            if h == 5:
                quantise_v()
            pair = (2 * (h - 6), 2 * (h - 6) + 1)
            if h >= 6:
                quantise_e(pair[0], 2)
            floor(h, SECOND if last else ALL)
            if h > 0:
                subtract(h - 1)
            if h >= 6:
                for i in pair:
                    contract(i)
            if h >= 2:
                maxima(h - 2)
            if h == 3:
                for i in range(6):
                    project(i)
                norm_inverses(4)
                park_keys(4)
            if h == 4:
                for i in range(6, NH):
                    project(i)
            if h == 6:
                normalise(0)
            if last:
                for i in pair:
                    normalise(i)

        scalar_share(7)
        for h in (4, 5):
            exponentials(h)
        subtract(7, FIRST)
        subtract(7, SECOND, nc.vector)
        for h in (6, 7):
            maxima(h)
        for h in (6, 7):
            exponentials(h)
        for h in range(4, NH):
            flip_e(h, v_copy if h < 6 else s_copy)
            quantise_e(h, 1)
            contract(h)
            if h > 4:
                normalise(h - 1)
        normalise(7)
